import numpy as np
import ml_dtypes


def mxq(x, axis, fmt="e4m3"):
    dtype, down = {"e4m3": (ml_dtypes.float8_e4m3fn, 7), "e5m2": (ml_dtypes.float8_e5m2, 14)}[fmt]
    v = np.moveaxis(np.asarray(x, np.float32).astype(ml_dtypes.bfloat16).astype(np.float64), axis, -1)
    blocks = v.reshape(v.shape[:-1] + (-1, 32))
    amax = np.abs(blocks).max(-1, keepdims=True)
    byte = np.maximum(np.where(amax > 0, np.frexp(amax)[1] - 1 + 127, 0) - down, 1)
    scale = np.exp2(byte - 127.0)
    codes = (blocks / scale).astype(np.float32).astype(dtype).astype(np.float64)
    return np.moveaxis((codes * scale).reshape(v.shape), -1, axis)


WIDE = False


def mx_kscale(k):
    if not WIDE:
        return np.ones(k)
    levels = np.array([10, -10, 5, -5, 0])
    if k % 512:
        return np.exp2(np.random.permutation(np.resize(levels, k // 32))).repeat(32)
    a = np.empty((k // 512, 16))
    for p in range(k // 512):
        a[p, :8] = np.random.permutation(np.resize(levels, 8))
        for g in range(8):
            far = levels[np.abs(levels - a[p, g]) >= 10]
            a[p, g + 8] = far[np.random.randint(len(far))]
    return np.exp2(a.ravel()).repeat(32)


BF16 = ml_dtypes.bfloat16


def bf(x):
    return np.asarray(x, np.float32).astype(BF16)


def f64(x):
    return np.asarray(x).astype(np.float64)


E2M1 = np.array([0.0, 0.5, 1.0, 1.5, 2.0, 3.0, 4.0, 6.0, -0.0, -0.5, -1.0, -1.5, -2.0, -3.0, -4.0, -6.0])


def pack_weight(w, fmt):
    k, n = w.shape
    w = f64(bf(w)).reshape(k // 32, 32, n)
    amax = np.abs(w).max(1)
    if fmt == "e4m3":
        byte = np.frexp(amax)[1] - 1 + 127 - 7
    else:
        mant, ex = np.frexp(amax / 6.0)
        byte = np.where(mant > 0.5, ex, ex - 1) + 127
    byte = np.clip(np.where(amax > 0, byte, 1), 1, 254)
    scaled = (w * np.exp2(127.0 - byte)[:, None, :]).reshape(k, n).astype(np.float32)
    by_word = np.ascontiguousarray(scaled.reshape(k // 512, 128, 4, n).transpose(0, 1, 3, 2))
    if fmt == "e4m3":
        words = by_word.astype(ml_dtypes.float8_e4m3fn).view(np.uint8)
    else:
        c = by_word.astype(ml_dtypes.float4_e2m1fn).view(np.uint8) & 0xF
        words = c[..., 0::2] | (c[..., 1::2] << 4)
    return np.ascontiguousarray(words), np.ascontiguousarray(byte.astype(np.uint8).reshape(k // 512, 16, n))


def unpack_weight(words, scales, fmt):
    g, p, n, _ = words.shape
    if fmt == "e4m3":
        vals = np.ascontiguousarray(words).view(ml_dtypes.float8_e4m3fn).astype(np.float64)
    else:
        nib = np.empty((g, p, n, 4), np.uint8)
        nib[..., 0::2] = words & 0xF
        nib[..., 1::2] = words >> 4
        vals = E2M1[nib]
    vals = vals * np.repeat(np.exp2(scales.astype(np.float64) - 127.0), 8, axis=1)[..., None]
    return vals.transpose(0, 1, 3, 2).reshape(g * 512, n)


T, B, F, H, R, O = 1024, 8, 1024, 1024, 512, 128


def draw0():
    s, t = mx_kscale(R), mx_kscale(H)
    z2 = bf(np.random.standard_normal((T, B, R)) * s)
    sw1_words, sw1_scales = pack_weight(np.random.standard_normal((R, H)) / np.sqrt(R) / s[:, None] * t, "e4m3")
    return {"z2": z2,
            "sw1_words": sw1_words,
            "sw1_scales": sw1_scales,
            "b2": bf(np.random.standard_normal((B, H)) * t),
            "w3": bf(np.random.standard_normal((B, H, O)) / np.sqrt(H) / t[:, None]),
            "b3": bf(np.random.standard_normal((B, O)))}


def core(z2, sw1_words, sw1_scales, b2, w3, b3):
    u = (mxq(f64(z2), 2, "e4m3").reshape(T * B, R) @ unpack_weight(sw1_words, sw1_scales, "e4m3")).reshape(T, B, H)
    h = np.maximum(u + f64(b2)[None, :, :], 0.0)
    out = (mxq(h, 2, "e4m3").transpose(1, 0, 2) @ mxq(f64(w3), 1, "e4m3")) + f64(b3)[:, None, :]
    return out.transpose(1, 0, 2)


def e4m3fn_bytes(y):
    return np.clip(np.asarray(y, np.float64), -448.0, 448.0).astype(np.float32).astype(ml_dtypes.float8_e4m3fn).view(np.uint8)


def e4m3fn_values(b):
    return np.asarray(b, np.uint8).view(ml_dtypes.float8_e4m3fn).astype(np.float64)


def setup_inputs():
    d = draw0()
    x0 = np.asarray(d['z2']).astype(np.float64)
    s = (np.max(np.abs(x0), axis=(0, 1), keepdims=True) / 448.0).astype(np.float32)
    out = {}
    for k, v in d.items():
        if k == 'z2':
            out['z2_bytes'] = e4m3fn_bytes(x0 / s.astype(np.float64))
            out['z2_scale'] = s
        else:
            out[k] = v
    return out


def reference(z2_bytes, z2_scale, sw1_words, sw1_scales, b2, w3, b3):
    return core(e4m3fn_values(z2_bytes) * z2_scale.astype(np.float64), sw1_words, sw1_scales, b2, w3, b3)

@@ -1,0 +1,381 @@
+from contextlib import ExitStack
+
+import concourse.mybir as mybir
+from concourse.masks import make_identity
+
+T, B, R, H, O = 1024, 8, 512, 1024, 128
+FLOPS = 2 * T * B * (R * H + H * O)
+
+F32 = mybir.dt.float32
+BF16 = mybir.dt.bfloat16
+U32 = mybir.dt.uint32
+I32 = mybir.dt.int32
+U8 = mybir.dt.uint8
+FP8 = mybir.dt.float8_e4m3fn
+FP8X4 = mybir.dt.float8_e4m3fn_x4
+ALU = mybir.AluOpType
+ACT = mybir.ActivationFunctionType
+
+P = 128
+PACK = 4
+G = H // 512
+ROWS = 512
+SUB = ROWS // P
+HALVES = T // ROWS
+STEPS = B * HALVES
+NT = 240
+
+
+def tile_mlpmodelpredictor_pb_t_w8_kernel(
+    tc, z2_bytes, z2_scale, sw1_words, sw1_scales, b2, w3, b3, out
+):
+    nc = tc.nc
+    with ExitStack() as ctx:
+        keep = ctx.enter_context(tc.tile_pool(name="keep", bufs=1))
+        loads = ctx.enter_context(tc.tile_pool(name="loads", bufs=1))
+        work = ctx.enter_context(tc.tile_pool(name="work", bufs=2))
+        psum = ctx.enter_context(tc.psum_pool(name="psum", bufs=1))
+        ctx.enter_context(tc.manual_schedule())
+
+        warm = keep.tile([P, 1], F32, name="warm")
+        ident_f = keep.tile([P, P], F32, name="ident_f")
+        ident_b = keep.tile([P, P], BF16, name="ident_b")
+        kscale = keep.tile([P, PACK], F32, name="kscale")
+        w1_raw = keep.tile([P, G, H // G], I32, name="w1_raw", align_bytes=64)
+        w1_codes = keep.tile([P, G, PACK, P], I32, name="w1_codes", align_bytes=64)
+        w1s_raw = keep.tile([P, H], U8, name="w1s_raw", align_bytes=64)
+        w1_scales = keep.tile([P, G, PACK, P], U8, name="w1_scales", align_bytes=64)
+        b2_rows = keep.tile([P, H // G], BF16, name="b2_rows")
+        b2_cols = keep.tile([P, B * G, PACK], BF16, name="b2_cols")
+        b3_rows = keep.tile([P, B, O], BF16, name="b3_rows")
+
+        zbytes = []
+        w3_raw = []
+        for b in range(B):
+            w3_tile = loads.tile([P, G, PACK, O], BF16, name="w3_tile", bufs=B)
+            w3_raw.append(w3_tile)
+            for hf in range(HALVES):
+                zb = loads.tile([P, SUB, R], U8, name="zb", bufs=STEPS, align_bytes=64)
+                zbytes.append(zb)
+
+        def load_z(s, n=SUB):
+            b, hf = divmod(s, HALVES)
+            for i in range(0, SUB, n):
+                row = hf * ROWS + i * P
+                nc.sync.dma_start(
+                    out=zbytes[s][:, i : i + n, :],
+                    in_=z2_bytes[row : row + n * P, b, :].rearrange("(i p) k -> p i k", p=P),
+                )
+
+        def load_w3(b):
+            nc.sync.dma_start(
+                out=w3_raw[b][:], in_=w3[b].rearrange("(g p j) o -> p g j o", p=P, j=PACK)
+            )
+
+        nc.vector.memset(warm[:], 0.0)
+        nc.vector.memset(b2_rows[:], 0.0)
+        nc.vector.memset(w1s_raw[:].bitcast(I32), 0)
+        make_identity(nc, ident_f[:])
+        make_identity(nc, ident_b[:])
+        load_z(0, 2)
+        nc.scalar.dma_start(
+            out=kscale[:], in_=z2_scale.rearrange("a c (p t) -> p (a c t)", t=PACK)
+        )
+        nc.scalar.dma_start(
+            out=b2_rows[0 : B * G, :], in_=b2.rearrange("b (g n) -> (b g) n", g=G)
+        )
+        nc.scalar.activation(out=warm[:], in_=warm[:], func=ACT.Relu)
+        w1_words = sw1_words[0].rearrange("p n t -> p (n t)").bitcast(I32)
+        for g in range(G):
+            cols = slice(g * H // G, (g + 1) * H // G)
+            nc.sync.dma_start(out=w1_raw[:, g, :], in_=w1_words[:, cols])
+        for q in range(4):
+            nc.sync.dma_start(
+                out=w1s_raw[32 * q : 32 * q + 4, :].bitcast(I32),
+                in_=sw1_scales[0, 4 * q : 4 * q + 4, :].bitcast(I32),
+            )
+        load_z(1)
+        load_w3(0)
+        load_z(2)
+        load_z(3)
+        load_z(4)
+        load_w3(1)
+        load_z(5)
+        nc.sync.dma_start(
+            out=b3_rows[:].rearrange("p b o -> p (b o)"),
+            in_=b3.rearrange("b o -> (b o)").partition_broadcast(P),
+        )
+        for b in range(2, B):
+            load_w3(b)
+            for s in range(2 * b + 2, min(2 * b + 4, STEPS)):
+                load_z(s)
+
+        zs, zi, zt, zc, zsc = {}, {}, {}, {}, {}
+        hp, hi, hc, hsc, acc1 = {}, {}, {}, {}, {}
+        mixed, acc2, w3i, w3c, w3s = {}, {}, {}, {}, {}
+
+        def permute_w1(g):
+            nc.vector.tensor_copy(
+                out=w1_codes[:, g], in_=w1_raw[:, g].rearrange("p (m t) -> p t m", t=PACK)
+            )
+            nc.vector.tensor_copy(
+                out=w1_scales[:, g],
+                in_=w1s_raw[:, g * H // G : (g + 1) * H // G].rearrange("p (m t) -> p t m", t=PACK),
+            )
+
+        def widen_z(s, copies):
+            t = work.tile([P, SUB, R], BF16, name="zwide", bufs=2)
+            zs[s] = t
+            for i, copy in enumerate(copies):
+                copy(out=t[:, i, :], in_=zbytes[s][:, i, :].bitcast(FP8))
+
+        def transpose_z(s, halves):
+            words = zs[s][:].rearrange("p i k -> p (i k)").bitcast(F32)
+            zt.setdefault(s, [])
+            for half in halves:
+                bank = psum.tile([P, 2, 2, P], F32, name="zbank", bufs=2)
+                zt[s].append(bank)
+                for i in range(2):
+                    base = 256 * (2 * half + i)
+                    for u in range(2):
+                        nc.tensor.transpose(
+                            bank[:, u, i, :], words[:, base + u : base + 256 : 2], ident_f[:]
+                        )
+
+        def scale_z(s, half):
+            if half == 0:
+                t = work.tile([P, ROWS, PACK], BF16, name="zinter", bufs=2, align_bytes=64)
+                zi[s] = t
+            n = ROWS // 2
+            nc.vector.tensor_tensor(
+                out=zi[s][:, half * n : (half + 1) * n, :].rearrange("p n (u e) -> p n u e", e=2),
+                in0=zt[s][half][:]
+                .rearrange("p u i r -> p (u i r)")
+                .bitcast(BF16)
+                .rearrange("p (u n e) -> p n u e", u=2, e=2),
+                in1=kscale[:]
+                .rearrange("p (u e) -> p u e", e=2)
+                .unsqueeze(1)
+                .to_broadcast([P, n, 2, 2]),
+                op=ALU.mult,
+            )
+
+        def quantize_z(s, cols):
+            if cols.start == 0:
+                c = work.tile([P, ROWS], U32, name="zcodes", bufs=2, align_bytes=64)
+                e = work.tile([P, ROWS], U8, name="zexp", bufs=2, align_bytes=64)
+                zc[s], zsc[s] = c, e
+            nc.vector.quantize_mx(
+                out=zc[s][:, cols].bitcast(FP8X4),
+                scales=zsc[s][:, cols],
+                in_=zi[s][:, cols, :].rearrange("p n j -> p (n j)"),
+            )
+
+        def hidden(s, g, cols, slots):
+            for t in slots:
+                if cols.start == 0:
+                    bank = psum.tile([P, ROWS], F32, name="hbank", bufs=4)
+                    acc1[s, g, t] = bank
+                nc.tensor.matmul_mx(
+                    out=acc1[s, g, t][:, cols],
+                    lhsT=w1_codes[:, g, t, :].bitcast(FP8X4),
+                    lhsT_scale=w1_scales[:, g, t, :],
+                    rhs=zc[s][:, cols].bitcast(FP8X4),
+                    rhs_scale=zsc[s][:, cols],
+                    start=True,
+                    stop=True,
+                )
+
+        def relu(s, g, cols):
+            if g == 0 and cols.start == 0:
+                planar = work.tile([P, G, PACK, ROWS], BF16, name="hplanar", bufs=3)
+                inter = work.tile([P, G, ROWS, PACK], BF16, name="hinter", bufs=4, align_bytes=64)
+                hp[s], hi[s] = planar, inter
+            b = s // HALVES
+            for t in range(PACK):
+                nc.scalar.activation(
+                    out=hp[s][:, g, t, cols],
+                    in_=acc1[s, g, t][:, cols],
+                    func=ACT.Relu,
+                    bias=b2_cols[:, b * G + g, t : t + 1],
+                )
+
+        def interleave_vector(s, passes, cols):
+            nc.vector.tensor_copy(
+                out=hi[s][:, passes, cols, :].rearrange("p g (c i) t -> p g c t i", i=4),
+                in_=hp[s][:, passes, :, cols].rearrange("p g t (c i) -> p g c t i", i=4),
+            )
+
+        def interleave_tensor(s, g):
+            bank = psum.tile([P, NT, PACK], BF16, name="ibank", bufs=1)
+            mixed[s, g] = bank
+            for n in range(0, NT, NT // 2):
+                nc.tensor.matmul(
+                    bank[:, n : n + NT // 2, :],
+                    lhsT=ident_b[:],
+                    rhs=hp[s][:, g, :, n : n + NT // 2].rearrange("p t n -> p n t"),
+                    start=True,
+                    stop=True,
+                )
+
+        def copy_h(s, g):
+            nc.scalar.copy(out=hi[s][:, g, 0:NT, :], in_=mixed[s, g][:])
+
+        def quantize_h_part(s, g, cols):
+            nc.vector.quantize_mx(
+                out=hc[s][:, g, cols].bitcast(FP8X4),
+                scales=hsc[s][:, g, cols],
+                in_=hi[s][:, g, cols, :].rearrange("p n j -> p (n j)"),
+            )
+
+        def new_hidden_codes(s):
+            c = work.tile([P, G, ROWS], U32, name="hcodes", bufs=2, align_bytes=64)
+            e = work.tile([P, G, ROWS], U8, name="hexp", bufs=2, align_bytes=64)
+            hc[s], hsc[s] = c, e
+
+        def quantize_h(s):
+            new_hidden_codes(s)
+            c, e = hc[s], hsc[s]
+            nc.vector.quantize_mx(
+                out=c[:].rearrange("p g n -> p (g n)").bitcast(FP8X4),
+                scales=e[:].rearrange("p g n -> p (g n)"),
+                in_=hi[s][:].rearrange("p g n j -> p (g n j)"),
+            )
+
+        def interleave_w3(b):
+            t = work.tile([P, G, O, PACK], BF16, name="w3inter", bufs=2, align_bytes=64)
+            w3i[b] = t
+            copy = nc.scalar.copy if b % 2 == 0 else nc.vector.tensor_copy
+            copy(
+                out=t[:].rearrange("p g (c i) t -> p g c t i", i=4),
+                in_=w3_raw[b][:].rearrange("p g t (c i) -> p g c t i", i=4),
+            )
+
+        def quantize_w3(b):
+            c = work.tile([P, G, O], U32, name="w3codes", bufs=B, align_bytes=64)
+            e = work.tile([P, G, O], U8, name="w3exp", bufs=B, align_bytes=64)
+            w3c[b], w3s[b] = c, e
+            nc.vector.quantize_mx(
+                out=c[:].rearrange("p g o -> p (g o)").bitcast(FP8X4),
+                scales=e[:].rearrange("p g o -> p (g o)"),
+                in_=w3i[b][:].rearrange("p g o j -> p (g o j)"),
+            )
+
+        def output(s, tiles):
+            b = s // HALVES
+            if tiles.start == 0:
+                bank = psum.tile([P, SUB, O], F32, name="obank", bufs=1)
+                acc2[s] = bank
+            bank = acc2[s]
+            for i in tiles:
+                rows = slice(i * P, (i + 1) * P)
+                for g in range(G):
+                    nc.tensor.matmul_mx(
+                        out=bank[:, i, :],
+                        lhsT=hc[s][:, g, rows].bitcast(FP8X4),
+                        lhsT_scale=hsc[s][:, g, rows],
+                        rhs=w3c[b][:, g, :].bitcast(FP8X4),
+                        rhs_scale=w3s[b][:, g, :],
+                        start=(g == 0),
+                        stop=(g == G - 1),
+                    )
+
+        def store(s, tiles):
+            b, hf = divmod(s, HALVES)
+            n = len(tiles)
+            t = work.tile([P, SUB, O], F32, name="result", bufs=3)
+            nc.vector.tensor_tensor(
+                out=t[:, 0:n, :],
+                in0=acc2[s][:, tiles.start : tiles.stop, :],
+                in1=b3_rows[:, b, :].unsqueeze(1).to_broadcast([P, n, O]),
+                op=ALU.add,
+            )
+            row = hf * ROWS + tiles.start * P
+            nc.sync.dma_start(
+                out=out[row : row + n * P, b, :].rearrange("(i p) o -> p i o", p=P),
+                in_=t[:, 0:n, :],
+            )
+
+        whole, left, right = slice(0, ROWS), slice(0, ROWS // 2), slice(ROWS // 2, ROWS)
+        both, rest = slice(0, G), slice(NT, ROWS)
+        on_v, on_s, on_g = nc.vector.tensor_copy, nc.scalar.copy, nc.gpsimd.tensor_copy
+        widen_z(0, [on_v, on_s, on_v, on_s])
+        widen_z(1, [on_s, on_s, on_s, on_s])
+        interleave_w3(0)
+        transpose_z(0, [0, 1])
+        bank = psum.tile([P, SUB, O], F32, name="obank", bufs=1)
+        b2_words = b2_rows[:].bitcast(F32)
+        for u in range(2):
+            nc.tensor.transpose(bank[:, u, :], b2_words[:, u::2], ident_f[:])
+        nc.scalar.copy(
+            out=b2_cols[:].rearrange("p c t -> p (c t)").bitcast(F32).rearrange("p (c u) -> p c u", u=2),
+            in_=bank[:, 0:2, 0 : B * G].rearrange("p u c -> p c u"),
+        )
+        scale_z(0, 0)
+        permute_w1(0)
+        quantize_z(0, left)
+        transpose_z(1, [0])
+        hidden(0, 0, left, range(PACK))
+        relu(0, 0, left)
+        scale_z(0, 1)
+        transpose_z(1, [1])
+        scale_z(1, 0)
+        quantize_z(0, right)
+        permute_w1(1)
+        scale_z(1, 1)
+        hidden(0, 0, right, range(PACK))
+        relu(0, 0, right)
+        widen_z(2, [on_g] * SUB)
+        widen_z(3, [on_g] * SUB)
+
+        last = STEPS - 1
+        for s in range(STEPS):
+            if s >= 1:
+                hidden(s, 0, whole, range(PACK))
+                relu(s, 0, whole)
+                interleave_vector(s - 1, both, rest)
+                interleave_tensor(s - 1, 1)
+                copy_h(s - 1, 1)
+            if s + 1 < STEPS:
+                quantize_z(s + 1, whole)
+            if s >= 2:
+                quantize_h(s - 2)
+            hidden(s, 1, whole, (0, 1))
+            if s % HALVES == 0:
+                quantize_w3(s // HALVES)
+            if s + 2 < STEPS:
+                transpose_z(s + 2, [0, 1])
+                scale_z(s + 2, 0)
+                scale_z(s + 2, 1)
+            if s + 4 < STEPS:
+                widen_z(s + 4, [on_g] * SUB)
+            if s % HALVES == 1 and s // HALVES + 1 < B:
+                interleave_w3(s // HALVES + 1)
+            hidden(s, 1, whole, (2, 3))
+            if s < last:
+                relu(s, 1, whole)
+                if s >= 2:
+                    output(s - 2, range(SUB))
+                    store(s - 2, range(SUB))
+                interleave_tensor(s, 0)
+                copy_h(s, 0)
+
+        relu(last, 1, left)
+        interleave_vector(last, slice(0, 1), rest)
+        output(last - 2, range(SUB))
+        interleave_tensor(last, 0)
+        copy_h(last, 0)
+        relu(last, 1, right)
+        store(last - 2, range(SUB))
+        quantize_h(last - 1)
+        interleave_vector(last, slice(1, 2), left)
+        output(last - 1, range(SUB))
+        new_hidden_codes(last)
+        quantize_h_part(last, 0, whole)
+        interleave_vector(last, slice(1, 2), right)
+        store(last - 1, range(SUB))
+        for cols, tiles in ((left, range(0, 2)), (right, range(2, 4))):
+            quantize_h_part(last, 1, cols)
+            output(last, tiles)
+        for tiles in (range(0, 2), range(2, 4)):
+            store(last, tiles)

@@ -23,7 +23,9 @@ ROWS = 512
 SUB = ROWS // P
 HALVES = T // ROWS
 STEPS = B * HALVES
-NT = 240
+NT = 256
+W3_ON_SCALAR = {3: 2, 5: 3, 7: 4, 9: 5}
+ZBUFS = 3
 
 
 def tile_mlpmodelpredictor_pb_t_w8_kernel(
@@ -49,13 +51,21 @@ def tile_mlpmodelpredictor_pb_t_w8_kernel(
         b2_cols = keep.tile([P, B * G, PACK], BF16, name="b2_cols")
         b3_rows = keep.tile([P, B, O], BF16, name="b3_rows")
 
+        zbuf = []
+        for i in range(ZBUFS):
+            t = keep.tile([P, ROWS * PACK], BF16, name="zbuf%d" % i, align_bytes=64)
+            zbuf.append(t)
+
+        def zbuf_of(s):
+            return zbuf[(s if s > 0 else 2) % ZBUFS]
+
         zbytes = []
         w3_raw = []
         for b in range(B):
             w3_tile = loads.tile([P, G, PACK, O], BF16, name="w3_tile", bufs=B)
             w3_raw.append(w3_tile)
             for hf in range(HALVES):
-                zb = loads.tile([P, SUB, R], U8, name="zb", bufs=STEPS, align_bytes=64)
+                zb = loads.tile([P, SUB * R], U8, name="zb", bufs=STEPS, align_bytes=64)
                 zbytes.append(zb)
 
         def load_z(s, n=SUB):
@@ -63,7 +73,7 @@ def tile_mlpmodelpredictor_pb_t_w8_kernel(
             for i in range(0, SUB, n):
                 row = hf * ROWS + i * P
                 nc.sync.dma_start(
-                    out=zbytes[s][:, i : i + n, :],
+                    out=zbytes[s][:, i * R : (i + n) * R].rearrange("p (i k) -> p i k", k=R),
                     in_=z2_bytes[row : row + n * P, b, :].rearrange("(i p) k -> p i k", p=P),
                 )
 
@@ -81,36 +91,37 @@ def tile_mlpmodelpredictor_pb_t_w8_kernel(
         nc.scalar.dma_start(
             out=kscale[:], in_=z2_scale.rearrange("a c (p t) -> p (a c t)", t=PACK)
         )
-        nc.scalar.dma_start(
-            out=b2_rows[0 : B * G, :], in_=b2.rearrange("b (g n) -> (b g) n", g=G)
-        )
-        nc.scalar.activation(out=warm[:], in_=warm[:], func=ACT.Relu)
         w1_words = sw1_words[0].rearrange("p n t -> p (n t)").bitcast(I32)
-        for g in range(G):
-            cols = slice(g * H // G, (g + 1) * H // G)
-            nc.sync.dma_start(out=w1_raw[:, g, :], in_=w1_words[:, cols])
+        nc.sync.dma_start(out=w1_raw[:, 0, :], in_=w1_words[:, 0 : H // G])
         for q in range(4):
             nc.sync.dma_start(
                 out=w1s_raw[32 * q : 32 * q + 4, :].bitcast(I32),
                 in_=sw1_scales[0, 4 * q : 4 * q + 4, :].bitcast(I32),
             )
+        nc.scalar.activation(out=warm[:], in_=warm[:], func=ACT.Relu)
+        nc.sync.dma_start(
+            out=b2_rows[0 : B * G, :], in_=b2.rearrange("b (g n) -> (b g) n", g=G)
+        )
         load_z(1)
-        load_w3(0)
+        nc.sync.dma_start(out=w1_raw[:, 1, :], in_=w1_words[:, H // G : H])
         load_z(2)
         load_z(3)
         load_z(4)
+        load_w3(0)
         load_w3(1)
         load_z(5)
+        load_w3(2)
+        load_w3(3)
         nc.sync.dma_start(
             out=b3_rows[:].rearrange("p b o -> p (b o)"),
             in_=b3.rearrange("b o -> (b o)").partition_broadcast(P),
         )
-        for b in range(2, B):
+        for b in range(4, B):
             load_w3(b)
-            for s in range(2 * b + 2, min(2 * b + 4, STEPS)):
-                load_z(s)
+        for s in range(6, STEPS):
+            load_z(s)
 
-        zs, zi, zt, zc, zsc = {}, {}, {}, {}, {}
+        zt, zc, zsc = {}, {}, {}
         hp, hi, hc, hsc, acc1 = {}, {}, {}, {}, {}
         mixed, acc2, w3i, w3c, w3s = {}, {}, {}, {}, {}
 
@@ -123,14 +134,12 @@ def tile_mlpmodelpredictor_pb_t_w8_kernel(
                 in_=w1s_raw[:, g * H // G : (g + 1) * H // G].rearrange("p (m t) -> p t m", t=PACK),
             )
 
-        def widen_z(s, copies):
-            t = work.tile([P, SUB, R], BF16, name="zwide", bufs=2)
-            zs[s] = t
-            for i, copy in enumerate(copies):
-                copy(out=t[:, i, :], in_=zbytes[s][:, i, :].bitcast(FP8))
+        def widen_z(s, copy, tiles):
+            cols = slice(tiles.start * R, tiles.stop * R)
+            copy(out=zbuf_of(s)[:, cols], in_=zbytes[s][:, cols].bitcast(FP8))
 
         def transpose_z(s, halves):
-            words = zs[s][:].rearrange("p i k -> p (i k)").bitcast(F32)
+            words = zbuf_of(s)[:].bitcast(F32)
             zt.setdefault(s, [])
             for half in halves:
                 bank = psum.tile([P, 2, 2, P], F32, name="zbank", bufs=2)
@@ -143,12 +152,11 @@ def tile_mlpmodelpredictor_pb_t_w8_kernel(
                         )
 
         def scale_z(s, half):
-            if half == 0:
-                t = work.tile([P, ROWS, PACK], BF16, name="zinter", bufs=2, align_bytes=64)
-                zi[s] = t
             n = ROWS // 2
             nc.vector.tensor_tensor(
-                out=zi[s][:, half * n : (half + 1) * n, :].rearrange("p n (u e) -> p n u e", e=2),
+                out=zbuf_of(s)[:, half * n * PACK : (half + 1) * n * PACK].rearrange(
+                    "p (n u e) -> p n u e", u=2, e=2
+                ),
                 in0=zt[s][half][:]
                 .rearrange("p u i r -> p (u i r)")
                 .bitcast(BF16)
@@ -162,13 +170,13 @@ def tile_mlpmodelpredictor_pb_t_w8_kernel(
 
         def quantize_z(s, cols):
             if cols.start == 0:
-                c = work.tile([P, ROWS], U32, name="zcodes", bufs=2, align_bytes=64)
-                e = work.tile([P, ROWS], U8, name="zexp", bufs=2, align_bytes=64)
+                c = work.tile([P, ROWS], U32, name="zcodes", bufs=3, align_bytes=64)
+                e = work.tile([P, ROWS], U8, name="zexp", bufs=3, align_bytes=64)
                 zc[s], zsc[s] = c, e
             nc.vector.quantize_mx(
                 out=zc[s][:, cols].bitcast(FP8X4),
                 scales=zsc[s][:, cols],
-                in_=zi[s][:, cols, :].rearrange("p n j -> p (n j)"),
+                in_=zbuf_of(s)[:, cols.start * PACK : cols.stop * PACK],
             )
 
         def hidden(s, g, cols, slots):
@@ -219,7 +227,10 @@ def tile_mlpmodelpredictor_pb_t_w8_kernel(
                 )
 
         def copy_h(s, g):
-            nc.scalar.copy(out=hi[s][:, g, 0:NT, :], in_=mixed[s, g][:])
+            nc.scalar.copy(
+                out=hi[s][:, g, 0:NT, :].rearrange("p n t -> p (n t)").bitcast(F32),
+                in_=mixed[s, g][:].rearrange("p n t -> p (n t)").bitcast(F32),
+            )
 
         def quantize_h_part(s, g, cols):
             nc.vector.quantize_mx(
@@ -229,8 +240,8 @@ def tile_mlpmodelpredictor_pb_t_w8_kernel(
             )
 
         def new_hidden_codes(s):
-            c = work.tile([P, G, ROWS], U32, name="hcodes", bufs=2, align_bytes=64)
-            e = work.tile([P, G, ROWS], U8, name="hexp", bufs=2, align_bytes=64)
+            c = work.tile([P, G, ROWS], U32, name="hcodes", bufs=3, align_bytes=64)
+            e = work.tile([P, G, ROWS], U8, name="hexp", bufs=3, align_bytes=64)
             hc[s], hsc[s] = c, e
 
         def quantize_h(s):
@@ -242,10 +253,9 @@ def tile_mlpmodelpredictor_pb_t_w8_kernel(
                 in_=hi[s][:].rearrange("p g n j -> p (g n j)"),
             )
 
-        def interleave_w3(b):
-            t = work.tile([P, G, O, PACK], BF16, name="w3inter", bufs=2, align_bytes=64)
+        def interleave_w3(b, copy):
+            t = work.tile([P, G, O, PACK], BF16, name="w3inter", bufs=3, align_bytes=64)
             w3i[b] = t
-            copy = nc.scalar.copy if b % 2 == 0 else nc.vector.tensor_copy
             copy(
                 out=t[:].rearrange("p g (c i) t -> p g c t i", i=4),
                 in_=w3_raw[b][:].rearrange("p g t (c i) -> p g c t i", i=4),
@@ -261,12 +271,10 @@ def tile_mlpmodelpredictor_pb_t_w8_kernel(
                 in_=w3i[b][:].rearrange("p g o j -> p (g o j)"),
             )
 
-        def output(s, tiles):
+        def output(s, tiles, tag="obank"):
             b = s // HALVES
-            if tiles.start == 0:
-                bank = psum.tile([P, SUB, O], F32, name="obank", bufs=1)
-                acc2[s] = bank
-            bank = acc2[s]
+            bank = psum.tile([P, SUB, O], F32, name=tag, bufs=1 if tag == "obank" else 2)
+            acc2[s] = bank
             for i in tiles:
                 rows = slice(i * P, (i + 1) * P)
                 for g in range(G):
@@ -299,14 +307,14 @@ def tile_mlpmodelpredictor_pb_t_w8_kernel(
         whole, left, right = slice(0, ROWS), slice(0, ROWS // 2), slice(ROWS // 2, ROWS)
         both, rest = slice(0, G), slice(NT, ROWS)
         on_v, on_s, on_g = nc.vector.tensor_copy, nc.scalar.copy, nc.gpsimd.tensor_copy
-        widen_z(0, [on_v, on_s, on_v, on_s])
-        widen_z(1, [on_s, on_s, on_s, on_s])
-        interleave_w3(0)
+        for i, copy in enumerate((on_v, on_s, on_v, on_s)):
+            widen_z(0, copy, range(i, i + 1))
         transpose_z(0, [0, 1])
         bank = psum.tile([P, SUB, O], F32, name="obank", bufs=1)
         b2_words = b2_rows[:].bitcast(F32)
         for u in range(2):
             nc.tensor.transpose(bank[:, u, :], b2_words[:, u::2], ident_f[:])
+        widen_z(1, on_s, range(0, 2))
         nc.scalar.copy(
             out=b2_cols[:].rearrange("p c t -> p (c t)").bitcast(F32).rearrange("p (c u) -> p c u", u=2),
             in_=bank[:, 0:2, 0 : B * G].rearrange("p u c -> p c u"),
@@ -314,68 +322,95 @@ def tile_mlpmodelpredictor_pb_t_w8_kernel(
         scale_z(0, 0)
         permute_w1(0)
         quantize_z(0, left)
-        transpose_z(1, [0])
         hidden(0, 0, left, range(PACK))
         relu(0, 0, left)
         scale_z(0, 1)
-        transpose_z(1, [1])
-        scale_z(1, 0)
+        widen_z(1, on_v, range(2, 4))
         quantize_z(0, right)
-        permute_w1(1)
-        scale_z(1, 1)
+        transpose_z(1, [0])
         hidden(0, 0, right, range(PACK))
         relu(0, 0, right)
-        widen_z(2, [on_g] * SUB)
-        widen_z(3, [on_g] * SUB)
+        permute_w1(1)
+        widen_z(2, on_g, range(SUB))
+        transpose_z(1, [1])
+        scale_z(1, 0)
+        scale_z(1, 1)
+        hidden(0, 1, whole, range(PACK))
 
         last = STEPS - 1
-        for s in range(STEPS):
+        for s in range(STEPS - 1):
             if s >= 1:
-                hidden(s, 0, whole, range(PACK))
                 relu(s, 0, whole)
-                interleave_vector(s - 1, both, rest)
                 interleave_tensor(s - 1, 1)
                 copy_h(s - 1, 1)
-            if s + 1 < STEPS:
-                quantize_z(s + 1, whole)
+                interleave_vector(s - 1, both, rest)
+            if s == 1:
+                interleave_w3(0, on_v)
+                interleave_w3(1, on_v)
+                quantize_w3(0)
+            if s in W3_ON_SCALAR:
+                interleave_w3(W3_ON_SCALAR[s], on_s)
+            if s - 1 in W3_ON_SCALAR:
+                quantize_w3(W3_ON_SCALAR[s - 1])
+            quantize_z(s + 1, whole)
             if s >= 2:
                 quantize_h(s - 2)
-            hidden(s, 1, whole, (0, 1))
-            if s % HALVES == 0:
-                quantize_w3(s // HALVES)
-            if s + 2 < STEPS:
+            elif s == 1:
+                quantize_w3(1)
+            else:
+                widen_z(3, on_v, range(SUB))
+            if s + 4 < STEPS:
+                widen_z(s + 4, on_g, range(SUB))
+            if s >= 3:
+                output(s - 3, range(SUB))
+            if s >= 1:
+                hidden(s, 1, whole, (0, 1))
+            if 1 <= s < STEPS - 2:
                 transpose_z(s + 2, [0, 1])
+            if s >= 1:
+                hidden(s, 1, whole, (2, 3))
+            relu(s, 1, whole)
+            interleave_tensor(s, 0)
+            copy_h(s, 0)
+            if s == 0:
+                transpose_z(2, [0, 1])
+            hidden(s + 1, 0, whole, range(PACK))
+            if s + 2 < STEPS:
                 scale_z(s + 2, 0)
                 scale_z(s + 2, 1)
-            if s + 4 < STEPS:
-                widen_z(s + 4, [on_g] * SUB)
-            if s % HALVES == 1 and s // HALVES + 1 < B:
-                interleave_w3(s // HALVES + 1)
-            hidden(s, 1, whole, (2, 3))
-            if s < last:
-                relu(s, 1, whole)
-                if s >= 2:
-                    output(s - 2, range(SUB))
-                    store(s - 2, range(SUB))
-                interleave_tensor(s, 0)
-                copy_h(s, 0)
+            if s >= 3:
+                store(s - 3, range(SUB))
 
+        interleave_w3(B - 2, on_v)
+        interleave_w3(B - 1, on_v)
+        quantize_w3(B - 2)
+        quantize_h(last - 2)
+        quantize_w3(B - 1)
+        output(last - 3, range(SUB), "zbank")
+        relu(last, 0, whole)
+        interleave_tensor(last - 1, 1)
+        copy_h(last - 1, 1)
+        output(last - 2, range(SUB), "zbank")
+        hidden(last, 1, whole, range(PACK))
+        store(last - 3, range(SUB))
+        interleave_vector(last - 1, both, rest)
+        store(last - 2, range(SUB))
         relu(last, 1, left)
         interleave_vector(last, slice(0, 1), rest)
-        output(last - 2, range(SUB))
+        quantize_h(last - 1)
         interleave_tensor(last, 0)
         copy_h(last, 0)
-        relu(last, 1, right)
-        store(last - 2, range(SUB))
-        quantize_h(last - 1)
-        interleave_vector(last, slice(1, 2), left)
+        interleave_tensor(last, 1)
         output(last - 1, range(SUB))
+        relu(last, 1, right)
+        copy_h(last, 1)
         new_hidden_codes(last)
         quantize_h_part(last, 0, whole)
-        interleave_vector(last, slice(1, 2), right)
         store(last - 1, range(SUB))
-        for cols, tiles in ((left, range(0, 2)), (right, range(2, 4))):
-            quantize_h_part(last, 1, cols)
-            output(last, tiles)
-        for tiles in (range(0, 2), range(2, 4)):
-            store(last, tiles)
+        interleave_vector(last, slice(1, 2), right)
+        quantize_h_part(last, 1, left)
+        quantize_h_part(last, 1, right)
+        output(last, range(0, 2), "zbank")
+        store(last, range(0, 2))
+        output(last, range(2, 4), "zbank")
+        store(last, range(2, 4))

@@ -197,8 +197,12 @@ def tile_mlpmodelpredictor_pb_t_w8_kernel(
         def relu(s, g, cols):
             if g == 0 and cols.start == 0:
                 planar = work.tile([P, G, PACK, ROWS], BF16, name="hplanar", bufs=3)
-                inter = work.tile([P, G, ROWS, PACK], BF16, name="hinter", bufs=4, align_bytes=64)
-                hp[s], hi[s] = planar, inter
+                hp[s] = planar
+                for side in range(2):
+                    inter = work.tile(
+                        [P, G, NT, PACK], BF16, name="hinter%d" % side, bufs=4, align_bytes=64
+                    )
+                    hi[s, side] = inter
             b = s // HALVES
             for t in range(PACK):
                 nc.scalar.activation(
@@ -208,10 +212,10 @@ def tile_mlpmodelpredictor_pb_t_w8_kernel(
                     bias=b2_cols[:, b * G + g, t : t + 1],
                 )
 
-        def interleave_vector(s, passes, cols):
+        def interleave_vector(s, passes):
             nc.vector.tensor_copy(
-                out=hi[s][:, passes, cols, :].rearrange("p g (c i) t -> p g c t i", i=4),
-                in_=hp[s][:, passes, :, cols].rearrange("p g t (c i) -> p g c t i", i=4),
+                out=hi[s, 1][:, passes].rearrange("p g (c i) t -> p g c t i", i=4),
+                in_=hp[s][:, passes, :, NT:ROWS].rearrange("p g t (c i) -> p g c t i", i=4),
             )
 
         def interleave_tensor(s, g):
@@ -228,29 +232,19 @@ def tile_mlpmodelpredictor_pb_t_w8_kernel(
 
         def copy_h(s, g):
             nc.scalar.copy(
-                out=hi[s][:, g, 0:NT, :].rearrange("p n t -> p (n t)").bitcast(F32),
+                out=hi[s, 0][:, g].rearrange("p n t -> p (n t)").bitcast(F32),
                 in_=mixed[s, g][:].rearrange("p n t -> p (n t)").bitcast(F32),
             )
 
-        def quantize_h_part(s, g, cols):
+        def quantize_h(s, side, passes):
+            if passes.start == 0:
+                c = work.tile([P, G, NT], U32, name="hcodes%d" % side, bufs=3, align_bytes=64)
+                e = work.tile([P, G, NT], U8, name="hexp%d" % side, bufs=3, align_bytes=64)
+                hc[s, side], hsc[s, side] = c, e
             nc.vector.quantize_mx(
-                out=hc[s][:, g, cols].bitcast(FP8X4),
-                scales=hsc[s][:, g, cols],
-                in_=hi[s][:, g, cols, :].rearrange("p n j -> p (n j)"),
-            )
-
-        def new_hidden_codes(s):
-            c = work.tile([P, G, ROWS], U32, name="hcodes", bufs=3, align_bytes=64)
-            e = work.tile([P, G, ROWS], U8, name="hexp", bufs=3, align_bytes=64)
-            hc[s], hsc[s] = c, e
-
-        def quantize_h(s):
-            new_hidden_codes(s)
-            c, e = hc[s], hsc[s]
-            nc.vector.quantize_mx(
-                out=c[:].rearrange("p g n -> p (g n)").bitcast(FP8X4),
-                scales=e[:].rearrange("p g n -> p (g n)"),
-                in_=hi[s][:].rearrange("p g n j -> p (g n j)"),
+                out=hc[s, side][:, passes].rearrange("p g n -> p (g n)").bitcast(FP8X4),
+                scales=hsc[s, side][:, passes].rearrange("p g n -> p (g n)"),
+                in_=hi[s, side][:, passes].rearrange("p g n j -> p (g n j)"),
             )
 
         def interleave_w3(b, copy):
@@ -276,12 +270,13 @@ def tile_mlpmodelpredictor_pb_t_w8_kernel(
             bank = psum.tile([P, SUB, O], F32, name=tag, bufs=1 if tag == "obank" else 2)
             acc2[s] = bank
             for i in tiles:
-                rows = slice(i * P, (i + 1) * P)
+                side, j = divmod(i, SUB // 2)
+                rows = slice(j * P, (j + 1) * P)
                 for g in range(G):
                     nc.tensor.matmul_mx(
                         out=bank[:, i, :],
-                        lhsT=hc[s][:, g, rows].bitcast(FP8X4),
-                        lhsT_scale=hsc[s][:, g, rows],
+                        lhsT=hc[s, side][:, g, rows].bitcast(FP8X4),
+                        lhsT_scale=hsc[s, side][:, g, rows],
                         rhs=w3c[b][:, g, :].bitcast(FP8X4),
                         rhs_scale=w3s[b][:, g, :],
                         start=(g == 0),
@@ -305,7 +300,7 @@ def tile_mlpmodelpredictor_pb_t_w8_kernel(
             )
 
         whole, left, right = slice(0, ROWS), slice(0, ROWS // 2), slice(ROWS // 2, ROWS)
-        both, rest = slice(0, G), slice(NT, ROWS)
+        both, first, second = slice(0, G), slice(0, 1), slice(1, 2)
         on_v, on_s, on_g = nc.vector.tensor_copy, nc.scalar.copy, nc.gpsimd.tensor_copy
         for i, copy in enumerate((on_v, on_s, on_v, on_s)):
             widen_z(0, copy, range(i, i + 1))
@@ -343,7 +338,7 @@ def tile_mlpmodelpredictor_pb_t_w8_kernel(
                 relu(s, 0, whole)
                 interleave_tensor(s - 1, 1)
                 copy_h(s - 1, 1)
-                interleave_vector(s - 1, both, rest)
+                interleave_vector(s - 1, both)
             if s == 1:
                 interleave_w3(0, on_v)
                 interleave_w3(1, on_v)
@@ -352,9 +347,11 @@ def tile_mlpmodelpredictor_pb_t_w8_kernel(
                 interleave_w3(W3_ON_SCALAR[s], on_s)
             if s - 1 in W3_ON_SCALAR:
                 quantize_w3(W3_ON_SCALAR[s - 1])
+            if s >= 2:
+                quantize_h(s - 2, 0, both)
             quantize_z(s + 1, whole)
             if s >= 2:
-                quantize_h(s - 2)
+                quantize_h(s - 2, 1, both)
             elif s == 1:
                 quantize_w3(1)
             else:
@@ -384,7 +381,8 @@ def tile_mlpmodelpredictor_pb_t_w8_kernel(
         interleave_w3(B - 2, on_v)
         interleave_w3(B - 1, on_v)
         quantize_w3(B - 2)
-        quantize_h(last - 2)
+        quantize_h(last - 2, 0, both)
+        quantize_h(last - 2, 1, both)
         quantize_w3(B - 1)
         output(last - 3, range(SUB), "zbank")
         relu(last, 0, whole)
@@ -393,23 +391,24 @@ def tile_mlpmodelpredictor_pb_t_w8_kernel(
         output(last - 2, range(SUB), "zbank")
         hidden(last, 1, whole, range(PACK))
         store(last - 3, range(SUB))
-        interleave_vector(last - 1, both, rest)
+        interleave_vector(last - 1, both)
         store(last - 2, range(SUB))
         relu(last, 1, left)
-        interleave_vector(last, slice(0, 1), rest)
-        quantize_h(last - 1)
+        interleave_vector(last, first)
+        quantize_h(last - 1, 1, both)
+        quantize_h(last - 1, 0, both)
         interleave_tensor(last, 0)
         copy_h(last, 0)
         interleave_tensor(last, 1)
         output(last - 1, range(SUB))
         relu(last, 1, right)
         copy_h(last, 1)
-        new_hidden_codes(last)
-        quantize_h_part(last, 0, whole)
+        quantize_h(last, 1, first)
+        quantize_h(last, 0, first)
         store(last - 1, range(SUB))
-        interleave_vector(last, slice(1, 2), right)
-        quantize_h_part(last, 1, left)
-        quantize_h_part(last, 1, right)
+        interleave_vector(last, second)
+        quantize_h(last, 0, second)
+        quantize_h(last, 1, second)
         output(last, range(0, 2), "zbank")
         store(last, range(0, 2))
         output(last, range(2, 4), "zbank")

@@ -23,8 +23,8 @@ ROWS = 512
 SUB = ROWS // P
 HALVES = T // ROWS
 STEPS = B * HALVES
-NT = 256
-W3_ON_SCALAR = {3: 2, 5: 3, 7: 4, 9: 5}
+NT = 192
+W3_ON_SCALAR = {3: 2, 5: 3, 7: 4, 9: 5, 11: 6, 12: 7}
 ZBUFS = 3
 
 
@@ -198,11 +198,8 @@ def tile_mlpmodelpredictor_pb_t_w8_kernel(
             if g == 0 and cols.start == 0:
                 planar = work.tile([P, G, PACK, ROWS], BF16, name="hplanar", bufs=3)
                 hp[s] = planar
-                for side in range(2):
-                    inter = work.tile(
-                        [P, G, NT, PACK], BF16, name="hinter%d" % side, bufs=4, align_bytes=64
-                    )
-                    hi[s, side] = inter
+                inter = work.tile([P, G * ROWS * PACK], BF16, name="hinter", bufs=4, align_bytes=64)
+                hi[s] = inter
             b = s // HALVES
             for t in range(PACK):
                 nc.scalar.activation(
@@ -212,39 +209,43 @@ def tile_mlpmodelpredictor_pb_t_w8_kernel(
                     bias=b2_cols[:, b * G + g, t : t + 1],
                 )
 
-        def interleave_vector(s, passes):
+        def interleave_vector(s, passes, cols):
             nc.vector.tensor_copy(
-                out=hi[s, 1][:, passes].rearrange("p g (c i) t -> p g c t i", i=4),
-                in_=hp[s][:, passes, :, NT:ROWS].rearrange("p g t (c i) -> p g c t i", i=4),
+                out=hi[s][:]
+                .rearrange("p (g n t) -> p g n t", g=G, t=PACK)[:, passes, cols, :]
+                .rearrange("p g (c i) t -> p g c t i", i=4),
+                in_=hp[s][:, passes, :, cols].rearrange("p g t (c i) -> p g c t i", i=4),
             )
 
-        def interleave_tensor(s, g):
-            bank = psum.tile([P, NT, PACK], BF16, name="ibank", bufs=1)
+        def interleave_tensor(s, g, nt=NT, tag="ibank"):
+            bank = psum.tile([P, ROWS // 2, PACK], BF16, name=tag, bufs=1 if tag == "ibank" else 2)
             mixed[s, g] = bank
-            for n in range(0, NT, NT // 2):
+            for n in range(0, nt, nt // 2):
                 nc.tensor.matmul(
-                    bank[:, n : n + NT // 2, :],
+                    bank[:, n : n + nt // 2, :],
                     lhsT=ident_b[:],
-                    rhs=hp[s][:, g, :, n : n + NT // 2].rearrange("p t n -> p n t"),
+                    rhs=hp[s][:, g, :, n : n + nt // 2].rearrange("p t n -> p n t"),
                     start=True,
                     stop=True,
                 )
 
-        def copy_h(s, g):
+        def copy_h(s, g, nt=NT):
+            start = g * ROWS * PACK
             nc.scalar.copy(
-                out=hi[s, 0][:, g].rearrange("p n t -> p (n t)").bitcast(F32),
-                in_=mixed[s, g][:].rearrange("p n t -> p (n t)").bitcast(F32),
+                out=hi[s][:, start : start + nt * PACK].bitcast(F32),
+                in_=mixed[s, g][:, 0:nt, :].rearrange("p n t -> p (n t)").bitcast(F32),
             )
 
-        def quantize_h(s, side, passes):
-            if passes.start == 0:
-                c = work.tile([P, G, NT], U32, name="hcodes%d" % side, bufs=3, align_bytes=64)
-                e = work.tile([P, G, NT], U8, name="hexp%d" % side, bufs=3, align_bytes=64)
-                hc[s, side], hsc[s, side] = c, e
+        def quantize_h(s, g, cols):
+            if g == 0 and cols.start == 0:
+                c = work.tile([P, G, ROWS], U32, name="hcodes", bufs=3, align_bytes=64)
+                e = work.tile([P, G, ROWS], U8, name="hexp", bufs=3, align_bytes=64)
+                hc[s], hsc[s] = c, e
+            start = g * ROWS
             nc.vector.quantize_mx(
-                out=hc[s, side][:, passes].rearrange("p g n -> p (g n)").bitcast(FP8X4),
-                scales=hsc[s, side][:, passes].rearrange("p g n -> p (g n)"),
-                in_=hi[s, side][:, passes].rearrange("p g n j -> p (g n j)"),
+                out=hc[s][:, g, cols].bitcast(FP8X4),
+                scales=hsc[s][:, g, cols],
+                in_=hi[s][:, (start + cols.start) * PACK : (start + cols.stop) * PACK],
             )
 
         def interleave_w3(b, copy):
@@ -270,13 +271,12 @@ def tile_mlpmodelpredictor_pb_t_w8_kernel(
             bank = psum.tile([P, SUB, O], F32, name=tag, bufs=1 if tag == "obank" else 2)
             acc2[s] = bank
             for i in tiles:
-                side, j = divmod(i, SUB // 2)
-                rows = slice(j * P, (j + 1) * P)
+                rows = slice(i * P, (i + 1) * P)
                 for g in range(G):
                     nc.tensor.matmul_mx(
                         out=bank[:, i, :],
-                        lhsT=hc[s, side][:, g, rows].bitcast(FP8X4),
-                        lhsT_scale=hsc[s, side][:, g, rows],
+                        lhsT=hc[s][:, g, rows].bitcast(FP8X4),
+                        lhsT_scale=hsc[s][:, g, rows],
                         rhs=w3c[b][:, g, :].bitcast(FP8X4),
                         rhs_scale=w3s[b][:, g, :],
                         start=(g == 0),
@@ -301,6 +301,7 @@ def tile_mlpmodelpredictor_pb_t_w8_kernel(
 
         whole, left, right = slice(0, ROWS), slice(0, ROWS // 2), slice(ROWS // 2, ROWS)
         both, first, second = slice(0, G), slice(0, 1), slice(1, 2)
+        rest = slice(NT, ROWS)
         on_v, on_s, on_g = nc.vector.tensor_copy, nc.scalar.copy, nc.gpsimd.tensor_copy
         for i, copy in enumerate((on_v, on_s, on_v, on_s)):
             widen_z(0, copy, range(i, i + 1))
@@ -338,7 +339,7 @@ def tile_mlpmodelpredictor_pb_t_w8_kernel(
                 relu(s, 0, whole)
                 interleave_tensor(s - 1, 1)
                 copy_h(s - 1, 1)
-                interleave_vector(s - 1, both)
+                interleave_vector(s - 1, both, rest)
             if s == 1:
                 interleave_w3(0, on_v)
                 interleave_w3(1, on_v)
@@ -348,10 +349,10 @@ def tile_mlpmodelpredictor_pb_t_w8_kernel(
             if s - 1 in W3_ON_SCALAR:
                 quantize_w3(W3_ON_SCALAR[s - 1])
             if s >= 2:
-                quantize_h(s - 2, 0, both)
+                quantize_h(s - 2, 0, whole)
             quantize_z(s + 1, whole)
             if s >= 2:
-                quantize_h(s - 2, 1, both)
+                quantize_h(s - 2, 1, whole)
             elif s == 1:
                 quantize_w3(1)
             else:
@@ -378,38 +379,32 @@ def tile_mlpmodelpredictor_pb_t_w8_kernel(
             if s >= 3:
                 store(s - 3, range(SUB))
 
-        interleave_w3(B - 2, on_v)
-        interleave_w3(B - 1, on_v)
-        quantize_w3(B - 2)
-        quantize_h(last - 2, 0, both)
-        quantize_h(last - 2, 1, both)
-        quantize_w3(B - 1)
-        output(last - 3, range(SUB), "zbank")
+        quantize_h(last - 2, 0, whole)
+        quantize_h(last - 2, 1, whole)
+        output(last - 3, range(SUB))
         relu(last, 0, whole)
         interleave_tensor(last - 1, 1)
         copy_h(last - 1, 1)
         output(last - 2, range(SUB), "zbank")
         hidden(last, 1, whole, range(PACK))
         store(last - 3, range(SUB))
-        interleave_vector(last - 1, both)
+        interleave_vector(last - 1, both, rest)
         store(last - 2, range(SUB))
+        interleave_tensor(last, 0, ROWS // 2, "zbank")
         relu(last, 1, left)
-        interleave_vector(last, first)
-        quantize_h(last - 1, 1, both)
-        quantize_h(last - 1, 0, both)
-        interleave_tensor(last, 0)
-        copy_h(last, 0)
-        interleave_tensor(last, 1)
-        output(last - 1, range(SUB))
+        copy_h(last, 0, ROWS // 2)
         relu(last, 1, right)
-        copy_h(last, 1)
-        quantize_h(last, 1, first)
-        quantize_h(last, 0, first)
-        store(last - 1, range(SUB))
-        interleave_vector(last, second)
-        quantize_h(last, 0, second)
-        quantize_h(last, 1, second)
+        quantize_h(last - 1, 0, whole)
+        interleave_vector(last, first, right)
+        quantize_h(last - 1, 1, whole)
+        output(last - 1, range(SUB))
+        interleave_vector(last, second, left)
+        quantize_h(last, 0, whole)
+        quantize_h(last, 1, left)
+        interleave_vector(last, second, right)
         output(last, range(0, 2), "zbank")
+        store(last - 1, range(SUB))
+        quantize_h(last, 1, right)
         store(last, range(0, 2))
         output(last, range(2, 4), "zbank")
         store(last, range(2, 4))

@@ -210,12 +210,14 @@ def tile_mlpmodelpredictor_pb_t_w8_kernel(
                 )
 
         def interleave_vector(s, passes, cols):
-            nc.vector.tensor_copy(
-                out=hi[s][:]
-                .rearrange("p (g n t) -> p g n t", g=G, t=PACK)[:, passes, cols, :]
-                .rearrange("p g (c i) t -> p g c t i", i=4),
-                in_=hp[s][:, passes, :, cols].rearrange("p g t (c i) -> p g c t i", i=4),
-            )
+            for g in passes:
+                start = g * ROWS
+                nc.vector.tensor_copy(
+                    out=hi[s][:, (start + cols.start) * PACK : (start + cols.stop) * PACK].rearrange(
+                        "p (c i t) -> p c t i", i=4, t=PACK
+                    ),
+                    in_=hp[s][:, g, :, cols].rearrange("p t (c i) -> p c t i", i=4),
+                )
 
         def interleave_tensor(s, g, nt=NT, tag="ibank"):
             bank = psum.tile([P, ROWS // 2, PACK], BF16, name=tag, bufs=1 if tag == "ibank" else 2)
@@ -300,7 +302,7 @@ def tile_mlpmodelpredictor_pb_t_w8_kernel(
             )
 
         whole, left, right = slice(0, ROWS), slice(0, ROWS // 2), slice(ROWS // 2, ROWS)
-        both, first, second = slice(0, G), slice(0, 1), slice(1, 2)
+        both, first, second = (0, 1), (0,), (1,)
         rest = slice(NT, ROWS)
         on_v, on_s, on_g = nc.vector.tensor_copy, nc.scalar.copy, nc.gpsimd.tensor_copy
         for i, copy in enumerate((on_v, on_s, on_v, on_s)):

@@ -23,8 +23,8 @@ ROWS = 512
 SUB = ROWS // P
 HALVES = T // ROWS
 STEPS = B * HALVES
-NT = 192
-W3_ON_SCALAR = {3: 2, 5: 3, 7: 4, 9: 5, 11: 6, 12: 7}
+NT = 208
+G_INT = (STEPS - 4, STEPS - 3)
 ZBUFS = 3
 
 
@@ -125,10 +125,12 @@ def tile_mlpmodelpredictor_pb_t_w8_kernel(
         hp, hi, hc, hsc, acc1 = {}, {}, {}, {}, {}
         mixed, acc2, w3i, w3c, w3s = {}, {}, {}, {}, {}
 
-        def permute_w1(g):
+        def permute_w1_codes(g):
             nc.vector.tensor_copy(
                 out=w1_codes[:, g], in_=w1_raw[:, g].rearrange("p (m t) -> p t m", t=PACK)
             )
+
+        def permute_w1_scales(g):
             nc.vector.tensor_copy(
                 out=w1_scales[:, g],
                 in_=w1s_raw[:, g * H // G : (g + 1) * H // G].rearrange("p (m t) -> p t m", t=PACK),
@@ -209,18 +211,32 @@ def tile_mlpmodelpredictor_pb_t_w8_kernel(
                     bias=b2_cols[:, b * G + g, t : t + 1],
                 )
 
+        def inter(s, g, cols):
+            if g == 1 and s + 1 in G_INT:
+                return zbuf_of(s + 2)[:, cols.start * PACK : cols.stop * PACK]
+            return hi[s][:, (g * ROWS + cols.start) * PACK : (g * ROWS + cols.stop) * PACK]
+
         def interleave_vector(s, passes, cols):
             for g in passes:
-                start = g * ROWS
                 nc.vector.tensor_copy(
-                    out=hi[s][:, (start + cols.start) * PACK : (start + cols.stop) * PACK].rearrange(
+                    out=inter(s, g, cols).rearrange(
                         "p (c i t) -> p c t i", i=4, t=PACK
                     ),
                     in_=hp[s][:, g, :, cols].rearrange("p t (c i) -> p c t i", i=4),
                 )
 
+        def interleave_gpsimd(s):
+            nc.gpsimd.tensor_scalar(
+                out=inter(s, 1, whole).rearrange("p (n t) -> p n t", t=PACK),
+                in0=hp[s][:, 1].rearrange("p t n -> p n t"),
+                scalar1=1.0,
+                scalar2=0.0,
+                op0=ALU.mult,
+                op1=ALU.add,
+            )
+
         def interleave_tensor(s, g, nt=NT, tag="ibank"):
-            bank = psum.tile([P, ROWS // 2, PACK], BF16, name=tag, bufs=1 if tag == "ibank" else 2)
+            bank = psum.tile([P, ROWS // 2, PACK], BF16, name=tag, bufs=2 if tag == "zbank" else 1)
             mixed[s, g] = bank
             for n in range(0, nt, nt // 2):
                 nc.tensor.matmul(
@@ -239,23 +255,23 @@ def tile_mlpmodelpredictor_pb_t_w8_kernel(
             )
 
         def quantize_h(s, g, cols):
-            if g == 0 and cols.start == 0:
+            if s not in hc:
                 c = work.tile([P, G, ROWS], U32, name="hcodes", bufs=3, align_bytes=64)
                 e = work.tile([P, G, ROWS], U8, name="hexp", bufs=3, align_bytes=64)
                 hc[s], hsc[s] = c, e
-            start = g * ROWS
             nc.vector.quantize_mx(
                 out=hc[s][:, g, cols].bitcast(FP8X4),
                 scales=hsc[s][:, g, cols],
-                in_=hi[s][:, (start + cols.start) * PACK : (start + cols.stop) * PACK],
+                in_=inter(s, g, cols),
             )
 
-        def interleave_w3(b, copy):
-            t = work.tile([P, G, O, PACK], BF16, name="w3inter", bufs=3, align_bytes=64)
-            w3i[b] = t
+        def interleave_w3(b, copy, passes):
+            if passes.start == 0:
+                t = work.tile([P, G, O, PACK], BF16, name="w3inter", bufs=3, align_bytes=64)
+                w3i[b] = t
             copy(
-                out=t[:].rearrange("p g (c i) t -> p g c t i", i=4),
-                in_=w3_raw[b][:].rearrange("p g t (c i) -> p g c t i", i=4),
+                out=w3i[b][:, passes].rearrange("p g (c i) t -> p g c t i", i=4),
+                in_=w3_raw[b][:, passes].rearrange("p g t (c i) -> p g c t i", i=4),
             )
 
         def quantize_w3(b):
@@ -271,7 +287,7 @@ def tile_mlpmodelpredictor_pb_t_w8_kernel(
         def output(s, tiles, tag="obank"):
             b = s // HALVES
             bank = psum.tile([P, SUB, O], F32, name=tag, bufs=1 if tag == "obank" else 2)
-            acc2[s] = bank
+            acc2[s, tiles.start] = bank
             for i in tiles:
                 rows = slice(i * P, (i + 1) * P)
                 for g in range(G):
@@ -291,7 +307,7 @@ def tile_mlpmodelpredictor_pb_t_w8_kernel(
             t = work.tile([P, SUB, O], F32, name="result", bufs=3)
             nc.vector.tensor_tensor(
                 out=t[:, 0:n, :],
-                in0=acc2[s][:, tiles.start : tiles.stop, :],
+                in0=acc2[s, tiles.start][:, tiles.start : tiles.stop, :],
                 in1=b3_rows[:, b, :].unsqueeze(1).to_broadcast([P, n, O]),
                 op=ALU.add,
             )
@@ -317,8 +333,9 @@ def tile_mlpmodelpredictor_pb_t_w8_kernel(
             out=b2_cols[:].rearrange("p c t -> p (c t)").bitcast(F32).rearrange("p (c u) -> p c u", u=2),
             in_=bank[:, 0:2, 0 : B * G].rearrange("p u c -> p c u"),
         )
+        permute_w1_codes(0)
         scale_z(0, 0)
-        permute_w1(0)
+        permute_w1_scales(0)
         quantize_z(0, left)
         hidden(0, 0, left, range(PACK))
         relu(0, 0, left)
@@ -328,7 +345,8 @@ def tile_mlpmodelpredictor_pb_t_w8_kernel(
         transpose_z(1, [0])
         hidden(0, 0, right, range(PACK))
         relu(0, 0, right)
-        permute_w1(1)
+        permute_w1_codes(1)
+        permute_w1_scales(1)
         widen_z(2, on_g, range(SUB))
         transpose_z(1, [1])
         scale_z(1, 0)
@@ -339,17 +357,20 @@ def tile_mlpmodelpredictor_pb_t_w8_kernel(
         for s in range(STEPS - 1):
             if s >= 1:
                 relu(s, 0, whole)
-                interleave_tensor(s - 1, 1)
-                copy_h(s - 1, 1)
-                interleave_vector(s - 1, both, rest)
+                if s in G_INT:
+                    interleave_vector(s - 1, first, rest)
+                else:
+                    interleave_tensor(s - 1, 1)
+                    copy_h(s - 1, 1)
+                    interleave_vector(s - 1, both, rest)
             if s == 1:
-                interleave_w3(0, on_v)
-                interleave_w3(1, on_v)
+                interleave_w3(0, on_v, slice(0, G))
+                interleave_w3(1, on_v, slice(0, G))
                 quantize_w3(0)
-            if s in W3_ON_SCALAR:
-                interleave_w3(W3_ON_SCALAR[s], on_s)
-            if s - 1 in W3_ON_SCALAR:
-                quantize_w3(W3_ON_SCALAR[s - 1])
+            if 2 <= s < STEPS - 2:
+                interleave_w3(s // 2 + 1, on_s, slice(s % 2, s % 2 + 1))
+            if s >= 4 and s % 2 == 0:
+                quantize_w3(s // 2)
             if s >= 2:
                 quantize_h(s - 2, 0, whole)
             quantize_z(s + 1, whole)
@@ -361,6 +382,8 @@ def tile_mlpmodelpredictor_pb_t_w8_kernel(
                 widen_z(3, on_v, range(SUB))
             if s + 4 < STEPS:
                 widen_z(s + 4, on_g, range(SUB))
+            if s in G_INT:
+                interleave_gpsimd(s - 1)
             if s >= 3:
                 output(s - 3, range(SUB))
             if s >= 1:
@@ -374,39 +397,46 @@ def tile_mlpmodelpredictor_pb_t_w8_kernel(
             copy_h(s, 0)
             if s == 0:
                 transpose_z(2, [0, 1])
-            hidden(s + 1, 0, whole, range(PACK))
+            hidden(s + 1, 0, whole, (0, 1))
+            if s == STEPS - 2:
+                output(s - 2, range(SUB), "zbank")
+            hidden(s + 1, 0, whole, (2, 3))
             if s + 2 < STEPS:
                 scale_z(s + 2, 0)
                 scale_z(s + 2, 1)
             if s >= 3:
                 store(s - 3, range(SUB))
+            if s == STEPS - 2:
+                quantize_h(s - 1, 0, whole)
+                quantize_h(s - 1, 1, whole)
 
-        quantize_h(last - 2, 0, whole)
-        quantize_h(last - 2, 1, whole)
-        output(last - 3, range(SUB))
+        third, fourth = slice(2 * P, 3 * P), slice(3 * P, ROWS)
+        output(last - 2, range(SUB), "zbank")
         relu(last, 0, whole)
         interleave_tensor(last - 1, 1)
         copy_h(last - 1, 1)
-        output(last - 2, range(SUB), "zbank")
         hidden(last, 1, whole, range(PACK))
-        store(last - 3, range(SUB))
         interleave_vector(last - 1, both, rest)
+        store(last - 3, range(SUB))
         store(last - 2, range(SUB))
-        interleave_tensor(last, 0, ROWS // 2, "zbank")
+        interleave_tensor(last, 0, ROWS // 2, "obank")
         relu(last, 1, left)
+        relu(last, 1, third)
         copy_h(last, 0, ROWS // 2)
-        relu(last, 1, right)
+        relu(last, 1, fourth)
         quantize_h(last - 1, 0, whole)
         interleave_vector(last, first, right)
         quantize_h(last - 1, 1, whole)
-        output(last - 1, range(SUB))
+        output(last - 1, range(SUB), "zbank")
         interleave_vector(last, second, left)
-        quantize_h(last, 0, whole)
+        interleave_vector(last, second, third)
         quantize_h(last, 1, left)
-        interleave_vector(last, second, right)
-        output(last, range(0, 2), "zbank")
         store(last - 1, range(SUB))
-        quantize_h(last, 1, right)
-        store(last, range(0, 2))
-        output(last, range(2, 4), "zbank")
-        store(last, range(2, 4))
+        quantize_h(last, 0, whole)
+        interleave_vector(last, second, fourth)
+        quantize_h(last, 1, third)
+        quantize_h(last, 1, fourth)
+        output(last, range(0, 3), "zbank")
+        output(last, range(3, 4))
+        store(last, range(0, 3))
+        store(last, range(3, 4))

@@ -24,8 +24,8 @@ SUB = ROWS // P
 HALVES = T // ROWS
 STEPS = B * HALVES
 NT = 208
-G_INT = (STEPS - 4, STEPS - 3)
-ZBUFS = 3
+G_INT = range(2, STEPS - 2)
+ZBUFS = 4
 
 
 def tile_mlpmodelpredictor_pb_t_w8_kernel(
@@ -51,13 +51,14 @@ def tile_mlpmodelpredictor_pb_t_w8_kernel(
         b2_cols = keep.tile([P, B * G, PACK], BF16, name="b2_cols")
         b3_rows = keep.tile([P, B, O], BF16, name="b3_rows")
 
+        gbuf = keep.tile([P, ROWS * PACK], BF16, name="gbuf", align_bytes=64)
         zbuf = []
         for i in range(ZBUFS):
             t = keep.tile([P, ROWS * PACK], BF16, name="zbuf%d" % i, align_bytes=64)
             zbuf.append(t)
 
         def zbuf_of(s):
-            return zbuf[(s if s > 0 else 2) % ZBUFS]
+            return zbuf[s % 2 if s < 3 else (1 - s) % ZBUFS]
 
         zbytes = []
         w3_raw = []
@@ -212,8 +213,8 @@ def tile_mlpmodelpredictor_pb_t_w8_kernel(
                 )
 
         def inter(s, g, cols):
-            if g == 1 and s + 1 in G_INT:
-                return zbuf_of(s + 2)[:, cols.start * PACK : cols.stop * PACK]
+            if g == 1 and s < STEPS - 3:
+                return gbuf[:, cols.start * PACK : cols.stop * PACK]
             return hi[s][:, (g * ROWS + cols.start) * PACK : (g * ROWS + cols.stop) * PACK]
 
         def interleave_vector(s, passes, cols):
@@ -248,9 +249,8 @@ def tile_mlpmodelpredictor_pb_t_w8_kernel(
                 )
 
         def copy_h(s, g, nt=NT):
-            start = g * ROWS * PACK
             nc.scalar.copy(
-                out=hi[s][:, start : start + nt * PACK].bitcast(F32),
+                out=inter(s, g, slice(0, nt)).bitcast(F32),
                 in_=mixed[s, g][:, 0:nt, :].rearrange("p n t -> p (n t)").bitcast(F32),
             )
 
@@ -357,6 +357,8 @@ def tile_mlpmodelpredictor_pb_t_w8_kernel(
         for s in range(STEPS - 1):
             if s >= 1:
                 relu(s, 0, whole)
+                if 2 <= s < STEPS - 4:
+                    widen_z(s + 4, on_s, range(SUB))
                 if s in G_INT:
                     interleave_vector(s - 1, first, rest)
                 else:
@@ -368,19 +370,18 @@ def tile_mlpmodelpredictor_pb_t_w8_kernel(
                 interleave_w3(1, on_v, slice(0, G))
                 quantize_w3(0)
             if 2 <= s < STEPS - 2:
-                interleave_w3(s // 2 + 1, on_s, slice(s % 2, s % 2 + 1))
+                interleave_w3(s // 2 + 1, on_v if s < STEPS - 4 else on_s, slice(s % 2, s % 2 + 1))
             if s >= 4 and s % 2 == 0:
                 quantize_w3(s // 2)
             if s >= 2:
                 quantize_h(s - 2, 0, whole)
-            quantize_z(s + 1, whole)
-            if s >= 2:
                 quantize_h(s - 2, 1, whole)
-            elif s == 1:
+            quantize_z(s + 1, whole)
+            if s == 1:
                 quantize_w3(1)
-            else:
+            if s == 0:
                 widen_z(3, on_v, range(SUB))
-            if s + 4 < STEPS:
+            if s < 2:
                 widen_z(s + 4, on_g, range(SUB))
             if s in G_INT:
                 interleave_gpsimd(s - 1)

@@ -23,7 +23,8 @@ ROWS = 512
 SUB = ROWS // P
 HALVES = T // ROWS
 STEPS = B * HALVES
-NT = 208
+V_RELU = range(2, STEPS - 4, 2)
+NT = 224
 G_INT = range(2, STEPS - 2)
 ZBUFS = 4
 
@@ -84,8 +85,8 @@ def tile_mlpmodelpredictor_pb_t_w8_kernel(
             )
 
         nc.vector.memset(warm[:], 0.0)
-        nc.vector.memset(b2_rows[:], 0.0)
         nc.vector.memset(w1s_raw[:].bitcast(I32), 0)
+        nc.vector.memset(b2_rows[:], 0.0)
         make_identity(nc, ident_f[:])
         make_identity(nc, ident_b[:])
         load_z(0, 2)
@@ -94,6 +95,7 @@ def tile_mlpmodelpredictor_pb_t_w8_kernel(
         )
         w1_words = sw1_words[0].rearrange("p n t -> p (n t)").bitcast(I32)
         nc.sync.dma_start(out=w1_raw[:, 0, :], in_=w1_words[:, 0 : H // G])
+        load_z(1)
         for q in range(4):
             nc.sync.dma_start(
                 out=w1s_raw[32 * q : 32 * q + 4, :].bitcast(I32),
@@ -103,13 +105,12 @@ def tile_mlpmodelpredictor_pb_t_w8_kernel(
         nc.sync.dma_start(
             out=b2_rows[0 : B * G, :], in_=b2.rearrange("b (g n) -> (b g) n", g=G)
         )
-        load_z(1)
         nc.sync.dma_start(out=w1_raw[:, 1, :], in_=w1_words[:, H // G : H])
         load_z(2)
-        load_z(3)
-        load_z(4)
         load_w3(0)
         load_w3(1)
+        load_z(3)
+        load_z(4)
         load_z(5)
         load_w3(2)
         load_w3(3)
@@ -197,14 +198,24 @@ def tile_mlpmodelpredictor_pb_t_w8_kernel(
                     stop=True,
                 )
 
-        def relu(s, g, cols):
+        def relu_vector(s, g, t):
+            nc.vector.tensor_scalar(
+                out=hp[s][:, g, t, :],
+                in0=acc1[s, g, t][:],
+                scalar1=b2_cols[:, s // HALVES * G + g, t : t + 1],
+                scalar2=0.0,
+                op0=ALU.add,
+                op1=ALU.max,
+            )
+
+        def relu(s, g, cols, slots=range(PACK)):
             if g == 0 and cols.start == 0:
                 planar = work.tile([P, G, PACK, ROWS], BF16, name="hplanar", bufs=3)
                 hp[s] = planar
                 inter = work.tile([P, G * ROWS * PACK], BF16, name="hinter", bufs=4, align_bytes=64)
                 hi[s] = inter
             b = s // HALVES
-            for t in range(PACK):
+            for t in slots:
                 nc.scalar.activation(
                     out=hp[s][:, g, t, cols],
                     in_=acc1[s, g, t][:, cols],
@@ -236,22 +247,22 @@ def tile_mlpmodelpredictor_pb_t_w8_kernel(
                 op1=ALU.add,
             )
 
-        def interleave_tensor(s, g, nt=NT, tag="ibank"):
+        def interleave_tensor(s, g, tag="ibank"):
             bank = psum.tile([P, ROWS // 2, PACK], BF16, name=tag, bufs=2 if tag == "zbank" else 1)
             mixed[s, g] = bank
-            for n in range(0, nt, nt // 2):
+            for n in range(0, NT, NT // 2):
                 nc.tensor.matmul(
-                    bank[:, n : n + nt // 2, :],
+                    bank[:, n : n + NT // 2, :],
                     lhsT=ident_b[:],
-                    rhs=hp[s][:, g, :, n : n + nt // 2].rearrange("p t n -> p n t"),
+                    rhs=hp[s][:, g, :, n : n + NT // 2].rearrange("p t n -> p n t"),
                     start=True,
                     stop=True,
                 )
 
-        def copy_h(s, g, nt=NT):
+        def copy_h(s, g):
             nc.scalar.copy(
-                out=inter(s, g, slice(0, nt)).bitcast(F32),
-                in_=mixed[s, g][:, 0:nt, :].rearrange("p n t -> p (n t)").bitcast(F32),
+                out=inter(s, g, slice(0, NT)).bitcast(F32),
+                in_=mixed[s, g][:, 0:NT, :].rearrange("p n t -> p (n t)").bitcast(F32),
             )
 
         def quantize_h(s, g, cols):
@@ -323,12 +334,12 @@ def tile_mlpmodelpredictor_pb_t_w8_kernel(
         on_v, on_s, on_g = nc.vector.tensor_copy, nc.scalar.copy, nc.gpsimd.tensor_copy
         for i, copy in enumerate((on_v, on_s, on_v, on_s)):
             widen_z(0, copy, range(i, i + 1))
+        widen_z(1, on_s, range(SUB))
         transpose_z(0, [0, 1])
         bank = psum.tile([P, SUB, O], F32, name="obank", bufs=1)
         b2_words = b2_rows[:].bitcast(F32)
         for u in range(2):
             nc.tensor.transpose(bank[:, u, :], b2_words[:, u::2], ident_f[:])
-        widen_z(1, on_s, range(0, 2))
         nc.scalar.copy(
             out=b2_cols[:].rearrange("p c t -> p (c t)").bitcast(F32).rearrange("p (c u) -> p c u", u=2),
             in_=bank[:, 0:2, 0 : B * G].rearrange("p u c -> p c u"),
@@ -337,20 +348,20 @@ def tile_mlpmodelpredictor_pb_t_w8_kernel(
         scale_z(0, 0)
         permute_w1_scales(0)
         quantize_z(0, left)
+        transpose_z(1, [0])
         hidden(0, 0, left, range(PACK))
         relu(0, 0, left)
         scale_z(0, 1)
-        widen_z(1, on_v, range(2, 4))
+        permute_w1_codes(1)
         quantize_z(0, right)
-        transpose_z(1, [0])
+        transpose_z(1, [1])
         hidden(0, 0, right, range(PACK))
         relu(0, 0, right)
-        permute_w1_codes(1)
         permute_w1_scales(1)
         widen_z(2, on_g, range(SUB))
-        transpose_z(1, [1])
         scale_z(1, 0)
         scale_z(1, 1)
+        interleave_w3(0, on_v, slice(0, G))
         hidden(0, 1, whole, range(PACK))
 
         last = STEPS - 1
@@ -366,8 +377,6 @@ def tile_mlpmodelpredictor_pb_t_w8_kernel(
                     copy_h(s - 1, 1)
                     interleave_vector(s - 1, both, rest)
             if s == 1:
-                interleave_w3(0, on_v, slice(0, G))
-                interleave_w3(1, on_v, slice(0, G))
                 quantize_w3(0)
             if 2 <= s < STEPS - 2:
                 interleave_w3(s // 2 + 1, on_v if s < STEPS - 4 else on_s, slice(s % 2, s % 2 + 1))
@@ -380,7 +389,7 @@ def tile_mlpmodelpredictor_pb_t_w8_kernel(
             if s == 1:
                 quantize_w3(1)
             if s == 0:
-                widen_z(3, on_v, range(SUB))
+                interleave_w3(1, on_v, slice(0, G))
             if s < 2:
                 widen_z(s + 4, on_g, range(SUB))
             if s in G_INT:
@@ -393,18 +402,21 @@ def tile_mlpmodelpredictor_pb_t_w8_kernel(
                 transpose_z(s + 2, [0, 1])
             if s >= 1:
                 hidden(s, 1, whole, (2, 3))
-            relu(s, 1, whole)
+            relu(s, 1, whole, range(PACK - 1) if s in V_RELU else range(PACK))
             interleave_tensor(s, 0)
             copy_h(s, 0)
             if s == 0:
+                widen_z(3, on_s, range(SUB))
                 transpose_z(2, [0, 1])
             hidden(s + 1, 0, whole, (0, 1))
             if s == STEPS - 2:
                 output(s - 2, range(SUB), "zbank")
-            hidden(s + 1, 0, whole, (2, 3))
             if s + 2 < STEPS:
                 scale_z(s + 2, 0)
                 scale_z(s + 2, 1)
+            if s in V_RELU:
+                relu_vector(s, 1, PACK - 1)
+            hidden(s + 1, 0, whole, (2, 3))
             if s >= 3:
                 store(s - 3, range(SUB))
             if s == STEPS - 2:
@@ -420,24 +432,24 @@ def tile_mlpmodelpredictor_pb_t_w8_kernel(
         interleave_vector(last - 1, both, rest)
         store(last - 3, range(SUB))
         store(last - 2, range(SUB))
-        interleave_tensor(last, 0, ROWS // 2, "obank")
+        interleave_tensor(last, 0, "obank")
         relu(last, 1, left)
+        copy_h(last, 0)
         relu(last, 1, third)
-        copy_h(last, 0, ROWS // 2)
         relu(last, 1, fourth)
         quantize_h(last - 1, 0, whole)
-        interleave_vector(last, first, right)
+        interleave_vector(last, first, rest)
         quantize_h(last - 1, 1, whole)
         output(last - 1, range(SUB), "zbank")
         interleave_vector(last, second, left)
-        interleave_vector(last, second, third)
-        quantize_h(last, 1, left)
-        store(last - 1, range(SUB))
         quantize_h(last, 0, whole)
+        quantize_h(last, 1, left)
+        interleave_vector(last, second, third)
+        output(last, range(0, 2), "zbank")
+        store(last - 1, range(SUB))
         interleave_vector(last, second, fourth)
         quantize_h(last, 1, third)
         quantize_h(last, 1, fourth)
-        output(last, range(0, 3), "zbank")
-        output(last, range(3, 4))
-        store(last, range(0, 3))
-        store(last, range(3, 4))
+        output(last, range(2, 4))
+        store(last, range(0, 2))
+        store(last, range(2, 4))

@@ -18,15 +18,16 @@ ACT = mybir.ActivationFunctionType
 
 P = 128
 PACK = 4
-G = H // 512
+G = H // (P * PACK)
 ROWS = 512
 SUB = ROWS // P
 HALVES = T // ROWS
 STEPS = B * HALVES
-V_RELU = range(2, STEPS - 4, 2)
-NT = 224
-G_INT = range(2, STEPS - 2)
+LAST = STEPS - 1
+LEAD = 4
 ZBUFS = 4
+NT = 208
+G_TURNS = range(2, STEPS - 2)
 
 
 def tile_mlpmodelpredictor_pb_t_w8_kernel(
@@ -40,7 +41,6 @@ def tile_mlpmodelpredictor_pb_t_w8_kernel(
         psum = ctx.enter_context(tc.psum_pool(name="psum", bufs=1))
         ctx.enter_context(tc.manual_schedule())
 
-        warm = keep.tile([P, 1], F32, name="warm")
         ident_f = keep.tile([P, P], F32, name="ident_f")
         ident_b = keep.tile([P, P], BF16, name="ident_b")
         kscale = keep.tile([P, PACK], F32, name="kscale")
@@ -55,8 +55,8 @@ def tile_mlpmodelpredictor_pb_t_w8_kernel(
         gbuf = keep.tile([P, ROWS * PACK], BF16, name="gbuf", align_bytes=64)
         zbuf = []
         for i in range(ZBUFS):
-            t = keep.tile([P, ROWS * PACK], BF16, name="zbuf%d" % i, align_bytes=64)
-            zbuf.append(t)
+            zbuf_tile = keep.tile([P, ROWS * PACK], BF16, name="zbuf%d" % i, align_bytes=64)
+            zbuf.append(zbuf_tile)
 
         def zbuf_of(s):
             return zbuf[s % 2 if s < 3 else (1 - s) % ZBUFS]
@@ -70,26 +70,29 @@ def tile_mlpmodelpredictor_pb_t_w8_kernel(
                 zb = loads.tile([P, SUB * R], U8, name="zb", bufs=STEPS, align_bytes=64)
                 zbytes.append(zb)
 
-        def load_z(s, n=SUB):
+        def load_z(s, tiles_a_load=SUB):
             b, hf = divmod(s, HALVES)
-            for i in range(0, SUB, n):
+            for i in range(0, SUB, tiles_a_load):
                 row = hf * ROWS + i * P
                 nc.sync.dma_start(
-                    out=zbytes[s][:, i * R : (i + n) * R].rearrange("p (i k) -> p i k", k=R),
-                    in_=z2_bytes[row : row + n * P, b, :].rearrange("(i p) k -> p i k", p=P),
+                    out=zbytes[s][:, i * R : (i + tiles_a_load) * R].rearrange(
+                        "p (i k) -> p i k", k=R
+                    ),
+                    in_=z2_bytes[row : row + tiles_a_load * P, b, :].rearrange(
+                        "(i p) k -> p i k", p=P
+                    ),
                 )
 
         def load_w3(b):
             nc.sync.dma_start(
-                out=w3_raw[b][:], in_=w3[b].rearrange("(g p j) o -> p g j o", p=P, j=PACK)
+                out=w3_raw[b][:], in_=w3[b].rearrange("(g p t) o -> p g t o", p=P, t=PACK)
             )
 
-        nc.vector.memset(warm[:], 0.0)
         nc.vector.memset(w1s_raw[:].bitcast(I32), 0)
         nc.vector.memset(b2_rows[:], 0.0)
         make_identity(nc, ident_f[:])
         make_identity(nc, ident_b[:])
-        load_z(0, 2)
+        load_z(0, SUB // 2)
         nc.scalar.dma_start(
             out=kscale[:], in_=z2_scale.rearrange("a c (p t) -> p (a c t)", t=PACK)
         )
@@ -101,7 +104,6 @@ def tile_mlpmodelpredictor_pb_t_w8_kernel(
                 out=w1s_raw[32 * q : 32 * q + 4, :].bitcast(I32),
                 in_=sw1_scales[0, 4 * q : 4 * q + 4, :].bitcast(I32),
             )
-        nc.scalar.activation(out=warm[:], in_=warm[:], func=ACT.Relu)
         nc.sync.dma_start(
             out=b2_rows[0 : B * G, :], in_=b2.rearrange("b (g n) -> (b g) n", g=G)
         )
@@ -123,9 +125,9 @@ def tile_mlpmodelpredictor_pb_t_w8_kernel(
         for s in range(6, STEPS):
             load_z(s)
 
-        zt, zc, zsc = {}, {}, {}
-        hp, hi, hc, hsc, acc1 = {}, {}, {}, {}, {}
-        mixed, acc2, w3i, w3c, w3s = {}, {}, {}, {}, {}
+        z_banks, z_codes, z_exps = {}, {}, {}
+        h_banks, h_planes, h_inter, h_codes, h_exps = {}, {}, {}, {}, {}
+        mixed, out_banks, w3_inter, w3_codes, w3_exps = {}, {}, {}, {}, {}
 
         def permute_w1_codes(g):
             nc.vector.tensor_copy(
@@ -133,26 +135,25 @@ def tile_mlpmodelpredictor_pb_t_w8_kernel(
             )
 
         def permute_w1_scales(g):
+            cols = slice(g * H // G, (g + 1) * H // G)
             nc.vector.tensor_copy(
-                out=w1_scales[:, g],
-                in_=w1s_raw[:, g * H // G : (g + 1) * H // G].rearrange("p (m t) -> p t m", t=PACK),
+                out=w1_scales[:, g], in_=w1s_raw[:, cols].rearrange("p (m t) -> p t m", t=PACK)
             )
 
         def widen_z(s, copy, tiles):
             cols = slice(tiles.start * R, tiles.stop * R)
             copy(out=zbuf_of(s)[:, cols], in_=zbytes[s][:, cols].bitcast(FP8))
 
-        def transpose_z(s, halves):
+        def transpose_z(s, halves=(0, 1)):
             words = zbuf_of(s)[:].bitcast(F32)
-            zt.setdefault(s, [])
             for half in halves:
                 bank = psum.tile([P, 2, 2, P], F32, name="zbank", bufs=2)
-                zt[s].append(bank)
+                z_banks[s, half] = bank
                 for i in range(2):
-                    base = 256 * (2 * half + i)
+                    base = R // 2 * (2 * half + i)
                     for u in range(2):
                         nc.tensor.transpose(
-                            bank[:, u, i, :], words[:, base + u : base + 256 : 2], ident_f[:]
+                            bank[:, u, i, :], words[:, base + u : base + R // 2 : 2], ident_f[:]
                         )
 
         def scale_z(s, half):
@@ -161,7 +162,7 @@ def tile_mlpmodelpredictor_pb_t_w8_kernel(
                 out=zbuf_of(s)[:, half * n * PACK : (half + 1) * n * PACK].rearrange(
                     "p (n u e) -> p n u e", u=2, e=2
                 ),
-                in0=zt[s][half][:]
+                in0=z_banks[s, half][:]
                 .rearrange("p u i r -> p (u i r)")
                 .bitcast(BF16)
                 .rearrange("p (u n e) -> p n u e", u=2, e=2),
@@ -174,73 +175,62 @@ def tile_mlpmodelpredictor_pb_t_w8_kernel(
 
         def quantize_z(s, cols):
             if cols.start == 0:
-                c = work.tile([P, ROWS], U32, name="zcodes", bufs=3, align_bytes=64)
-                e = work.tile([P, ROWS], U8, name="zexp", bufs=3, align_bytes=64)
-                zc[s], zsc[s] = c, e
+                codes = work.tile([P, ROWS], U32, name="zcodes", bufs=3, align_bytes=64)
+                exps = work.tile([P, ROWS], U8, name="zexp", bufs=3, align_bytes=64)
+                z_codes[s], z_exps[s] = codes, exps
             nc.vector.quantize_mx(
-                out=zc[s][:, cols].bitcast(FP8X4),
-                scales=zsc[s][:, cols],
+                out=z_codes[s][:, cols].bitcast(FP8X4),
+                scales=z_exps[s][:, cols],
                 in_=zbuf_of(s)[:, cols.start * PACK : cols.stop * PACK],
             )
 
-        def hidden(s, g, cols, slots):
+        def hidden(s, g, slots, cols=slice(0, ROWS)):
             for t in slots:
                 if cols.start == 0:
-                    bank = psum.tile([P, ROWS], F32, name="hbank", bufs=4)
-                    acc1[s, g, t] = bank
+                    bank = psum.tile([P, ROWS], F32, name="hbank", bufs=PACK)
+                    h_banks[s, g, t] = bank
                 nc.tensor.matmul_mx(
-                    out=acc1[s, g, t][:, cols],
+                    out=h_banks[s, g, t][:, cols],
                     lhsT=w1_codes[:, g, t, :].bitcast(FP8X4),
                     lhsT_scale=w1_scales[:, g, t, :],
-                    rhs=zc[s][:, cols].bitcast(FP8X4),
-                    rhs_scale=zsc[s][:, cols],
+                    rhs=z_codes[s][:, cols].bitcast(FP8X4),
+                    rhs_scale=z_exps[s][:, cols],
                     start=True,
                     stop=True,
                 )
 
-        def relu_vector(s, g, t):
-            nc.vector.tensor_scalar(
-                out=hp[s][:, g, t, :],
-                in0=acc1[s, g, t][:],
-                scalar1=b2_cols[:, s // HALVES * G + g, t : t + 1],
-                scalar2=0.0,
-                op0=ALU.add,
-                op1=ALU.max,
-            )
-
-        def relu(s, g, cols, slots=range(PACK)):
+        def relu(s, g, cols):
             if g == 0 and cols.start == 0:
-                planar = work.tile([P, G, PACK, ROWS], BF16, name="hplanar", bufs=3)
-                hp[s] = planar
-                inter = work.tile([P, G * ROWS * PACK], BF16, name="hinter", bufs=4, align_bytes=64)
-                hi[s] = inter
-            b = s // HALVES
-            for t in slots:
+                planes = work.tile([P, G, PACK, ROWS], BF16, name="hplanar", bufs=3)
+                h_planes[s] = planes
+                inter = work.tile(
+                    [P, G * ROWS * PACK], BF16, name="hinter", bufs=4, align_bytes=64
+                )
+                h_inter[s] = inter
+            for t in range(PACK):
                 nc.scalar.activation(
-                    out=hp[s][:, g, t, cols],
-                    in_=acc1[s, g, t][:, cols],
+                    out=h_planes[s][:, g, t, cols],
+                    in_=h_banks[s, g, t][:, cols],
                     func=ACT.Relu,
-                    bias=b2_cols[:, b * G + g, t : t + 1],
+                    bias=b2_cols[:, s // HALVES * G + g, t : t + 1],
                 )
 
-        def inter(s, g, cols):
-            if g == 1 and s < STEPS - 3:
+        def interleaved(s, g, cols):
+            if g == 1 and s < G_TURNS.stop - 1:
                 return gbuf[:, cols.start * PACK : cols.stop * PACK]
-            return hi[s][:, (g * ROWS + cols.start) * PACK : (g * ROWS + cols.stop) * PACK]
+            return h_inter[s][:, (g * ROWS + cols.start) * PACK : (g * ROWS + cols.stop) * PACK]
 
         def interleave_vector(s, passes, cols):
             for g in passes:
                 nc.vector.tensor_copy(
-                    out=inter(s, g, cols).rearrange(
-                        "p (c i t) -> p c t i", i=4, t=PACK
-                    ),
-                    in_=hp[s][:, g, :, cols].rearrange("p t (c i) -> p c t i", i=4),
+                    out=interleaved(s, g, cols).rearrange("p (c i t) -> p c t i", i=4, t=PACK),
+                    in_=h_planes[s][:, g, :, cols].rearrange("p t (c i) -> p c t i", i=4),
                 )
 
         def interleave_gpsimd(s):
             nc.gpsimd.tensor_scalar(
-                out=inter(s, 1, whole).rearrange("p (n t) -> p n t", t=PACK),
-                in0=hp[s][:, 1].rearrange("p t n -> p n t"),
+                out=interleaved(s, 1, whole).rearrange("p (n t) -> p n t", t=PACK),
+                in0=h_planes[s][:, 1].rearrange("p t n -> p n t"),
                 scalar1=1.0,
                 scalar2=0.0,
                 op0=ALU.mult,
@@ -248,66 +238,66 @@ def tile_mlpmodelpredictor_pb_t_w8_kernel(
             )
 
         def interleave_tensor(s, g, tag="ibank"):
-            bank = psum.tile([P, ROWS // 2, PACK], BF16, name=tag, bufs=2 if tag == "zbank" else 1)
+            bank = psum.tile([P, ROWS // 2, PACK], BF16, name=tag, bufs=1)
             mixed[s, g] = bank
             for n in range(0, NT, NT // 2):
                 nc.tensor.matmul(
                     bank[:, n : n + NT // 2, :],
                     lhsT=ident_b[:],
-                    rhs=hp[s][:, g, :, n : n + NT // 2].rearrange("p t n -> p n t"),
+                    rhs=h_planes[s][:, g, :, n : n + NT // 2].rearrange("p t n -> p n t"),
                     start=True,
                     stop=True,
                 )
 
-        def copy_h(s, g):
+        def copy_mixed(s, g):
             nc.scalar.copy(
-                out=inter(s, g, slice(0, NT)).bitcast(F32),
+                out=interleaved(s, g, slice(0, NT)).bitcast(F32),
                 in_=mixed[s, g][:, 0:NT, :].rearrange("p n t -> p (n t)").bitcast(F32),
             )
 
         def quantize_h(s, g, cols):
-            if s not in hc:
-                c = work.tile([P, G, ROWS], U32, name="hcodes", bufs=3, align_bytes=64)
-                e = work.tile([P, G, ROWS], U8, name="hexp", bufs=3, align_bytes=64)
-                hc[s], hsc[s] = c, e
+            if s not in h_codes:
+                codes = work.tile([P, G, ROWS], U32, name="hcodes", bufs=3, align_bytes=64)
+                exps = work.tile([P, G, ROWS], U8, name="hexp", bufs=3, align_bytes=64)
+                h_codes[s], h_exps[s] = codes, exps
             nc.vector.quantize_mx(
-                out=hc[s][:, g, cols].bitcast(FP8X4),
-                scales=hsc[s][:, g, cols],
-                in_=inter(s, g, cols),
+                out=h_codes[s][:, g, cols].bitcast(FP8X4),
+                scales=h_exps[s][:, g, cols],
+                in_=interleaved(s, g, cols),
             )
 
         def interleave_w3(b, copy, passes):
             if passes.start == 0:
-                t = work.tile([P, G, O, PACK], BF16, name="w3inter", bufs=3, align_bytes=64)
-                w3i[b] = t
+                tile = work.tile([P, G, O, PACK], BF16, name="w3inter", bufs=3, align_bytes=64)
+                w3_inter[b] = tile
             copy(
-                out=w3i[b][:, passes].rearrange("p g (c i) t -> p g c t i", i=4),
+                out=w3_inter[b][:, passes].rearrange("p g (c i) t -> p g c t i", i=4),
                 in_=w3_raw[b][:, passes].rearrange("p g t (c i) -> p g c t i", i=4),
             )
 
         def quantize_w3(b):
-            c = work.tile([P, G, O], U32, name="w3codes", bufs=B, align_bytes=64)
-            e = work.tile([P, G, O], U8, name="w3exp", bufs=B, align_bytes=64)
-            w3c[b], w3s[b] = c, e
+            codes = work.tile([P, G, O], U32, name="w3codes", bufs=B, align_bytes=64)
+            exps = work.tile([P, G, O], U8, name="w3exp", bufs=B, align_bytes=64)
+            w3_codes[b], w3_exps[b] = codes, exps
             nc.vector.quantize_mx(
-                out=c[:].rearrange("p g o -> p (g o)").bitcast(FP8X4),
-                scales=e[:].rearrange("p g o -> p (g o)"),
-                in_=w3i[b][:].rearrange("p g o j -> p (g o j)"),
+                out=codes[:].rearrange("p g o -> p (g o)").bitcast(FP8X4),
+                scales=exps[:].rearrange("p g o -> p (g o)"),
+                in_=w3_inter[b][:].rearrange("p g o t -> p (g o t)"),
             )
 
         def output(s, tiles, tag="obank"):
             b = s // HALVES
             bank = psum.tile([P, SUB, O], F32, name=tag, bufs=1 if tag == "obank" else 2)
-            acc2[s, tiles.start] = bank
+            out_banks[s, tiles.start] = bank
             for i in tiles:
                 rows = slice(i * P, (i + 1) * P)
                 for g in range(G):
                     nc.tensor.matmul_mx(
                         out=bank[:, i, :],
-                        lhsT=hc[s][:, g, rows].bitcast(FP8X4),
-                        lhsT_scale=hsc[s][:, g, rows],
-                        rhs=w3c[b][:, g, :].bitcast(FP8X4),
-                        rhs_scale=w3s[b][:, g, :],
+                        lhsT=h_codes[s][:, g, rows].bitcast(FP8X4),
+                        lhsT_scale=h_exps[s][:, g, rows],
+                        rhs=w3_codes[b][:, g, :].bitcast(FP8X4),
+                        rhs_scale=w3_exps[b][:, g, :],
                         start=(g == 0),
                         stop=(g == G - 1),
                     )
@@ -315,73 +305,82 @@ def tile_mlpmodelpredictor_pb_t_w8_kernel(
         def store(s, tiles):
             b, hf = divmod(s, HALVES)
             n = len(tiles)
-            t = work.tile([P, SUB, O], F32, name="result", bufs=3)
+            result = work.tile([P, SUB, O], F32, name="result", bufs=3)
             nc.vector.tensor_tensor(
-                out=t[:, 0:n, :],
-                in0=acc2[s, tiles.start][:, tiles.start : tiles.stop, :],
+                out=result[:, 0:n, :],
+                in0=out_banks[s, tiles.start][:, tiles.start : tiles.stop, :],
                 in1=b3_rows[:, b, :].unsqueeze(1).to_broadcast([P, n, O]),
                 op=ALU.add,
             )
             row = hf * ROWS + tiles.start * P
             nc.sync.dma_start(
                 out=out[row : row + n * P, b, :].rearrange("(i p) o -> p i o", p=P),
-                in_=t[:, 0:n, :],
+                in_=result[:, 0:n, :],
             )
 
-        whole, left, right = slice(0, ROWS), slice(0, ROWS // 2), slice(ROWS // 2, ROWS)
-        both, first, second = (0, 1), (0,), (1,)
-        rest = slice(NT, ROWS)
+        def on_s_activation(out, in_):
+            nc.scalar.activation(out=out, in_=in_, func=ACT.Copy)
+
+        whole, rest = slice(0, ROWS), slice(NT, ROWS)
+        left, right = slice(0, ROWS // 2), slice(ROWS // 2, ROWS)
+        third, fourth = slice(2 * P, 3 * P), slice(3 * P, ROWS)
+        all_tiles, both_passes = range(SUB), slice(0, G)
         on_v, on_s, on_g = nc.vector.tensor_copy, nc.scalar.copy, nc.gpsimd.tensor_copy
-        for i, copy in enumerate((on_v, on_s, on_v, on_s)):
+
+        for i, copy in enumerate((on_v, on_s_activation, on_v, on_s)):
             widen_z(0, copy, range(i, i + 1))
-        widen_z(1, on_s, range(SUB))
-        transpose_z(0, [0, 1])
-        bank = psum.tile([P, SUB, O], F32, name="obank", bufs=1)
+        widen_z(1, on_s, all_tiles)
+        transpose_z(0)
+        b2_bank = psum.tile([P, SUB, O], F32, name="obank", bufs=1)
         b2_words = b2_rows[:].bitcast(F32)
         for u in range(2):
-            nc.tensor.transpose(bank[:, u, :], b2_words[:, u::2], ident_f[:])
+            nc.tensor.transpose(b2_bank[:, u, :], b2_words[:, u::2], ident_f[:])
         nc.scalar.copy(
-            out=b2_cols[:].rearrange("p c t -> p (c t)").bitcast(F32).rearrange("p (c u) -> p c u", u=2),
-            in_=bank[:, 0:2, 0 : B * G].rearrange("p u c -> p c u"),
+            out=b2_cols[:]
+            .rearrange("p c t -> p (c t)")
+            .bitcast(F32)
+            .rearrange("p (c u) -> p c u", u=2),
+            in_=b2_bank[:, 0:2, 0 : B * G].rearrange("p u c -> p c u"),
         )
         permute_w1_codes(0)
         scale_z(0, 0)
         permute_w1_scales(0)
         quantize_z(0, left)
-        transpose_z(1, [0])
-        hidden(0, 0, left, range(PACK))
+        transpose_z(1, (0,))
+        hidden(0, 0, range(PACK), left)
         relu(0, 0, left)
         scale_z(0, 1)
         permute_w1_codes(1)
         quantize_z(0, right)
-        transpose_z(1, [1])
-        hidden(0, 0, right, range(PACK))
+        transpose_z(1, (1,))
+        hidden(0, 0, range(PACK), right)
         relu(0, 0, right)
         permute_w1_scales(1)
-        widen_z(2, on_g, range(SUB))
+        widen_z(2, on_g, all_tiles)
         scale_z(1, 0)
         scale_z(1, 1)
-        interleave_w3(0, on_v, slice(0, G))
-        hidden(0, 1, whole, range(PACK))
+        interleave_w3(0, on_v, both_passes)
+        hidden(0, 1, range(PACK))
 
-        last = STEPS - 1
-        for s in range(STEPS - 1):
+        for s in range(LAST):
+            scalar_widens = 2 <= s < STEPS - LEAD
             if s >= 1:
                 relu(s, 0, whole)
-                if 2 <= s < STEPS - 4:
-                    widen_z(s + 4, on_s, range(SUB))
-                if s in G_INT:
-                    interleave_vector(s - 1, first, rest)
+                if scalar_widens:
+                    widen_z(s + LEAD, on_s, all_tiles)
+                if s in G_TURNS:
+                    interleave_vector(s - 1, (0,), rest)
                 else:
                     interleave_tensor(s - 1, 1)
-                    copy_h(s - 1, 1)
-                    interleave_vector(s - 1, both, rest)
+                    copy_mixed(s - 1, 1)
+                    interleave_vector(s - 1, (0, 1), rest)
             if s == 1:
                 quantize_w3(0)
             if 2 <= s < STEPS - 2:
-                interleave_w3(s // 2 + 1, on_v if s < STEPS - 4 else on_s, slice(s % 2, s % 2 + 1))
-            if s >= 4 and s % 2 == 0:
-                quantize_w3(s // 2)
+                g = s % G
+                interleave_w3(s // G + 1, on_v if scalar_widens else on_s, slice(g, g + 1))
+            if s >= 2 * G and s % G == 0:
+                quantize_w3(s // G)
             if s >= 2:
                 quantize_h(s - 2, 0, whole)
                 quantize_h(s - 2, 1, whole)
@@ -389,67 +388,62 @@ def tile_mlpmodelpredictor_pb_t_w8_kernel(
             if s == 1:
                 quantize_w3(1)
             if s == 0:
-                interleave_w3(1, on_v, slice(0, G))
+                interleave_w3(1, on_v, both_passes)
             if s < 2:
-                widen_z(s + 4, on_g, range(SUB))
-            if s in G_INT:
+                widen_z(s + LEAD, on_g, all_tiles)
+            if s in G_TURNS:
                 interleave_gpsimd(s - 1)
             if s >= 3:
-                output(s - 3, range(SUB))
+                output(s - 3, all_tiles)
             if s >= 1:
-                hidden(s, 1, whole, (0, 1))
-            if 1 <= s < STEPS - 2:
-                transpose_z(s + 2, [0, 1])
-            if s >= 1:
-                hidden(s, 1, whole, (2, 3))
-            relu(s, 1, whole, range(PACK - 1) if s in V_RELU else range(PACK))
+                hidden(s, 1, (0, 1))
+                if s + 2 < STEPS:
+                    transpose_z(s + 2)
+                hidden(s, 1, (2, 3))
+            relu(s, 1, whole)
             interleave_tensor(s, 0)
-            copy_h(s, 0)
+            copy_mixed(s, 0)
             if s == 0:
-                widen_z(3, on_s, range(SUB))
-                transpose_z(2, [0, 1])
-            hidden(s + 1, 0, whole, (0, 1))
-            if s == STEPS - 2:
-                output(s - 2, range(SUB), "zbank")
+                widen_z(3, on_s, all_tiles)
+                transpose_z(2)
+            hidden(s + 1, 0, (0, 1))
             if s + 2 < STEPS:
                 scale_z(s + 2, 0)
                 scale_z(s + 2, 1)
-            if s in V_RELU:
-                relu_vector(s, 1, PACK - 1)
-            hidden(s + 1, 0, whole, (2, 3))
+            else:
+                output(s - 2, all_tiles, "zbank")
+            hidden(s + 1, 0, (2, 3))
             if s >= 3:
-                store(s - 3, range(SUB))
-            if s == STEPS - 2:
-                quantize_h(s - 1, 0, whole)
-                quantize_h(s - 1, 1, whole)
+                store(s - 3, all_tiles)
 
-        third, fourth = slice(2 * P, 3 * P), slice(3 * P, ROWS)
-        output(last - 2, range(SUB), "zbank")
-        relu(last, 0, whole)
-        interleave_tensor(last - 1, 1)
-        copy_h(last - 1, 1)
-        hidden(last, 1, whole, range(PACK))
-        interleave_vector(last - 1, both, rest)
-        store(last - 3, range(SUB))
-        store(last - 2, range(SUB))
-        interleave_tensor(last, 0, "obank")
-        relu(last, 1, left)
-        copy_h(last, 0)
-        relu(last, 1, third)
-        relu(last, 1, fourth)
-        quantize_h(last - 1, 0, whole)
-        interleave_vector(last, first, rest)
-        quantize_h(last - 1, 1, whole)
-        output(last - 1, range(SUB), "zbank")
-        interleave_vector(last, second, left)
-        quantize_h(last, 0, whole)
-        quantize_h(last, 1, left)
-        interleave_vector(last, second, third)
-        output(last, range(0, 2), "zbank")
-        store(last - 1, range(SUB))
-        interleave_vector(last, second, fourth)
-        quantize_h(last, 1, third)
-        quantize_h(last, 1, fourth)
-        output(last, range(2, 4))
-        store(last, range(0, 2))
-        store(last, range(2, 4))
+        quantize_h(LAST - 2, 0, whole)
+        quantize_h(LAST - 2, 1, whole)
+        output(LAST - 2, all_tiles, "zbank")
+        relu(LAST, 0, whole)
+        interleave_tensor(LAST - 1, 1)
+        copy_mixed(LAST - 1, 1)
+        hidden(LAST, 1, range(PACK))
+        interleave_vector(LAST - 1, (0, 1), rest)
+        store(LAST - 3, all_tiles)
+        store(LAST - 2, all_tiles)
+        interleave_tensor(LAST, 0, "obank")
+        relu(LAST, 1, left)
+        copy_mixed(LAST, 0)
+        relu(LAST, 1, third)
+        relu(LAST, 1, fourth)
+        quantize_h(LAST - 1, 0, whole)
+        interleave_vector(LAST, (0,), rest)
+        quantize_h(LAST - 1, 1, whole)
+        output(LAST - 1, all_tiles, "zbank")
+        interleave_vector(LAST, (1,), left)
+        quantize_h(LAST, 0, whole)
+        quantize_h(LAST, 1, left)
+        interleave_vector(LAST, (1,), third)
+        output(LAST, range(0, 2), "zbank")
+        store(LAST - 1, all_tiles)
+        interleave_vector(LAST, (1,), fourth)
+        quantize_h(LAST, 1, third)
+        quantize_h(LAST, 1, fourth)
+        output(LAST, range(2, 4))
+        store(LAST, range(0, 2))
+        store(LAST, range(2, 4))

@@ -26,8 +26,9 @@ STEPS = B * HALVES
 LAST = STEPS - 1
 LEAD = 4
 ZBUFS = 4
-NT = 208
+NT = 240
 G_TURNS = range(2, STEPS - 2)
+V_TURNS = range(2, STEPS - LEAD, 2)
 
 
 def tile_mlpmodelpredictor_pb_t_w8_kernel(
@@ -50,6 +51,7 @@ def tile_mlpmodelpredictor_pb_t_w8_kernel(
         w1_scales = keep.tile([P, G, PACK, P], U8, name="w1_scales", align_bytes=64)
         b2_rows = keep.tile([P, H // G], BF16, name="b2_rows")
         b2_cols = keep.tile([P, B * G, PACK], BF16, name="b2_cols")
+        b2_wide = keep.tile([P, B * G, PACK], F32, name="b2_wide")
         b3_rows = keep.tile([P, B, O], BF16, name="b3_rows")
 
         gbuf = keep.tile([P, ROWS * PACK], BF16, name="gbuf", align_bytes=64)
@@ -199,7 +201,17 @@ def tile_mlpmodelpredictor_pb_t_w8_kernel(
                     stop=True,
                 )
 
-        def relu(s, g, cols):
+        def relu_vector(s, g, t):
+            nc.vector.tensor_scalar(
+                out=h_planes[s][:, g, t, :],
+                in0=h_banks[s, g, t][:],
+                scalar1=b2_wide[:, s // HALVES * G + g, t : t + 1],
+                scalar2=0.0,
+                op0=ALU.add,
+                op1=ALU.max,
+            )
+
+        def relu(s, g, cols, slots=range(PACK)):
             if g == 0 and cols.start == 0:
                 planes = work.tile([P, G, PACK, ROWS], BF16, name="hplanar", bufs=3)
                 h_planes[s] = planes
@@ -207,7 +219,7 @@ def tile_mlpmodelpredictor_pb_t_w8_kernel(
                     [P, G * ROWS * PACK], BF16, name="hinter", bufs=4, align_bytes=64
                 )
                 h_inter[s] = inter
-            for t in range(PACK):
+            for t in slots:
                 nc.scalar.activation(
                     out=h_planes[s][:, g, t, cols],
                     in_=h_banks[s, g, t][:, cols],
@@ -359,6 +371,7 @@ def tile_mlpmodelpredictor_pb_t_w8_kernel(
         widen_z(2, on_g, all_tiles)
         scale_z(1, 0)
         scale_z(1, 1)
+        nc.vector.tensor_copy(out=b2_wide[:], in_=b2_cols[:])
         interleave_w3(0, on_v, both_passes)
         hidden(0, 1, range(PACK))
 
@@ -400,7 +413,9 @@ def tile_mlpmodelpredictor_pb_t_w8_kernel(
                 if s + 2 < STEPS:
                     transpose_z(s + 2)
                 hidden(s, 1, (2, 3))
-            relu(s, 1, whole)
+            if s in V_TURNS:
+                relu_vector(s, 1, 0)
+            relu(s, 1, whole, range(1, PACK) if s in V_TURNS else range(PACK))
             interleave_tensor(s, 0)
             copy_mixed(s, 0)
             if s == 0:

@@ -235,8 +235,8 @@ def tile_mlpmodelpredictor_pb_t_w8_kernel(
         def interleave_vector(s, passes, cols):
             for g in passes:
                 nc.vector.tensor_copy(
-                    out=interleaved(s, g, cols).rearrange("p (c i t) -> p c t i", i=4, t=PACK),
-                    in_=h_planes[s][:, g, :, cols].rearrange("p t (c i) -> p c t i", i=4),
+                    out=interleaved(s, g, cols).rearrange("p (c i t) -> p c t i", i=2, t=PACK),
+                    in_=h_planes[s][:, g, :, cols].rearrange("p t (c i) -> p c t i", i=2),
                 )
 
         def interleave_gpsimd(s):
@@ -278,13 +278,13 @@ def tile_mlpmodelpredictor_pb_t_w8_kernel(
                 in_=interleaved(s, g, cols),
             )
 
-        def interleave_w3(b, copy, passes):
+        def interleave_w3(b, copy, passes, run=2):
             if passes.start == 0:
                 tile = work.tile([P, G, O, PACK], BF16, name="w3inter", bufs=3, align_bytes=64)
                 w3_inter[b] = tile
             copy(
-                out=w3_inter[b][:, passes].rearrange("p g (c i) t -> p g c t i", i=4),
-                in_=w3_raw[b][:, passes].rearrange("p g t (c i) -> p g c t i", i=4),
+                out=w3_inter[b][:, passes].rearrange("p g (c i) t -> p g c t i", i=run),
+                in_=w3_raw[b][:, passes].rearrange("p g t (c i) -> p g c t i", i=run),
             )
 
         def quantize_w3(b):
@@ -391,7 +391,10 @@ def tile_mlpmodelpredictor_pb_t_w8_kernel(
                 quantize_w3(0)
             if 2 <= s < STEPS - 2:
                 g = s % G
-                interleave_w3(s // G + 1, on_v if scalar_widens else on_s, slice(g, g + 1))
+                if scalar_widens:
+                    interleave_w3(s // G + 1, on_v, slice(g, g + 1))
+                else:
+                    interleave_w3(s // G + 1, on_s, slice(g, g + 1), 4)
             if s >= 2 * G and s % G == 0:
                 quantize_w3(s // G)
             if s >= 2:

@@ -24,11 +24,13 @@ SUB = ROWS // P
 HALVES = T // ROWS
 STEPS = B * HALVES
 LAST = STEPS - 1
+
+COLS = G * ROWS
 LEAD = 4
-ZBUFS = 4
-NT = 240
-G_TURNS = range(2, STEPS - 2)
-V_TURNS = range(2, STEPS - LEAD, 2)
+ZBUFS = 5
+G_FROM = 384
+G_STEPS = range(0, STEPS - 2)
+NT = 192
 
 
 def tile_mlpmodelpredictor_pb_t_w8_kernel(
@@ -51,26 +53,29 @@ def tile_mlpmodelpredictor_pb_t_w8_kernel(
         w1_scales = keep.tile([P, G, PACK, P], U8, name="w1_scales", align_bytes=64)
         b2_rows = keep.tile([P, H // G], BF16, name="b2_rows")
         b2_cols = keep.tile([P, B * G, PACK], BF16, name="b2_cols")
-        b2_wide = keep.tile([P, B * G, PACK], F32, name="b2_wide")
         b3_rows = keep.tile([P, B, O], BF16, name="b3_rows")
+        w3_codes = keep.tile([P, B, G, O], U32, name="w3_codes", align_bytes=64)
+        w3_exps = keep.tile([P, B, G, O], U8, name="w3_exps", align_bytes=64)
 
-        gbuf = keep.tile([P, ROWS * PACK], BF16, name="gbuf", align_bytes=64)
+        gbuf = keep.tile([P, (COLS - G_FROM) * PACK], BF16, name="gbuf", align_bytes=64)
         zbuf = []
         for i in range(ZBUFS):
             zbuf_tile = keep.tile([P, ROWS * PACK], BF16, name="zbuf%d" % i, align_bytes=64)
             zbuf.append(zbuf_tile)
 
         def zbuf_of(s):
-            return zbuf[s % 2 if s < 3 else (1 - s) % ZBUFS]
+            if s == 0:
+                return gbuf[:, 0 : ROWS * PACK]
+            return zbuf[s % ZBUFS][:]
 
         zbytes = []
+        for s in range(STEPS):
+            zb = loads.tile([P, SUB * R], U8, name="zb", bufs=STEPS, align_bytes=64)
+            zbytes.append(zb)
         w3_raw = []
-        for b in range(B):
-            w3_tile = loads.tile([P, G, PACK, O], BF16, name="w3_tile", bufs=B)
+        for pair in range(B // 2):
+            w3_tile = loads.tile([P, 2 * G, PACK, O], BF16, name="w3_tile", bufs=B // 2)
             w3_raw.append(w3_tile)
-            for hf in range(HALVES):
-                zb = loads.tile([P, SUB * R], U8, name="zb", bufs=STEPS, align_bytes=64)
-                zbytes.append(zb)
 
         def load_z(s, tiles_a_load=SUB):
             b, hf = divmod(s, HALVES)
@@ -85,9 +90,12 @@ def tile_mlpmodelpredictor_pb_t_w8_kernel(
                     ),
                 )
 
-        def load_w3(b):
+        def load_w3(pair):
             nc.sync.dma_start(
-                out=w3_raw[b][:], in_=w3[b].rearrange("(g p t) o -> p g t o", p=P, t=PACK)
+                out=w3_raw[pair][:].rearrange("p c t o -> p c (t o)"),
+                in_=w3[2 * pair : 2 * pair + 2].rearrange(
+                    "b (g p t) o -> p (b g) (t o)", p=P, t=PACK
+                ),
             )
 
         nc.vector.memset(w1s_raw[:].bitcast(I32), 0)
@@ -111,25 +119,24 @@ def tile_mlpmodelpredictor_pb_t_w8_kernel(
         )
         nc.sync.dma_start(out=w1_raw[:, 1, :], in_=w1_words[:, H // G : H])
         load_z(2)
-        load_w3(0)
-        load_w3(1)
         load_z(3)
+        load_w3(0)
         load_z(4)
+        load_w3(1)
         load_z(5)
-        load_w3(2)
-        load_w3(3)
         nc.sync.dma_start(
             out=b3_rows[:].rearrange("p b o -> p (b o)"),
             in_=b3.rearrange("b o -> (b o)").partition_broadcast(P),
         )
-        for b in range(4, B):
-            load_w3(b)
-        for s in range(6, STEPS):
+        load_z(6)
+        load_w3(2)
+        load_w3(3)
+        for s in range(7, STEPS):
             load_z(s)
 
         z_banks, z_codes, z_exps = {}, {}, {}
         h_banks, h_planes, h_inter, h_codes, h_exps = {}, {}, {}, {}, {}
-        mixed, out_banks, w3_inter, w3_codes, w3_exps = {}, {}, {}, {}, {}
+        v_banks, mixed, out_banks, w3_inter = {}, {}, {}, {}
 
         def permute_w1_codes(g):
             nc.vector.tensor_copy(
@@ -147,7 +154,7 @@ def tile_mlpmodelpredictor_pb_t_w8_kernel(
             copy(out=zbuf_of(s)[:, cols], in_=zbytes[s][:, cols].bitcast(FP8))
 
         def transpose_z(s, halves=(0, 1)):
-            words = zbuf_of(s)[:].bitcast(F32)
+            words = zbuf_of(s).bitcast(F32)
             for half in halves:
                 bank = psum.tile([P, 2, 2, P], F32, name="zbank", bufs=2)
                 z_banks[s, half] = bank
@@ -186,130 +193,173 @@ def tile_mlpmodelpredictor_pb_t_w8_kernel(
                 in_=zbuf_of(s)[:, cols.start * PACK : cols.stop * PACK],
             )
 
-        def hidden(s, g, slots, cols=slice(0, ROWS)):
-            for t in slots:
-                if cols.start == 0:
-                    bank = psum.tile([P, ROWS], F32, name="hbank", bufs=PACK)
-                    h_banks[s, g, t] = bank
-                nc.tensor.matmul_mx(
-                    out=h_banks[s, g, t][:, cols],
-                    lhsT=w1_codes[:, g, t, :].bitcast(FP8X4),
-                    lhsT_scale=w1_scales[:, g, t, :],
-                    rhs=z_codes[s][:, cols].bitcast(FP8X4),
-                    rhs_scale=z_exps[s][:, cols],
-                    start=True,
-                    stop=True,
-                )
+        def product(dst, s, g, t, lo, hi):
+            nc.tensor.matmul_mx(
+                out=dst,
+                lhsT=w1_codes[:, g, t, :].bitcast(FP8X4),
+                lhsT_scale=w1_scales[:, g, t, :],
+                rhs=z_codes[s][:, lo:hi].bitcast(FP8X4),
+                rhs_scale=z_exps[s][:, lo:hi],
+                start=True,
+                stop=True,
+            )
 
-        def relu_vector(s, g, t):
+        def hidden(s, g, slots, cols, tag="hbank"):
+            for t in slots:
+                if (s, g, t) not in h_banks:
+                    bank = psum.tile([P, ROWS], F32, name=tag, bufs=PACK if tag == "hbank" else 2)
+                    h_banks[s, g, t] = bank
+                lo = cols.start
+                for width in (ROWS, ROWS // 2, ROWS // 4):
+                    if cols.stop - lo >= width:
+                        product(h_banks[s, g, t][:, lo : lo + width], s, g, t, lo, lo + width)
+                        lo += width
+
+        def inter_tile(s):
+            if s not in h_inter:
+                tile = work.tile([P, COLS * PACK], BF16, name="hinter", bufs=4, align_bytes=64)
+                h_inter[s] = tile
+            return h_inter[s]
+
+        def interleaved(s, lo, hi):
+            if s in G_STEPS and lo >= G_FROM:
+                return gbuf[:, (lo - G_FROM) * PACK : (hi - G_FROM) * PACK]
+            return inter_tile(s)[:, lo * PACK : hi * PACK]
+
+        def hidden_tile(s, g, i, tag="xbank"):
+            bank = psum.tile([P, PACK, P], F32, name=tag, bufs=1 if tag == "xbank" else 2)
+            v_banks[s, g, i] = bank
+            for t in range(PACK):
+                product(bank[:, t, :], s, g, t, i * P, (i + 1) * P)
+
+        def add_bias(s, g, i):
+            lo = g * ROWS + i * P
+            nc.vector.tensor_tensor(
+                out=interleaved(s, lo, lo + P).rearrange("p (n t) -> p n t", t=PACK),
+                in0=v_banks[s, g, i][:].rearrange("p t n -> p n t"),
+                in1=b2_cols[:, s // HALVES * G + g, :].unsqueeze(1).to_broadcast([P, P, PACK]),
+                op=ALU.add,
+            )
+
+        def relu_in_place(s, lo, hi):
             nc.vector.tensor_scalar(
-                out=h_planes[s][:, g, t, :],
-                in0=h_banks[s, g, t][:],
-                scalar1=b2_wide[:, s // HALVES * G + g, t : t + 1],
-                scalar2=0.0,
-                op0=ALU.add,
-                op1=ALU.max,
+                out=interleaved(s, lo, hi),
+                in0=interleaved(s, lo, hi),
+                scalar1=0.0,
+                scalar2=None,
+                op0=ALU.max,
             )
 
         def relu(s, g, cols, slots=range(PACK)):
-            if g == 0 and cols.start == 0:
-                planes = work.tile([P, G, PACK, ROWS], BF16, name="hplanar", bufs=3)
+            if s not in h_planes:
+                planes = work.tile([P, PACK, COLS], BF16, name="hplanar", bufs=3)
                 h_planes[s] = planes
-                inter = work.tile(
-                    [P, G * ROWS * PACK], BF16, name="hinter", bufs=4, align_bytes=64
-                )
-                h_inter[s] = inter
             for t in slots:
                 nc.scalar.activation(
-                    out=h_planes[s][:, g, t, cols],
+                    out=h_planes[s][:, t, g * ROWS + cols.start : g * ROWS + cols.stop],
                     in_=h_banks[s, g, t][:, cols],
                     func=ACT.Relu,
                     bias=b2_cols[:, s // HALVES * G + g, t : t + 1],
                 )
 
-        def interleaved(s, g, cols):
-            if g == 1 and s < G_TURNS.stop - 1:
-                return gbuf[:, cols.start * PACK : cols.stop * PACK]
-            return h_inter[s][:, (g * ROWS + cols.start) * PACK : (g * ROWS + cols.stop) * PACK]
-
-        def interleave_vector(s, passes, cols):
-            for g in passes:
-                nc.vector.tensor_copy(
-                    out=interleaved(s, g, cols).rearrange("p (c i t) -> p c t i", i=2, t=PACK),
-                    in_=h_planes[s][:, g, :, cols].rearrange("p t (c i) -> p c t i", i=2),
-                )
-
-        def interleave_gpsimd(s):
-            nc.gpsimd.tensor_scalar(
-                out=interleaved(s, 1, whole).rearrange("p (n t) -> p n t", t=PACK),
-                in0=h_planes[s][:, 1].rearrange("p t n -> p n t"),
-                scalar1=1.0,
-                scalar2=0.0,
-                op0=ALU.mult,
-                op1=ALU.add,
+        def interleave_vector(s, lo, hi):
+            nc.vector.tensor_copy(
+                out=interleaved(s, lo, hi).rearrange("p (c i t) -> p c t i", i=2, t=PACK),
+                in_=h_planes[s][:, :, lo:hi].rearrange("p t (c i) -> p c t i", i=2),
             )
 
-        def interleave_tensor(s, g, tag="ibank"):
+        def copy_gpsimd(out, in_):
+            nc.gpsimd.tensor_scalar(
+                out=out, in0=in_, scalar1=1.0, scalar2=0.0, op0=ALU.mult, op1=ALU.add
+            )
+
+        def interleave_gpsimd(s):
+            copy_gpsimd(
+                out=interleaved(s, G_FROM, COLS).rearrange("p (n t) -> p n t", t=PACK),
+                in_=h_planes[s][:, :, G_FROM:COLS].rearrange("p t n -> p n t"),
+            )
+
+        def interleave_tensor(s, lo, hi, tag="ibank"):
             bank = psum.tile([P, ROWS // 2, PACK], BF16, name=tag, bufs=1)
-            mixed[s, g] = bank
-            for n in range(0, NT, NT // 2):
+            mixed[s, lo] = bank
+            n = (hi - lo) // 2
+            for j in range(2):
                 nc.tensor.matmul(
-                    bank[:, n : n + NT // 2, :],
+                    bank[:, j * n : (j + 1) * n, :],
                     lhsT=ident_b[:],
-                    rhs=h_planes[s][:, g, :, n : n + NT // 2].rearrange("p t n -> p n t"),
+                    rhs=h_planes[s][:, :, lo + j * n : lo + (j + 1) * n].rearrange(
+                        "p t n -> p n t"
+                    ),
                     start=True,
                     stop=True,
                 )
 
-        def copy_mixed(s, g):
+        def copy_mixed(s, lo, hi):
             nc.scalar.copy(
-                out=interleaved(s, g, slice(0, NT)).bitcast(F32),
-                in_=mixed[s, g][:, 0:NT, :].rearrange("p n t -> p (n t)").bitcast(F32),
+                out=interleaved(s, lo, hi).bitcast(F32),
+                in_=mixed[s, lo][:, 0 : hi - lo, :].rearrange("p n t -> p (n t)").bitcast(F32),
             )
 
-        def quantize_h(s, g, cols):
+        def quantize_h(s, lo, hi):
             if s not in h_codes:
-                codes = work.tile([P, G, ROWS], U32, name="hcodes", bufs=3, align_bytes=64)
-                exps = work.tile([P, G, ROWS], U8, name="hexp", bufs=3, align_bytes=64)
+                codes = work.tile([P, COLS], U32, name="hcodes", bufs=3, align_bytes=64)
+                exps = work.tile([P, COLS], U8, name="hexp", bufs=3, align_bytes=64)
                 h_codes[s], h_exps[s] = codes, exps
             nc.vector.quantize_mx(
-                out=h_codes[s][:, g, cols].bitcast(FP8X4),
-                scales=h_exps[s][:, g, cols],
-                in_=interleaved(s, g, cols),
+                out=h_codes[s][:, lo:hi].bitcast(FP8X4),
+                scales=h_exps[s][:, lo:hi],
+                in_=interleaved(s, lo, hi),
             )
 
-        def interleave_w3(b, copy, passes, run=2):
-            if passes.start == 0:
-                tile = work.tile([P, G, O, PACK], BF16, name="w3inter", bufs=3, align_bytes=64)
+        def quantize_step(s):
+            quantize_h(s, 0, G_FROM)
+            quantize_h(s, G_FROM, ROWS)
+            quantize_h(s, ROWS, COLS)
+
+        def interleave_w3_pair(pair):
+            copy_gpsimd(
+                out=gbuf[:, 0 : 2 * G * O * PACK].rearrange("p (c o t) -> p c o t", o=O, t=PACK),
+                in_=w3_raw[pair][:].rearrange("p c t o -> p c o t"),
+            )
+
+        def quantize_w3_pair(pair):
+            nc.vector.quantize_mx(
+                out=w3_codes[:, 2 * pair : 2 * pair + 2]
+                .rearrange("p b g o -> p (b g o)")
+                .bitcast(FP8X4),
+                scales=w3_exps[:, 2 * pair : 2 * pair + 2].rearrange("p b g o -> p (b g o)"),
+                in_=gbuf[:, 0 : 2 * G * O * PACK],
+            )
+
+        def interleave_w3(b, g, copy, run):
+            if g == 0:
+                tile = work.tile([P, G, O, PACK], BF16, name="w3inter", bufs=2, align_bytes=64)
                 w3_inter[b] = tile
             copy(
-                out=w3_inter[b][:, passes].rearrange("p g (c i) t -> p g c t i", i=run),
-                in_=w3_raw[b][:, passes].rearrange("p g t (c i) -> p g c t i", i=run),
+                out=w3_inter[b][:, g].rearrange("p (c i) t -> p c t i", i=run),
+                in_=w3_raw[b // 2][:, b % 2 * G + g].rearrange("p t (c i) -> p c t i", i=run),
             )
 
         def quantize_w3(b):
-            codes = work.tile([P, G, O], U32, name="w3codes", bufs=B, align_bytes=64)
-            exps = work.tile([P, G, O], U8, name="w3exp", bufs=B, align_bytes=64)
-            w3_codes[b], w3_exps[b] = codes, exps
             nc.vector.quantize_mx(
-                out=codes[:].rearrange("p g o -> p (g o)").bitcast(FP8X4),
-                scales=exps[:].rearrange("p g o -> p (g o)"),
+                out=w3_codes[:, b].rearrange("p g o -> p (g o)").bitcast(FP8X4),
+                scales=w3_exps[:, b].rearrange("p g o -> p (g o)"),
                 in_=w3_inter[b][:].rearrange("p g o t -> p (g o t)"),
             )
 
-        def output(s, tiles, tag="obank"):
+        def output(s, tiles, tag="xbank"):
             b = s // HALVES
-            bank = psum.tile([P, SUB, O], F32, name=tag, bufs=1 if tag == "obank" else 2)
+            bank = psum.tile([P, SUB, O], F32, name=tag, bufs=2 if tag == "zbank" else 1)
             out_banks[s, tiles.start] = bank
             for i in tiles:
-                rows = slice(i * P, (i + 1) * P)
                 for g in range(G):
+                    rows = slice(g * ROWS + i * P, g * ROWS + (i + 1) * P)
                     nc.tensor.matmul_mx(
                         out=bank[:, i, :],
-                        lhsT=h_codes[s][:, g, rows].bitcast(FP8X4),
-                        lhsT_scale=h_exps[s][:, g, rows],
-                        rhs=w3_codes[b][:, g, :].bitcast(FP8X4),
-                        rhs_scale=w3_exps[b][:, g, :],
+                        lhsT=h_codes[s][:, rows].bitcast(FP8X4),
+                        lhsT_scale=h_exps[s][:, rows],
+                        rhs=w3_codes[:, b, g, :].bitcast(FP8X4),
+                        rhs_scale=w3_exps[:, b, g, :],
                         start=(g == 0),
                         stop=(g == G - 1),
                     )
@@ -333,20 +383,20 @@ def tile_mlpmodelpredictor_pb_t_w8_kernel(
         def on_s_activation(out, in_):
             nc.scalar.activation(out=out, in_=in_, func=ACT.Copy)
 
-        whole, rest = slice(0, ROWS), slice(NT, ROWS)
+        whole, rest = slice(0, ROWS), slice(P, ROWS)
         left, right = slice(0, ROWS // 2), slice(ROWS // 2, ROWS)
-        third, fourth = slice(2 * P, 3 * P), slice(3 * P, ROWS)
-        all_tiles, both_passes = range(SUB), slice(0, G)
-        on_v, on_s, on_g = nc.vector.tensor_copy, nc.scalar.copy, nc.gpsimd.tensor_copy
+        all_tiles, all_slots = range(SUB), range(PACK)
+        on_v, on_s = nc.vector.tensor_copy, nc.scalar.copy
 
         for i, copy in enumerate((on_v, on_s_activation, on_v, on_s)):
             widen_z(0, copy, range(i, i + 1))
         widen_z(1, on_s, all_tiles)
         transpose_z(0)
-        b2_bank = psum.tile([P, SUB, O], F32, name="obank", bufs=1)
+        b2_bank = psum.tile([P, SUB, O], F32, name="xbank", bufs=1)
         b2_words = b2_rows[:].bitcast(F32)
         for u in range(2):
             nc.tensor.transpose(b2_bank[:, u, :], b2_words[:, u::2], ident_f[:])
+        widen_z(2, on_s, all_tiles)
         nc.scalar.copy(
             out=b2_cols[:]
             .rearrange("p c t -> p (c t)")
@@ -354,114 +404,113 @@ def tile_mlpmodelpredictor_pb_t_w8_kernel(
             .rearrange("p (c u) -> p c u", u=2),
             in_=b2_bank[:, 0:2, 0 : B * G].rearrange("p u c -> p c u"),
         )
+        widen_z(3, on_s, all_tiles)
         permute_w1_codes(0)
         scale_z(0, 0)
         permute_w1_scales(0)
         quantize_z(0, left)
         transpose_z(1, (0,))
-        hidden(0, 0, range(PACK), left)
+        hidden(0, 0, all_slots, left)
         relu(0, 0, left)
         scale_z(0, 1)
         permute_w1_codes(1)
         quantize_z(0, right)
         transpose_z(1, (1,))
-        hidden(0, 0, range(PACK), right)
+        hidden(0, 0, all_slots, right)
         relu(0, 0, right)
         permute_w1_scales(1)
-        widen_z(2, on_g, all_tiles)
+        interleave_w3_pair(0)
         scale_z(1, 0)
         scale_z(1, 1)
-        nc.vector.tensor_copy(out=b2_wide[:], in_=b2_cols[:])
-        interleave_w3(0, on_v, both_passes)
-        hidden(0, 1, range(PACK))
 
-        for s in range(LAST):
-            scalar_widens = 2 <= s < STEPS - LEAD
+        def t_range(s):
+            return (0, ROWS // 2) if s == 0 else (P, P + NT)
+
+        for s in range(STEPS - 2):
             if s >= 1:
-                relu(s, 0, whole)
-                if scalar_widens:
-                    widen_z(s + LEAD, on_s, all_tiles)
-                if s in G_TURNS:
-                    interleave_vector(s - 1, (0,), rest)
-                else:
-                    interleave_tensor(s - 1, 1)
-                    copy_mixed(s - 1, 1)
-                    interleave_vector(s - 1, (0, 1), rest)
-            if s == 1:
-                quantize_w3(0)
-            if 2 <= s < STEPS - 2:
-                g = s % G
-                if scalar_widens:
-                    interleave_w3(s // G + 1, on_v, slice(g, g + 1))
-                else:
-                    interleave_w3(s // G + 1, on_s, slice(g, g + 1), 4)
-            if s >= 2 * G and s % G == 0:
-                quantize_w3(s // G)
-            if s >= 2:
-                quantize_h(s - 2, 0, whole)
-                quantize_h(s - 2, 1, whole)
-            quantize_z(s + 1, whole)
-            if s == 1:
-                quantize_w3(1)
-            if s == 0:
-                interleave_w3(1, on_v, both_passes)
+                relu(s, 0, rest)
+            if s + LEAD < STEPS:
+                widen_z(s + LEAD, on_s, all_tiles)
+            if s >= 1:
+                interleave_vector(s - 1, t_range(s - 1)[1], G_FROM)
+                relu_in_place(s, 0, P)
+            if 1 <= s <= 4:
+                interleave_w3((s + 7) // 2, (s + 7) % 2, on_v, 2)
+            if 12 <= s <= 13:
+                interleave_w3(s - 6, 0, on_s, 4)
+                interleave_w3(s - 6, 1, on_s, 4)
+            if s in (3, 5):
+                quantize_w3((s + 5) // 2)
+            if s == 13:
+                quantize_w3(6)
             if s < 2:
-                widen_z(s + LEAD, on_g, all_tiles)
-            if s in G_TURNS:
+                quantize_w3_pair(s)
+            else:
+                quantize_step(s - 2)
+            quantize_z(s + 1, whole)
+            if s == 0:
+                interleave_w3_pair(1)
+            else:
                 interleave_gpsimd(s - 1)
             if s >= 3:
                 output(s - 3, all_tiles)
-            if s >= 1:
-                hidden(s, 1, (0, 1))
-                if s + 2 < STEPS:
-                    transpose_z(s + 2)
-                hidden(s, 1, (2, 3))
-            if s in V_TURNS:
-                relu_vector(s, 1, 0)
-            relu(s, 1, whole, range(1, PACK) if s in V_TURNS else range(PACK))
-            interleave_tensor(s, 0)
-            copy_mixed(s, 0)
-            if s == 0:
-                widen_z(3, on_s, all_tiles)
-                transpose_z(2)
-            hidden(s + 1, 0, (0, 1))
-            if s + 2 < STEPS:
-                scale_z(s + 2, 0)
-                scale_z(s + 2, 1)
-            else:
-                output(s - 2, all_tiles, "zbank")
-            hidden(s + 1, 0, (2, 3))
-            if s >= 3:
                 store(s - 3, all_tiles)
+            hidden(s, 1, (0, 1), whole)
+            transpose_z(s + 2)
+            hidden(s, 1, (2, 3), whole)
+            scale_z(s + 2, 0)
+            scale_z(s + 2, 1)
+            relu(s, 1, whole)
+            interleave_tensor(s, *t_range(s))
+            copy_mixed(s, *t_range(s))
+            hidden_tile(s + 1, 0, 0)
+            add_bias(s + 1, 0, 0)
+            hidden(s + 1, 0, all_slots, rest)
 
-        quantize_h(LAST - 2, 0, whole)
-        quantize_h(LAST - 2, 1, whole)
-        output(LAST - 2, all_tiles, "zbank")
-        relu(LAST, 0, whole)
-        interleave_tensor(LAST - 1, 1)
-        copy_mixed(LAST - 1, 1)
-        hidden(LAST, 1, range(PACK))
-        interleave_vector(LAST - 1, (0, 1), rest)
-        store(LAST - 3, all_tiles)
-        store(LAST - 2, all_tiles)
-        interleave_tensor(LAST, 0, "obank")
-        relu(LAST, 1, left)
-        copy_mixed(LAST, 0)
-        relu(LAST, 1, third)
-        relu(LAST, 1, fourth)
-        quantize_h(LAST - 1, 0, whole)
-        interleave_vector(LAST, (0,), rest)
-        quantize_h(LAST - 1, 1, whole)
-        output(LAST - 1, all_tiles, "zbank")
-        interleave_vector(LAST, (1,), left)
-        quantize_h(LAST, 0, whole)
-        quantize_h(LAST, 1, left)
-        interleave_vector(LAST, (1,), third)
-        output(LAST, range(0, 2), "zbank")
-        store(LAST - 1, all_tiles)
-        interleave_vector(LAST, (1,), fourth)
-        quantize_h(LAST, 1, third)
-        quantize_h(LAST, 1, fourth)
-        output(LAST, range(2, 4))
-        store(LAST, range(0, 2))
-        store(LAST, range(2, 4))
+        A, Z = LAST - 1, LAST
+        Q = ROWS // 2
+        relu(A, 0, rest)
+        interleave_vector(A - 1, t_range(A - 1)[1], G_FROM)
+        relu_in_place(A, 0, P)
+        quantize_w3(B - 1)
+        quantize_step(A - 2)
+        quantize_z(Z, whole)
+        interleave_gpsimd(A - 1)
+        output(A - 3, all_tiles)
+        store(A - 3, all_tiles)
+        hidden(A, 1, all_slots, whole)
+        relu(A, 1, whole)
+        output(A - 2, all_tiles, "zbank")
+        store(A - 2, all_tiles)
+        for i, tag in enumerate(("zbank", "xbank", "zbank", "zbank")):
+            hidden_tile(Z, 0, i, tag)
+            add_bias(Z, 0, i)
+            if i == 1:
+                interleave_tensor(A, P, P + Q)
+                copy_mixed(A, P, P + Q)
+        hidden(Z, 1, all_slots, whole)
+        interleave_tensor(A, ROWS, ROWS + Q)
+        relu(Z, 1, whole, (0, 1))
+        copy_mixed(A, ROWS, ROWS + Q)
+        interleave_tensor(A, ROWS + Q, COLS, "xbank")
+        relu(Z, 1, whole, (2, 3))
+        copy_mixed(A, ROWS + Q, COLS)
+        interleave_vector(A, P + Q, ROWS)
+        relu_in_place(Z, 0, ROWS)
+        quantize_step(A - 1)
+        output(A - 1, all_tiles, "zbank")
+        quantize_h(Z, 0, ROWS)
+        interleave_tensor(Z, ROWS, ROWS + Q)
+        copy_mixed(Z, ROWS, ROWS + Q)
+        quantize_h(A, 0, ROWS)
+        interleave_vector(Z, ROWS + Q, COLS)
+        quantize_h(A, ROWS, COLS)
+        store(A - 1, all_tiles)
+        output(A, all_tiles, "zbank")
+        quantize_h(Z, ROWS + Q, COLS)
+        quantize_h(Z, ROWS, ROWS + Q)
+        output(Z, range(2, 4), "zbank")
+        store(A, all_tiles)
+        output(Z, range(0, 2))
+        store(Z, range(2, 4))
+        store(Z, range(0, 2))

@@ -235,9 +235,12 @@ def tile_mlpmodelpredictor_pb_t_w8_kernel(
         def add_bias(s, g, i):
             lo = g * ROWS + i * P
             nc.vector.tensor_tensor(
-                out=interleaved(s, lo, lo + P).rearrange("p (n t) -> p n t", t=PACK),
-                in0=v_banks[s, g, i][:].rearrange("p t n -> p n t"),
-                in1=b2_cols[:, s // HALVES * G + g, :].unsqueeze(1).to_broadcast([P, P, PACK]),
+                out=interleaved(s, lo, lo + P).rearrange("p (c j t) -> p c t j", j=2, t=PACK),
+                in0=v_banks[s, g, i][:].rearrange("p t (c j) -> p c t j", j=2),
+                in1=b2_cols[:, s // HALVES * G + g, :]
+                .unsqueeze(1)
+                .unsqueeze(3)
+                .to_broadcast([P, P // 2, PACK, 2]),
                 op=ALU.add,
             )
 

@@ -26,11 +26,11 @@ STEPS = B * HALVES
 LAST = STEPS - 1
 
 COLS = G * ROWS
-LEAD = 4
-ZBUFS = 5
-G_FROM = 384
+LEAD = 5
+ZBUFS = 6
+G_FROM = 448
 G_STEPS = range(0, STEPS - 2)
-NT = 192
+NT = 176
 
 
 def tile_mlpmodelpredictor_pb_t_w8_kernel(
@@ -54,8 +54,8 @@ def tile_mlpmodelpredictor_pb_t_w8_kernel(
         b2_rows = keep.tile([P, H // G], BF16, name="b2_rows")
         b2_cols = keep.tile([P, B * G, PACK], BF16, name="b2_cols")
         b3_rows = keep.tile([P, B, O], BF16, name="b3_rows")
-        w3_codes = keep.tile([P, B, G, O], U32, name="w3_codes", align_bytes=64)
-        w3_exps = keep.tile([P, B, G, O], U8, name="w3_exps", align_bytes=64)
+        w3_codes = keep.tile([P, B * G * O], U32, name="w3_codes", align_bytes=64)
+        w3_exps = keep.tile([P, B * G * O], U8, name="w3_exps", align_bytes=64)
 
         gbuf = keep.tile([P, (COLS - G_FROM) * PACK], BF16, name="gbuf", align_bytes=64)
         zbuf = []
@@ -72,10 +72,7 @@ def tile_mlpmodelpredictor_pb_t_w8_kernel(
         for s in range(STEPS):
             zb = loads.tile([P, SUB * R], U8, name="zb", bufs=STEPS, align_bytes=64)
             zbytes.append(zb)
-        w3_raw = []
-        for pair in range(B // 2):
-            w3_tile = loads.tile([P, 2 * G, PACK, O], BF16, name="w3_tile", bufs=B // 2)
-            w3_raw.append(w3_tile)
+        w3_raw = {}
 
         def load_z(s, tiles_a_load=SUB):
             b, hf = divmod(s, HALVES)
@@ -90,12 +87,12 @@ def tile_mlpmodelpredictor_pb_t_w8_kernel(
                     ),
                 )
 
-        def load_w3(pair):
+        def load_w3(lo, hi):
+            tile = loads.tile([P, hi - lo, PACK, O], BF16, name="w3_raw%d" % lo)
+            w3_raw[lo] = tile
             nc.sync.dma_start(
-                out=w3_raw[pair][:].rearrange("p c t o -> p c (t o)"),
-                in_=w3[2 * pair : 2 * pair + 2].rearrange(
-                    "b (g p t) o -> p (b g) (t o)", p=P, t=PACK
-                ),
+                out=tile[:].rearrange("p c t o -> p c (t o)"),
+                in_=w3.rearrange("b (g p t) o -> p (b g) (t o)", p=P, t=PACK)[:, lo:hi],
             )
 
         nc.vector.memset(w1s_raw[:].bitcast(I32), 0)
@@ -107,8 +104,8 @@ def tile_mlpmodelpredictor_pb_t_w8_kernel(
             out=kscale[:], in_=z2_scale.rearrange("a c (p t) -> p (a c t)", t=PACK)
         )
         w1_words = sw1_words[0].rearrange("p n t -> p (n t)").bitcast(I32)
-        nc.sync.dma_start(out=w1_raw[:, 0, :], in_=w1_words[:, 0 : H // G])
         load_z(1)
+        nc.sync.dma_start(out=w1_raw[:, 0, :], in_=w1_words[:, 0 : H // G])
         for q in range(4):
             nc.sync.dma_start(
                 out=w1s_raw[32 * q : 32 * q + 4, :].bitcast(I32),
@@ -117,22 +114,24 @@ def tile_mlpmodelpredictor_pb_t_w8_kernel(
         nc.sync.dma_start(
             out=b2_rows[0 : B * G, :], in_=b2.rearrange("b (g n) -> (b g) n", g=G)
         )
-        nc.sync.dma_start(out=w1_raw[:, 1, :], in_=w1_words[:, H // G : H])
         load_z(2)
         load_z(3)
-        load_w3(0)
+        nc.sync.dma_start(out=w1_raw[:, 1, :], in_=w1_words[:, H // G : H])
         load_z(4)
-        load_w3(1)
+        load_w3(0, 3)
         load_z(5)
+        load_w3(3, 7)
+        load_z(6)
+        for c in range(7, 10):
+            load_w3(c, c + 1)
         nc.sync.dma_start(
             out=b3_rows[:].rearrange("p b o -> p (b o)"),
             in_=b3.rearrange("b o -> (b o)").partition_broadcast(P),
         )
-        load_z(6)
-        load_w3(2)
-        load_w3(3)
         for s in range(7, STEPS):
             load_z(s)
+        for c in range(10, B * G, G):
+            load_w3(c, c + G)
 
         z_banks, z_codes, z_exps = {}, {}, {}
         h_banks, h_planes, h_inter, h_codes, h_exps = {}, {}, {}, {}, {}
@@ -215,6 +214,9 @@ def tile_mlpmodelpredictor_pb_t_w8_kernel(
                         product(h_banks[s, g, t][:, lo : lo + width], s, g, t, lo, lo + width)
                         lo += width
 
+        def g_from(s):
+            return ROWS if s == 0 else G_FROM
+
         def inter_tile(s):
             if s not in h_inter:
                 tile = work.tile([P, COLS * PACK], BF16, name="hinter", bufs=4, align_bytes=64)
@@ -222,8 +224,8 @@ def tile_mlpmodelpredictor_pb_t_w8_kernel(
             return h_inter[s]
 
         def interleaved(s, lo, hi):
-            if s in G_STEPS and lo >= G_FROM:
-                return gbuf[:, (lo - G_FROM) * PACK : (hi - G_FROM) * PACK]
+            if s in G_STEPS and lo >= g_from(s):
+                return gbuf[:, (lo - g_from(s)) * PACK : (hi - g_from(s)) * PACK]
             return inter_tile(s)[:, lo * PACK : hi * PACK]
 
         def hidden_tile(s, g, i, tag="xbank"):
@@ -278,15 +280,17 @@ def tile_mlpmodelpredictor_pb_t_w8_kernel(
 
         def interleave_gpsimd(s):
             copy_gpsimd(
-                out=interleaved(s, G_FROM, COLS).rearrange("p (n t) -> p n t", t=PACK),
-                in_=h_planes[s][:, :, G_FROM:COLS].rearrange("p t n -> p n t"),
+                out=interleaved(s, g_from(s), COLS).rearrange("p (n t) -> p n t", t=PACK),
+                in_=h_planes[s][:, :, g_from(s) : COLS].rearrange("p t n -> p n t"),
             )
 
-        def interleave_tensor(s, lo, hi, tag="ibank"):
-            bank = psum.tile([P, ROWS // 2, PACK], BF16, name=tag, bufs=1)
-            mixed[s, lo] = bank
+        def interleave_tensor(s, lo, hi, tag="ibank", parts=(0, 1)):
+            if 0 in parts:
+                bank = psum.tile([P, ROWS // 2, PACK], BF16, name=tag, bufs=1)
+                mixed[s, lo] = bank
+            bank = mixed[s, lo]
             n = (hi - lo) // 2
-            for j in range(2):
+            for j in parts:
                 nc.tensor.matmul(
                     bank[:, j * n : (j + 1) * n, :],
                     lhsT=ident_b[:],
@@ -314,40 +318,50 @@ def tile_mlpmodelpredictor_pb_t_w8_kernel(
                 in_=interleaved(s, lo, hi),
             )
 
+        def quantize_own(s):
+            cuts = [0, ROWS] if s == 0 else [0, 3 * P, G_FROM]
+            for lo, hi in zip(cuts, cuts[1:]):
+                quantize_h(s, lo, hi)
+
+        def quantize_gbuf(s):
+            cuts = [ROWS, COLS] if s == 0 else [G_FROM, ROWS, COLS]
+            for lo, hi in zip(cuts, cuts[1:]):
+                quantize_h(s, lo, hi)
+
         def quantize_step(s):
-            quantize_h(s, 0, G_FROM)
-            quantize_h(s, G_FROM, ROWS)
-            quantize_h(s, ROWS, COLS)
+            quantize_own(s)
+            quantize_gbuf(s)
 
-        def interleave_w3_pair(pair):
+        def interleave_w3_gpsimd(lo, hi):
+            w3_inter[lo] = gbuf
             copy_gpsimd(
-                out=gbuf[:, 0 : 2 * G * O * PACK].rearrange("p (c o t) -> p c o t", o=O, t=PACK),
-                in_=w3_raw[pair][:].rearrange("p c t o -> p c o t"),
+                out=gbuf[:, 0 : (hi - lo) * O * PACK].rearrange(
+                    "p (c o t) -> p c o t", o=O, t=PACK
+                ),
+                in_=w3_raw[lo][:].rearrange("p c t o -> p c o t"),
             )
 
-        def quantize_w3_pair(pair):
+        def interleave_w3_scalar(lo, hi):
+            tile = work.tile([P, G * O * PACK], BF16, name="w3inter", bufs=2, align_bytes=64)
+            w3_inter[lo] = tile
+            nc.scalar.copy(
+                out=tile[:, 0 : (hi - lo) * O * PACK].rearrange(
+                    "p (c j i t) -> p c j t i", c=hi - lo, i=4, t=PACK
+                ),
+                in_=w3_raw[lo][:].rearrange("p c t (j i) -> p c j t i", i=4),
+            )
+
+        def quantize_w3(lo, hi):
             nc.vector.quantize_mx(
-                out=w3_codes[:, 2 * pair : 2 * pair + 2]
-                .rearrange("p b g o -> p (b g o)")
-                .bitcast(FP8X4),
-                scales=w3_exps[:, 2 * pair : 2 * pair + 2].rearrange("p b g o -> p (b g o)"),
-                in_=gbuf[:, 0 : 2 * G * O * PACK],
+                out=w3_codes[:, lo * O : hi * O].bitcast(FP8X4),
+                scales=w3_exps[:, lo * O : hi * O],
+                in_=w3_inter[lo][:, 0 : (hi - lo) * O * PACK],
             )
 
-        def interleave_w3(b, g, copy, run):
-            if g == 0:
-                tile = work.tile([P, G, O, PACK], BF16, name="w3inter", bufs=2, align_bytes=64)
-                w3_inter[b] = tile
-            copy(
-                out=w3_inter[b][:, g].rearrange("p (c i) t -> p c t i", i=run),
-                in_=w3_raw[b // 2][:, b % 2 * G + g].rearrange("p t (c i) -> p c t i", i=run),
-            )
-
-        def quantize_w3(b):
-            nc.vector.quantize_mx(
-                out=w3_codes[:, b].rearrange("p g o -> p (g o)").bitcast(FP8X4),
-                scales=w3_exps[:, b].rearrange("p g o -> p (g o)"),
-                in_=w3_inter[b][:].rearrange("p g o t -> p (g o t)"),
+        def interleave_scalar(s, lo, hi):
+            nc.scalar.copy(
+                out=interleaved(s, lo, hi).rearrange("p (c i t) -> p c t i", i=4, t=PACK),
+                in_=h_planes[s][:, :, lo:hi].rearrange("p t (c i) -> p c t i", i=4),
             )
 
         def output(s, tiles, tag="xbank"):
@@ -357,12 +371,13 @@ def tile_mlpmodelpredictor_pb_t_w8_kernel(
             for i in tiles:
                 for g in range(G):
                     rows = slice(g * ROWS + i * P, g * ROWS + (i + 1) * P)
+                    chans = slice((b * G + g) * O, (b * G + g + 1) * O)
                     nc.tensor.matmul_mx(
                         out=bank[:, i, :],
                         lhsT=h_codes[s][:, rows].bitcast(FP8X4),
                         lhsT_scale=h_exps[s][:, rows],
-                        rhs=w3_codes[:, b, g, :].bitcast(FP8X4),
-                        rhs_scale=w3_exps[:, b, g, :],
+                        rhs=w3_codes[:, chans].bitcast(FP8X4),
+                        rhs_scale=w3_exps[:, chans],
                         start=(g == 0),
                         stop=(g == G - 1),
                     )
@@ -370,7 +385,7 @@ def tile_mlpmodelpredictor_pb_t_w8_kernel(
         def store(s, tiles):
             b, hf = divmod(s, HALVES)
             n = len(tiles)
-            result = work.tile([P, SUB, O], F32, name="result", bufs=3)
+            result = work.tile([P, SUB, O], F32, name="result", bufs=4)
             nc.vector.tensor_tensor(
                 out=result[:, 0:n, :],
                 in0=out_banks[s, tiles.start][:, tiles.start : tiles.stop, :],
@@ -408,6 +423,7 @@ def tile_mlpmodelpredictor_pb_t_w8_kernel(
             in_=b2_bank[:, 0:2, 0 : B * G].rearrange("p u c -> p c u"),
         )
         widen_z(3, on_s, all_tiles)
+        widen_z(4, on_s, all_tiles)
         permute_w1_codes(0)
         scale_z(0, 0)
         permute_w1_scales(0)
@@ -422,37 +438,46 @@ def tile_mlpmodelpredictor_pb_t_w8_kernel(
         hidden(0, 0, all_slots, right)
         relu(0, 0, right)
         permute_w1_scales(1)
-        interleave_w3_pair(0)
+        interleave_w3_gpsimd(0, 3)
         scale_z(1, 0)
         scale_z(1, 1)
 
+        def v_tiles(s):
+            return 2 if s <= 3 else 1
+
         def t_range(s):
-            return (0, ROWS // 2) if s == 0 else (P, P + NT)
+            return (0, 2 * P) if s == 0 else (v_tiles(s) * P, G_FROM if s <= 3 else P + NT)
 
         for s in range(STEPS - 2):
             if s >= 1:
-                relu(s, 0, rest)
+                relu(s, 0, slice(v_tiles(s) * P, ROWS))
             if s + LEAD < STEPS:
                 widen_z(s + LEAD, on_s, all_tiles)
-            if s >= 1:
-                interleave_vector(s - 1, t_range(s - 1)[1], G_FROM)
-                relu_in_place(s, 0, P)
-            if 1 <= s <= 4:
-                interleave_w3((s + 7) // 2, (s + 7) % 2, on_v, 2)
-            if 12 <= s <= 13:
-                interleave_w3(s - 6, 0, on_s, 4)
-                interleave_w3(s - 6, 1, on_s, 4)
-            if s in (3, 5):
-                quantize_w3((s + 5) // 2)
-            if s == 13:
-                quantize_w3(6)
-            if s < 2:
-                quantize_w3_pair(s)
             else:
-                quantize_step(s - 2)
+                interleave_w3_scalar(2 * s - 12, 2 * s - 10)
+            if 1 <= s <= 3:
+                interleave_w3_scalar(s + 6, s + 7)
+            if s == 1:
+                interleave_vector(0, 2 * P, ROWS)
+            elif s >= 5:
+                interleave_vector(s - 1, t_range(s - 1)[1], G_FROM)
+            if 2 <= s <= 4:
+                quantize_w3(s + 5, s + 6)
+            if s >= 2:
+                quantize_own(s - 2)
+            if s >= 1:
+                relu_in_place(s, 0, v_tiles(s) * P)
+            if s >= 12:
+                quantize_w3(2 * s - 14, 2 * s - 12)
+            if s == 0:
+                quantize_w3(0, 3)
+            elif s == 1:
+                quantize_w3(3, 7)
+            else:
+                quantize_gbuf(s - 2)
             quantize_z(s + 1, whole)
             if s == 0:
-                interleave_w3_pair(1)
+                interleave_w3_gpsimd(3, 7)
             else:
                 interleave_gpsimd(s - 1)
             if s >= 3:
@@ -462,57 +487,67 @@ def tile_mlpmodelpredictor_pb_t_w8_kernel(
             transpose_z(s + 2)
             hidden(s, 1, (2, 3), whole)
             scale_z(s + 2, 0)
+            if v_tiles(s + 1) == 2:
+                hidden_tile(s + 1, 0, 1)
+                add_bias(s + 1, 0, 1)
             scale_z(s + 2, 1)
             relu(s, 1, whole)
             interleave_tensor(s, *t_range(s))
             copy_mixed(s, *t_range(s))
             hidden_tile(s + 1, 0, 0)
             add_bias(s + 1, 0, 0)
-            hidden(s + 1, 0, all_slots, rest)
+            hidden(s + 1, 0, all_slots, slice(v_tiles(s + 1) * P, ROWS))
 
         A, Z = LAST - 1, LAST
         Q = ROWS // 2
         relu(A, 0, rest)
         interleave_vector(A - 1, t_range(A - 1)[1], G_FROM)
+        quantize_own(A - 2)
         relu_in_place(A, 0, P)
-        quantize_w3(B - 1)
-        quantize_step(A - 2)
+        quantize_w3(B * G - 2, B * G)
+        quantize_gbuf(A - 2)
         quantize_z(Z, whole)
         interleave_gpsimd(A - 1)
         output(A - 3, all_tiles)
         store(A - 3, all_tiles)
         hidden(A, 1, all_slots, whole)
         relu(A, 1, whole)
+        interleave_tensor(A, P, P + Q, parts=(0,))
         output(A - 2, all_tiles, "zbank")
         store(A - 2, all_tiles)
-        for i, tag in enumerate(("zbank", "xbank", "zbank", "zbank")):
-            hidden_tile(Z, 0, i, tag)
-            add_bias(Z, 0, i)
-            if i == 1:
-                interleave_tensor(A, P, P + Q)
-                copy_mixed(A, P, P + Q)
-        hidden(Z, 1, all_slots, whole)
+        hidden_tile(Z, 0, 0, "zbank")
+        add_bias(Z, 0, 0)
+        hidden_tile(Z, 0, 1)
+        add_bias(Z, 0, 1)
+        interleave_tensor(A, P, P + Q, parts=(1,))
+        copy_mixed(A, P, P + Q)
+        hidden_tile(Z, 0, 2, "zbank")
+        add_bias(Z, 0, 2)
+        hidden(Z, 1, (0, 1), whole)
+        hidden_tile(Z, 0, 3, "zbank")
+        add_bias(Z, 0, 3)
+        hidden(Z, 1, (2, 3), whole)
+        interleave_scalar(A, P + Q, ROWS)
         interleave_tensor(A, ROWS, ROWS + Q)
-        relu(Z, 1, whole, (0, 1))
-        copy_mixed(A, ROWS, ROWS + Q)
         interleave_tensor(A, ROWS + Q, COLS, "xbank")
-        relu(Z, 1, whole, (2, 3))
+        relu(Z, 1, whole)
+        copy_mixed(A, ROWS, ROWS + Q)
         copy_mixed(A, ROWS + Q, COLS)
-        interleave_vector(A, P + Q, ROWS)
-        relu_in_place(Z, 0, ROWS)
         quantize_step(A - 1)
         output(A - 1, all_tiles, "zbank")
-        quantize_h(Z, 0, ROWS)
-        interleave_tensor(Z, ROWS, ROWS + Q)
-        copy_mixed(Z, ROWS, ROWS + Q)
+        relu_in_place(Z, 0, ROWS)
         quantize_h(A, 0, ROWS)
-        interleave_vector(Z, ROWS + Q, COLS)
-        quantize_h(A, ROWS, COLS)
+        quantize_h(Z, 0, ROWS)
+        interleave_vector(Z, ROWS + Q + P, COLS)
         store(A - 1, all_tiles)
+        quantize_h(A, ROWS, COLS)
+        interleave_tensor(Z, ROWS, ROWS + Q)
+        interleave_scalar(Z, ROWS + Q, ROWS + Q + P)
+        copy_mixed(Z, ROWS, ROWS + Q)
         output(A, all_tiles, "zbank")
         quantize_h(Z, ROWS + Q, COLS)
-        quantize_h(Z, ROWS, ROWS + Q)
         output(Z, range(2, 4), "zbank")
+        quantize_h(Z, ROWS, ROWS + Q)
         store(A, all_tiles)
         output(Z, range(0, 2))
         store(Z, range(2, 4))

@@ -27,10 +27,11 @@ LAST = STEPS - 1
 
 COLS = G * ROWS
 LEAD = 5
-ZBUFS = 6
-G_FROM = 448
+ZBUFS = 7
+G_FROM = 384
 G_STEPS = range(0, STEPS - 2)
-NT = 176
+JOINED = range(2, STEPS - 2)
+NT = 256
 
 
 def tile_mlpmodelpredictor_pb_t_w8_kernel(
@@ -57,7 +58,8 @@ def tile_mlpmodelpredictor_pb_t_w8_kernel(
         w3_codes = keep.tile([P, B * G * O], U32, name="w3_codes", align_bytes=64)
         w3_exps = keep.tile([P, B * G * O], U8, name="w3_exps", align_bytes=64)
 
-        gbuf = keep.tile([P, (COLS - G_FROM) * PACK], BF16, name="gbuf", align_bytes=64)
+        hbuf = keep.tile([P, (COLS + G_FROM) * PACK], BF16, name="hbuf", align_bytes=64)
+        gbuf = hbuf[:, G_FROM * PACK : COLS * PACK]
         zbuf = []
         for i in range(ZBUFS):
             zbuf_tile = keep.tile([P, ROWS * PACK], BF16, name="zbuf%d" % i, align_bytes=64)
@@ -130,8 +132,10 @@ def tile_mlpmodelpredictor_pb_t_w8_kernel(
         )
         for s in range(7, STEPS):
             load_z(s)
-        for c in range(10, B * G, G):
-            load_w3(c, c + G)
+        load_w3(10, 11)
+        load_w3(11, 12)
+        load_w3(12, 15)
+        load_w3(15, 16)
 
         z_banks, z_codes, z_exps = {}, {}, {}
         h_banks, h_planes, h_inter, h_codes, h_exps = {}, {}, {}, {}, {}
@@ -183,8 +187,8 @@ def tile_mlpmodelpredictor_pb_t_w8_kernel(
 
         def quantize_z(s, cols):
             if cols.start == 0:
-                codes = work.tile([P, ROWS], U32, name="zcodes", bufs=3, align_bytes=64)
-                exps = work.tile([P, ROWS], U8, name="zexp", bufs=3, align_bytes=64)
+                codes = work.tile([P, ROWS], U32, name="zcodes", bufs=4, align_bytes=64)
+                exps = work.tile([P, ROWS], U8, name="zexp", bufs=4, align_bytes=64)
                 z_codes[s], z_exps[s] = codes, exps
             nc.vector.quantize_mx(
                 out=z_codes[s][:, cols].bitcast(FP8X4),
@@ -219,13 +223,16 @@ def tile_mlpmodelpredictor_pb_t_w8_kernel(
 
         def inter_tile(s):
             if s not in h_inter:
-                tile = work.tile([P, COLS * PACK], BF16, name="hinter", bufs=4, align_bytes=64)
+                tile = work.tile([P, COLS * PACK], BF16, name="hinter", bufs=2, align_bytes=64)
                 h_inter[s] = tile
             return h_inter[s]
 
         def interleaved(s, lo, hi):
             if s in G_STEPS and lo >= g_from(s):
                 return gbuf[:, (lo - g_from(s)) * PACK : (hi - g_from(s)) * PACK]
+            if s in JOINED:
+                base = s % 2 * COLS
+                return hbuf[:, (base + lo) * PACK : (base + hi) * PACK]
             return inter_tile(s)[:, lo * PACK : hi * PACK]
 
         def hidden_tile(s, g, i, tag="xbank"):
@@ -307,30 +314,30 @@ def tile_mlpmodelpredictor_pb_t_w8_kernel(
                 in_=mixed[s, lo][:, 0 : hi - lo, :].rearrange("p n t -> p (n t)").bitcast(F32),
             )
 
+        def code_tiles(s):
+            codes = work.tile([P, COLS], U32, name="hcodes", bufs=3, align_bytes=64)
+            exps = work.tile([P, COLS], U8, name="hexp", bufs=3, align_bytes=64)
+            h_codes[s], h_exps[s] = codes, exps
+
         def quantize_h(s, lo, hi):
             if s not in h_codes:
-                codes = work.tile([P, COLS], U32, name="hcodes", bufs=3, align_bytes=64)
-                exps = work.tile([P, COLS], U8, name="hexp", bufs=3, align_bytes=64)
-                h_codes[s], h_exps[s] = codes, exps
+                code_tiles(s)
             nc.vector.quantize_mx(
                 out=h_codes[s][:, lo:hi].bitcast(FP8X4),
                 scales=h_exps[s][:, lo:hi],
                 in_=interleaved(s, lo, hi),
             )
 
-        def quantize_own(s):
-            cuts = [0, ROWS] if s == 0 else [0, 3 * P, G_FROM]
-            for lo, hi in zip(cuts, cuts[1:]):
-                quantize_h(s, lo, hi)
-
-        def quantize_gbuf(s):
-            cuts = [ROWS, COLS] if s == 0 else [G_FROM, ROWS, COLS]
-            for lo, hi in zip(cuts, cuts[1:]):
-                quantize_h(s, lo, hi)
+        def turned(s):
+            return G_FROM if s in JOINED and s % 2 == 1 else 0
 
         def quantize_step(s):
-            quantize_own(s)
-            quantize_gbuf(s)
+            code_tiles(s)
+            nc.vector.quantize_mx(
+                out=h_codes[s][:].bitcast(FP8X4),
+                scales=h_exps[s][:],
+                in_=hbuf[:, turned(s) * PACK : (turned(s) + COLS) * PACK],
+            )
 
         def interleave_w3_gpsimd(lo, hi):
             w3_inter[lo] = gbuf
@@ -342,7 +349,7 @@ def tile_mlpmodelpredictor_pb_t_w8_kernel(
             )
 
         def interleave_w3_scalar(lo, hi):
-            tile = work.tile([P, G * O * PACK], BF16, name="w3inter", bufs=2, align_bytes=64)
+            tile = work.tile([P, 3 * O * PACK], BF16, name="w3inter", bufs=2, align_bytes=64)
             w3_inter[lo] = tile
             nc.scalar.copy(
                 out=tile[:, 0 : (hi - lo) * O * PACK].rearrange(
@@ -370,7 +377,8 @@ def tile_mlpmodelpredictor_pb_t_w8_kernel(
             out_banks[s, tiles.start] = bank
             for i in tiles:
                 for g in range(G):
-                    rows = slice(g * ROWS + i * P, g * ROWS + (i + 1) * P)
+                    at = (g * ROWS + i * P - turned(s)) % COLS
+                    rows = slice(at, at + P)
                     chans = slice((b * G + g) * O, (b * G + g + 1) * O)
                     nc.tensor.matmul_mx(
                         out=bank[:, i, :],
@@ -443,108 +451,141 @@ def tile_mlpmodelpredictor_pb_t_w8_kernel(
         scale_z(1, 1)
 
         def v_tiles(s):
-            return 2 if s <= 3 else 1
+            return 2 if s in (1, 2, 3) or (s % 2 == 0 and s >= 4) else 0
 
         def t_range(s):
-            return (0, 2 * P) if s == 0 else (v_tiles(s) * P, G_FROM if s <= 3 else P + NT)
+            return (2 * P, G_FROM) if v_tiles(s) else (0, NT)
 
+        def widen_halves(lo, hi):
+            for j in range(lo, min(hi, 2 * STEPS)):
+                if j % 2 == 0 and j + 1 < hi:
+                    widen_z(j // 2, on_s, all_tiles)
+                elif j % 2 == 0 or j == lo:
+                    widen_z(j // 2, on_s, range(j % 2 * 2, j % 2 * 2 + 2))
+
+        def vector_tile(s, i):
+            hidden_tile(s, 0, i)
+            add_bias(s, 0, i)
+
+        def tile_of_turn(s):
+            return (3, s - 2) if s < 4 else (s - s % 2, s % 2)
+
+        w3_on_s = {1: (7, 8), 2: (8, 9), 3: (9, 10), 10: (10, 11), 11: (11, 12), 12: (12, 15), 13: (15, 16)}
         for s in range(STEPS - 2):
             if s >= 1:
-                relu(s, 0, slice(v_tiles(s) * P, ROWS))
-            if s + LEAD < STEPS:
-                widen_z(s + LEAD, on_s, all_tiles)
+                relu(s, 0, slice(v_tiles(s) * P, ROWS), (0, 1))
+                copy_mixed(s - 1, *t_range(s - 1))
+                relu(s, 0, slice(v_tiles(s) * P, ROWS), (2, 3))
+            if s < 4:
+                widen_halves(2 * (s + LEAD), 2 * (s + LEAD + 1))
+            elif s % 2 == 0:
+                widen_halves(2 * (s + LEAD), 2 * (s + LEAD) + 3)
             else:
-                interleave_w3_scalar(2 * s - 12, 2 * s - 10)
-            if 1 <= s <= 3:
-                interleave_w3_scalar(s + 6, s + 7)
+                widen_halves(2 * (s + LEAD) + 1, 2 * (s + LEAD) + 2)
+            if s in w3_on_s:
+                interleave_w3_scalar(*w3_on_s[s])
             if s == 1:
-                interleave_vector(0, 2 * P, ROWS)
-            elif s >= 5:
-                interleave_vector(s - 1, t_range(s - 1)[1], G_FROM)
-            if 2 <= s <= 4:
-                quantize_w3(s + 5, s + 6)
-            if s >= 2:
-                quantize_own(s - 2)
-            if s >= 1:
-                relu_in_place(s, 0, v_tiles(s) * P)
-            if s >= 12:
-                quantize_w3(2 * s - 14, 2 * s - 12)
+                interleave_vector(0, NT, ROWS)
+            if s == 2:
+                quantize_h(0, 0, ROWS)
+            if s in (1, 2):
+                relu_in_place(s, 0, 2 * P)
+            elif s >= 3:
+                step, i = tile_of_turn(s - 1)
+                relu_in_place(step, i * P, (i + 1) * P)
+            if s >= 2 and not v_tiles(s - 1):
+                interleave_vector(s - 1, NT, G_FROM)
+            if s - 1 in w3_on_s:
+                quantize_w3(*w3_on_s[s - 1])
             if s == 0:
                 quantize_w3(0, 3)
             elif s == 1:
                 quantize_w3(3, 7)
+            elif s == 2:
+                quantize_h(0, ROWS, COLS)
+            elif s == 3:
+                quantize_h(1, 0, G_FROM)
+                quantize_h(1, G_FROM, ROWS)
+                quantize_h(1, ROWS, COLS)
             else:
-                quantize_gbuf(s - 2)
+                quantize_step(s - 2)
             quantize_z(s + 1, whole)
             if s == 0:
                 interleave_w3_gpsimd(3, 7)
             else:
                 interleave_gpsimd(s - 1)
             if s >= 3:
-                output(s - 3, all_tiles)
-                store(s - 3, all_tiles)
+                vector_tile(*tile_of_turn(s))
             hidden(s, 1, (0, 1), whole)
             transpose_z(s + 2)
             hidden(s, 1, (2, 3), whole)
             scale_z(s + 2, 0)
-            if v_tiles(s + 1) == 2:
-                hidden_tile(s + 1, 0, 1)
-                add_bias(s + 1, 0, 1)
+            if s < 2:
+                vector_tile(s + 1, 1)
+            elif s == 2:
+                vector_tile(3, 0)
             scale_z(s + 2, 1)
             relu(s, 1, whole)
+            if s >= 3:
+                output(s - 2, all_tiles)
+                store(s - 2, all_tiles)
+            hidden(s + 1, 0, (0, 1), slice(v_tiles(s + 1) * P, ROWS))
             interleave_tensor(s, *t_range(s))
-            copy_mixed(s, *t_range(s))
-            hidden_tile(s + 1, 0, 0)
-            add_bias(s + 1, 0, 0)
-            hidden(s + 1, 0, all_slots, slice(v_tiles(s + 1) * P, ROWS))
+            if s < 2:
+                vector_tile(s + 1, 0)
+            elif s == 2:
+                output(0, all_tiles)
+                store(0, all_tiles)
+            hidden(s + 1, 0, (2, 3), slice(v_tiles(s + 1) * P, ROWS))
 
         A, Z = LAST - 1, LAST
         Q = ROWS // 2
-        relu(A, 0, rest)
-        interleave_vector(A - 1, t_range(A - 1)[1], G_FROM)
-        quantize_own(A - 2)
-        relu_in_place(A, 0, P)
-        quantize_w3(B * G - 2, B * G)
-        quantize_gbuf(A - 2)
+        last_tile = slice(3 * P, ROWS)
+        relu(A, 0, right, (0, 1))
+        copy_mixed(A - 1, *t_range(A - 1))
+        relu(A, 0, right, (2, 3))
+        relu_in_place(A - 2, P, 2 * P)
+        interleave_vector(A - 1, NT, G_FROM)
+        quantize_w3(*w3_on_s[A - 1])
+        quantize_step(A - 2)
         quantize_z(Z, whole)
         interleave_gpsimd(A - 1)
-        output(A - 3, all_tiles)
-        store(A - 3, all_tiles)
+        hidden_tile(A, 0, 0)
+        hidden_tile(A, 0, 1, "zbank")
+        add_bias(A, 0, 0)
+        add_bias(A, 0, 1)
         hidden(A, 1, all_slots, whole)
-        relu(A, 1, whole)
-        interleave_tensor(A, P, P + Q, parts=(0,))
         output(A - 2, all_tiles, "zbank")
         store(A - 2, all_tiles)
-        hidden_tile(Z, 0, 0, "zbank")
-        add_bias(Z, 0, 0)
-        hidden_tile(Z, 0, 1)
-        add_bias(Z, 0, 1)
-        interleave_tensor(A, P, P + Q, parts=(1,))
-        copy_mixed(A, P, P + Q)
-        hidden_tile(Z, 0, 2, "zbank")
-        add_bias(Z, 0, 2)
-        hidden(Z, 1, (0, 1), whole)
-        hidden_tile(Z, 0, 3, "zbank")
-        add_bias(Z, 0, 3)
-        hidden(Z, 1, (2, 3), whole)
-        interleave_scalar(A, P + Q, ROWS)
-        interleave_tensor(A, ROWS, ROWS + Q)
-        interleave_tensor(A, ROWS + Q, COLS, "xbank")
-        relu(Z, 1, whole)
-        copy_mixed(A, ROWS, ROWS + Q)
-        copy_mixed(A, ROWS + Q, COLS)
+        relu(A, 1, whole)
+        interleave_scalar(A, ROWS, 5 * P)
+        interleave_tensor(A, Q, ROWS, parts=(0,))
+        for i, tag in enumerate(("xbank", "zbank", "zbank")):
+            hidden_tile(Z, 0, i, tag)
+            add_bias(Z, 0, i)
+            if i == 1:
+                interleave_tensor(A, Q, ROWS, parts=(1,))
+        copy_mixed(A, Q, ROWS)
+        hidden(Z, 0, all_slots, last_tile)
+        relu(Z, 0, last_tile)
+        hidden(Z, 1, all_slots, whole)
+        interleave_tensor(A, 5 * P, 7 * P)
+        relu(Z, 1, whole, (0, 1))
+        copy_mixed(A, 5 * P, 7 * P)
+        relu(Z, 1, whole, (2, 3))
+        interleave_scalar(Z, 3 * P, ROWS)
+        relu_in_place(A, 0, Q)
         quantize_step(A - 1)
         output(A - 1, all_tiles, "zbank")
-        relu_in_place(Z, 0, ROWS)
-        quantize_h(A, 0, ROWS)
-        quantize_h(Z, 0, ROWS)
-        interleave_vector(Z, ROWS + Q + P, COLS)
+        relu_in_place(Z, 0, 3 * P)
+        interleave_vector(A, 7 * P, COLS)
         store(A - 1, all_tiles)
-        quantize_h(A, ROWS, COLS)
+        quantize_h(A, 0, COLS)
         interleave_tensor(Z, ROWS, ROWS + Q)
-        interleave_scalar(Z, ROWS + Q, ROWS + Q + P)
         copy_mixed(Z, ROWS, ROWS + Q)
         output(A, all_tiles, "zbank")
+        interleave_vector(Z, ROWS + Q, COLS)
+        quantize_h(Z, 0, ROWS)
         quantize_h(Z, ROWS + Q, COLS)
         output(Z, range(2, 4), "zbank")
         quantize_h(Z, ROWS, ROWS + Q)

@@ -107,6 +107,7 @@ def tile_mlpmodelpredictor_pb_t_w8_kernel(
         )
         w1_words = sw1_words[0].rearrange("p n t -> p (n t)").bitcast(I32)
         load_z(1)
+        load_z(2)
         nc.sync.dma_start(out=w1_raw[:, 0, :], in_=w1_words[:, 0 : H // G])
         for q in range(4):
             nc.sync.dma_start(
@@ -116,21 +117,24 @@ def tile_mlpmodelpredictor_pb_t_w8_kernel(
         nc.sync.dma_start(
             out=b2_rows[0 : B * G, :], in_=b2.rearrange("b (g n) -> (b g) n", g=G)
         )
-        load_z(2)
         load_z(3)
         nc.sync.dma_start(out=w1_raw[:, 1, :], in_=w1_words[:, H // G : H])
-        load_z(4)
         load_w3(0, 3)
+        load_z(4)
         load_z(5)
         load_w3(3, 7)
         load_z(6)
-        for c in range(7, 10):
-            load_w3(c, c + 1)
+        load_w3(7, 8)
+        load_z(7)
+        load_w3(8, 9)
+        load_w3(9, 10)
+        for s in range(8, 11):
+            load_z(s)
         nc.sync.dma_start(
             out=b3_rows[:].rearrange("p b o -> p (b o)"),
             in_=b3.rearrange("b o -> (b o)").partition_broadcast(P),
         )
-        for s in range(7, STEPS):
+        for s in range(11, STEPS):
             load_z(s)
         load_w3(10, 11)
         load_w3(11, 12)
@@ -159,7 +163,7 @@ def tile_mlpmodelpredictor_pb_t_w8_kernel(
         def transpose_z(s, halves=(0, 1)):
             words = zbuf_of(s).bitcast(F32)
             for half in halves:
-                bank = psum.tile([P, 2, 2, P], F32, name="zbank", bufs=2)
+                bank = psum.tile([P, 2, 2, P], F32, name="rbank", bufs=4)
                 z_banks[s, half] = bank
                 for i in range(2):
                     base = R // 2 * (2 * half + i)
@@ -207,10 +211,10 @@ def tile_mlpmodelpredictor_pb_t_w8_kernel(
                 stop=True,
             )
 
-        def hidden(s, g, slots, cols, tag="hbank"):
+        def hidden(s, g, slots, cols):
             for t in slots:
                 if (s, g, t) not in h_banks:
-                    bank = psum.tile([P, ROWS], F32, name=tag, bufs=PACK if tag == "hbank" else 2)
+                    bank = psum.tile([P, ROWS], F32, name="hbank", bufs=PACK)
                     h_banks[s, g, t] = bank
                 lo = cols.start
                 for width in (ROWS, ROWS // 2, ROWS // 4):
@@ -235,8 +239,8 @@ def tile_mlpmodelpredictor_pb_t_w8_kernel(
                 return hbuf[:, (base + lo) * PACK : (base + hi) * PACK]
             return inter_tile(s)[:, lo * PACK : hi * PACK]
 
-        def hidden_tile(s, g, i, tag="xbank"):
-            bank = psum.tile([P, PACK, P], F32, name=tag, bufs=1 if tag == "xbank" else 2)
+        def hidden_tile(s, g, i):
+            bank = psum.tile([P, PACK, P], F32, name="rbank", bufs=4)
             v_banks[s, g, i] = bank
             for t in range(PACK):
                 product(bank[:, t, :], s, g, t, i * P, (i + 1) * P)
@@ -291,9 +295,9 @@ def tile_mlpmodelpredictor_pb_t_w8_kernel(
                 in_=h_planes[s][:, :, g_from(s) : COLS].rearrange("p t n -> p n t"),
             )
 
-        def interleave_tensor(s, lo, hi, tag="ibank", parts=(0, 1)):
+        def interleave_tensor(s, lo, hi, parts=(0, 1)):
             if 0 in parts:
-                bank = psum.tile([P, ROWS // 2, PACK], BF16, name=tag, bufs=1)
+                bank = psum.tile([P, ROWS // 2, PACK], BF16, name="rbank", bufs=4)
                 mixed[s, lo] = bank
             bank = mixed[s, lo]
             n = (hi - lo) // 2
@@ -353,9 +357,19 @@ def tile_mlpmodelpredictor_pb_t_w8_kernel(
             w3_inter[lo] = tile
             nc.scalar.copy(
                 out=tile[:, 0 : (hi - lo) * O * PACK].rearrange(
-                    "p (c j i t) -> p c j t i", c=hi - lo, i=4, t=PACK
+                    "p (c o t) -> p c o t", o=O, t=PACK
                 ),
-                in_=w3_raw[lo][:].rearrange("p c t (j i) -> p c j t i", i=4),
+                in_=w3_raw[lo][:].rearrange("p c t o -> p c o t"),
+            )
+
+        def interleave_w3_vector(lo, hi):
+            tile = work.tile([P, 3 * O * PACK], BF16, name="w3inter", bufs=2, align_bytes=64)
+            w3_inter[lo] = tile
+            nc.vector.tensor_copy(
+                out=tile[:, 0 : (hi - lo) * O * PACK].rearrange(
+                    "p (c j i t) -> p c j t i", c=hi - lo, i=2, t=PACK
+                ),
+                in_=w3_raw[lo][:].rearrange("p c t (j i) -> p c j t i", i=2),
             )
 
         def quantize_w3(lo, hi):
@@ -367,13 +381,13 @@ def tile_mlpmodelpredictor_pb_t_w8_kernel(
 
         def interleave_scalar(s, lo, hi):
             nc.scalar.copy(
-                out=interleaved(s, lo, hi).rearrange("p (c i t) -> p c t i", i=4, t=PACK),
-                in_=h_planes[s][:, :, lo:hi].rearrange("p t (c i) -> p c t i", i=4),
+                out=interleaved(s, lo, hi).rearrange("p (n t) -> p n t", t=PACK),
+                in_=h_planes[s][:, :, lo:hi].rearrange("p t n -> p n t"),
             )
 
-        def output(s, tiles, tag="xbank"):
+        def output(s, tiles):
             b = s // HALVES
-            bank = psum.tile([P, SUB, O], F32, name=tag, bufs=2 if tag == "zbank" else 1)
+            bank = psum.tile([P, SUB, O], F32, name="rbank", bufs=4)
             out_banks[s, tiles.start] = bank
             for i in tiles:
                 for g in range(G):
@@ -418,7 +432,7 @@ def tile_mlpmodelpredictor_pb_t_w8_kernel(
             widen_z(0, copy, range(i, i + 1))
         widen_z(1, on_s, all_tiles)
         transpose_z(0)
-        b2_bank = psum.tile([P, SUB, O], F32, name="xbank", bufs=1)
+        b2_bank = psum.tile([P, SUB, O], F32, name="rbank", bufs=4)
         b2_words = b2_rows[:].bitcast(F32)
         for u in range(2):
             nc.tensor.transpose(b2_bank[:, u, :], b2_words[:, u::2], ident_f[:])
@@ -431,14 +445,14 @@ def tile_mlpmodelpredictor_pb_t_w8_kernel(
             in_=b2_bank[:, 0:2, 0 : B * G].rearrange("p u c -> p c u"),
         )
         widen_z(3, on_s, all_tiles)
-        widen_z(4, on_s, all_tiles)
-        permute_w1_codes(0)
         scale_z(0, 0)
-        permute_w1_scales(0)
+        permute_w1_codes(0)
         quantize_z(0, left)
+        permute_w1_scales(0)
         transpose_z(1, (0,))
         hidden(0, 0, all_slots, left)
         relu(0, 0, left)
+        widen_z(4, on_s, all_tiles)
         scale_z(0, 1)
         permute_w1_codes(1)
         quantize_z(0, right)
@@ -470,7 +484,8 @@ def tile_mlpmodelpredictor_pb_t_w8_kernel(
         def tile_of_turn(s):
             return (3, s - 2) if s < 4 else (s - s % 2, s % 2)
 
-        w3_on_s = {1: (7, 8), 2: (8, 9), 3: (9, 10), 10: (10, 11), 11: (11, 12), 12: (12, 15), 13: (15, 16)}
+        w3_on_v = {1: (7, 8)}
+        w3_on_s = {2: (8, 9), 3: (9, 10), 10: (10, 11), 11: (11, 12), 12: (12, 15), 13: (15, 16)}
         for s in range(STEPS - 2):
             if s >= 1:
                 relu(s, 0, slice(v_tiles(s) * P, ROWS), (0, 1))
@@ -497,6 +512,10 @@ def tile_mlpmodelpredictor_pb_t_w8_kernel(
                 interleave_vector(s - 1, NT, G_FROM)
             if s - 1 in w3_on_s:
                 quantize_w3(*w3_on_s[s - 1])
+            if s - 1 in w3_on_v:
+                quantize_w3(*w3_on_v[s - 1])
+            if s in w3_on_v:
+                interleave_w3_vector(*w3_on_v[s])
             if s == 0:
                 quantize_w3(0, 3)
             elif s == 1:
@@ -551,43 +570,41 @@ def tile_mlpmodelpredictor_pb_t_w8_kernel(
         quantize_z(Z, whole)
         interleave_gpsimd(A - 1)
         hidden_tile(A, 0, 0)
-        hidden_tile(A, 0, 1, "zbank")
+        hidden_tile(A, 0, 1)
         add_bias(A, 0, 0)
         add_bias(A, 0, 1)
         hidden(A, 1, all_slots, whole)
-        output(A - 2, all_tiles, "zbank")
+        output(A - 2, all_tiles)
         store(A - 2, all_tiles)
         relu(A, 1, whole)
-        interleave_scalar(A, ROWS, 5 * P)
-        interleave_tensor(A, Q, ROWS, parts=(0,))
-        for i, tag in enumerate(("xbank", "zbank", "zbank")):
-            hidden_tile(Z, 0, i, tag)
+        for i in range(3):
+            hidden_tile(Z, 0, i)
             add_bias(Z, 0, i)
-            if i == 1:
-                interleave_tensor(A, Q, ROWS, parts=(1,))
-        copy_mixed(A, Q, ROWS)
         hidden(Z, 0, all_slots, last_tile)
         relu(Z, 0, last_tile)
+        interleave_scalar(A, ROWS, 5 * P)
+        interleave_tensor(A, Q, ROWS, parts=(0,))
         hidden(Z, 1, all_slots, whole)
+        interleave_tensor(A, Q, ROWS, parts=(1,))
         interleave_tensor(A, 5 * P, 7 * P)
-        relu(Z, 1, whole, (0, 1))
+        relu(Z, 1, whole)
+        copy_mixed(A, Q, ROWS)
         copy_mixed(A, 5 * P, 7 * P)
-        relu(Z, 1, whole, (2, 3))
         interleave_scalar(Z, 3 * P, ROWS)
         relu_in_place(A, 0, Q)
         quantize_step(A - 1)
-        output(A - 1, all_tiles, "zbank")
+        output(A - 1, all_tiles)
         relu_in_place(Z, 0, 3 * P)
         interleave_vector(A, 7 * P, COLS)
-        store(A - 1, all_tiles)
-        quantize_h(A, 0, COLS)
         interleave_tensor(Z, ROWS, ROWS + Q)
         copy_mixed(Z, ROWS, ROWS + Q)
-        output(A, all_tiles, "zbank")
         interleave_vector(Z, ROWS + Q, COLS)
+        store(A - 1, all_tiles)
+        quantize_h(A, 0, COLS)
+        output(A, all_tiles)
         quantize_h(Z, 0, ROWS)
         quantize_h(Z, ROWS + Q, COLS)
-        output(Z, range(2, 4), "zbank")
+        output(Z, range(2, 4))
         quantize_h(Z, ROWS, ROWS + Q)
         store(A, all_tiles)
         output(Z, range(0, 2))

@@ -31,6 +31,9 @@ ZBUFS = 7
 G_FROM = 384
 G_STEPS = range(0, STEPS - 2)
 JOINED = range(2, STEPS - 2)
+W3G = 8
+G0 = 384
+W3S = {2: (8, 9), 3: (9, 10), 10: (10, 11), 11: (11, 12), 12: (12, 15), 13: (15, 16)}
 NT = 256
 
 
@@ -101,33 +104,45 @@ def tile_mlpmodelpredictor_pb_t_w8_kernel(
         nc.vector.memset(b2_rows[:], 0.0)
         make_identity(nc, ident_f[:])
         make_identity(nc, ident_b[:])
-        load_z(0, SUB // 2)
-        nc.scalar.dma_start(
-            out=kscale[:], in_=z2_scale.rearrange("a c (p t) -> p (a c t)", t=PACK)
-        )
         w1_words = sw1_words[0].rearrange("p n t -> p (n t)").bitcast(I32)
-        load_z(1)
-        load_z(2)
-        nc.sync.dma_start(out=w1_raw[:, 0, :], in_=w1_words[:, 0 : H // G])
-        for q in range(4):
-            nc.sync.dma_start(
-                out=w1s_raw[32 * q : 32 * q + 4, :].bitcast(I32),
-                in_=sw1_scales[0, 4 * q : 4 * q + 4, :].bitcast(I32),
+
+        def load_kscale():
+            nc.scalar.dma_start(
+                out=kscale[:], in_=z2_scale.rearrange("a c (p t) -> p (a c t)", t=PACK)
             )
-        nc.sync.dma_start(
-            out=b2_rows[0 : B * G, :], in_=b2.rearrange("b (g n) -> (b g) n", g=G)
-        )
+
+        def load_w1(g):
+            nc.sync.dma_start(out=w1_raw[:, g, :], in_=w1_words[:, g * H // G : (g + 1) * H // G])
+
+        def load_w1s():
+            for q in range(4):
+                nc.sync.dma_start(
+                    out=w1s_raw[32 * q : 32 * q + 4, :].bitcast(I32),
+                    in_=sw1_scales[0, 4 * q : 4 * q + 4, :].bitcast(I32),
+                )
+
+        def load_b2():
+            nc.sync.dma_start(
+                out=b2_rows[0 : B * G, :], in_=b2.rearrange("b (g n) -> (b g) n", g=G)
+            )
+
+        load_z(0, SUB // 2)
+        load_kscale()
+        load_w1(0)
+        load_z(1)
+        load_b2()
+        load_z(2)
+        load_w1s()
         load_z(3)
-        nc.sync.dma_start(out=w1_raw[:, 1, :], in_=w1_words[:, H // G : H])
+        load_w1(1)
         load_w3(0, 3)
         load_z(4)
         load_z(5)
-        load_w3(3, 7)
+        load_w3(3, W3G)
         load_z(6)
-        load_w3(7, 8)
+        for c in range(W3G, 10):
+            load_w3(c, c + 1)
         load_z(7)
-        load_w3(8, 9)
-        load_w3(9, 10)
         for s in range(8, 11):
             load_z(s)
         nc.sync.dma_start(
@@ -136,10 +151,9 @@ def tile_mlpmodelpredictor_pb_t_w8_kernel(
         )
         for s in range(11, STEPS):
             load_z(s)
-        load_w3(10, 11)
-        load_w3(11, 12)
-        load_w3(12, 15)
-        load_w3(15, 16)
+        for turn in sorted(W3S):
+            if W3S[turn][0] >= 10:
+                load_w3(*W3S[turn])
 
         z_banks, z_codes, z_exps = {}, {}, {}
         h_banks, h_planes, h_inter, h_codes, h_exps = {}, {}, {}, {}, {}
@@ -189,6 +203,31 @@ def tile_mlpmodelpredictor_pb_t_w8_kernel(
                 op=ALU.mult,
             )
 
+        def transpose_tile(s, i):
+            words = zbuf_of(s).bitcast(F32)
+            bank = psum.tile([P, 2, P], F32, name="rbank", bufs=4)
+            z_banks[s, i, "t"] = bank
+            for u in range(2):
+                nc.tensor.transpose(
+                    bank[:, u, :], words[:, R // 2 * i + u : R // 2 * (i + 1) : 2], ident_f[:]
+                )
+
+        def scale_tile(s, i):
+            nc.vector.tensor_tensor(
+                out=zbuf_of(s)[:, i * P * PACK : (i + 1) * P * PACK].rearrange(
+                    "p (n u e) -> p n u e", u=2, e=2
+                ),
+                in0=z_banks[s, i, "t"][:]
+                .rearrange("p u r -> p (u r)")
+                .bitcast(BF16)
+                .rearrange("p (u n e) -> p n u e", u=2, e=2),
+                in1=kscale[:]
+                .rearrange("p (u e) -> p u e", e=2)
+                .unsqueeze(1)
+                .to_broadcast([P, P, 2, 2]),
+                op=ALU.mult,
+            )
+
         def quantize_z(s, cols):
             if cols.start == 0:
                 codes = work.tile([P, ROWS], U32, name="zcodes", bufs=4, align_bytes=64)
@@ -223,7 +262,7 @@ def tile_mlpmodelpredictor_pb_t_w8_kernel(
                         lo += width
 
         def g_from(s):
-            return ROWS if s == 0 else G_FROM
+            return G0 if s == 0 else G_FROM
 
         def inter_tile(s):
             if s not in h_inter:
@@ -268,7 +307,7 @@ def tile_mlpmodelpredictor_pb_t_w8_kernel(
 
         def relu(s, g, cols, slots=range(PACK)):
             if s not in h_planes:
-                planes = work.tile([P, PACK, COLS], BF16, name="hplanar", bufs=3)
+                planes = work.tile([P, PACK, COLS], BF16, name="hplanar", bufs=4)
                 h_planes[s] = planes
             for t in slots:
                 nc.scalar.activation(
@@ -289,15 +328,16 @@ def tile_mlpmodelpredictor_pb_t_w8_kernel(
                 out=out, in0=in_, scalar1=1.0, scalar2=0.0, op0=ALU.mult, op1=ALU.add
             )
 
-        def interleave_gpsimd(s):
+        def interleave_gpsimd(s, lo=None):
+            lo = g_from(s) if lo is None else lo
             copy_gpsimd(
-                out=interleaved(s, g_from(s), COLS).rearrange("p (n t) -> p n t", t=PACK),
-                in_=h_planes[s][:, :, g_from(s) : COLS].rearrange("p t n -> p n t"),
+                out=interleaved(s, lo, COLS).rearrange("p (n t) -> p n t", t=PACK),
+                in_=h_planes[s][:, :, lo:COLS].rearrange("p t n -> p n t"),
             )
 
-        def interleave_tensor(s, lo, hi, parts=(0, 1)):
+        def interleave_tensor(s, lo, hi, parts=(0, 1), tag="rbank"):
             if 0 in parts:
-                bank = psum.tile([P, ROWS // 2, PACK], BF16, name="rbank", bufs=4)
+                bank = psum.tile([P, ROWS // 2, PACK], BF16, name=tag, bufs=4)
                 mixed[s, lo] = bank
             bank = mixed[s, lo]
             n = (hi - lo) // 2
@@ -344,9 +384,10 @@ def tile_mlpmodelpredictor_pb_t_w8_kernel(
             )
 
         def interleave_w3_gpsimd(lo, hi):
-            w3_inter[lo] = gbuf
+            dst = hbuf[:, COLS * PACK - max(hi - lo, 5) * O * PACK : COLS * PACK]
+            w3_inter[lo] = dst
             copy_gpsimd(
-                out=gbuf[:, 0 : (hi - lo) * O * PACK].rearrange(
+                out=dst[:, 0 : (hi - lo) * O * PACK].rearrange(
                     "p (c o t) -> p c o t", o=O, t=PACK
                 ),
                 in_=w3_raw[lo][:].rearrange("p c t o -> p c o t"),
@@ -372,11 +413,12 @@ def tile_mlpmodelpredictor_pb_t_w8_kernel(
                 in_=w3_raw[lo][:].rearrange("p c t (j i) -> p c j t i", i=2),
             )
 
-        def quantize_w3(lo, hi):
+        def quantize_w3(lo, hi, first=None):
+            first = lo if first is None else first
             nc.vector.quantize_mx(
                 out=w3_codes[:, lo * O : hi * O].bitcast(FP8X4),
                 scales=w3_exps[:, lo * O : hi * O],
-                in_=w3_inter[lo][:, 0 : (hi - lo) * O * PACK],
+                in_=w3_inter[first][:, (lo - first) * O * PACK : (hi - first) * O * PACK],
             )
 
         def interleave_scalar(s, lo, hi):
@@ -407,7 +449,7 @@ def tile_mlpmodelpredictor_pb_t_w8_kernel(
         def store(s, tiles):
             b, hf = divmod(s, HALVES)
             n = len(tiles)
-            result = work.tile([P, SUB, O], F32, name="result", bufs=4)
+            result = work.tile([P, SUB, O], F32, name="result", bufs=STEPS + 1)
             nc.vector.tensor_tensor(
                 out=result[:, 0:n, :],
                 in0=out_banks[s, tiles.start][:, tiles.start : tiles.stop, :],
@@ -428,32 +470,44 @@ def tile_mlpmodelpredictor_pb_t_w8_kernel(
         all_tiles, all_slots = range(SUB), range(PACK)
         on_v, on_s = nc.vector.tensor_copy, nc.scalar.copy
 
-        for i, copy in enumerate((on_v, on_s_activation, on_v, on_s)):
-            widen_z(0, copy, range(i, i + 1))
+        def turn_b2():
+            bank = psum.tile([P, SUB, O], F32, name="rbank", bufs=4)
+            out_banks["b2"] = bank
+            b2_words = b2_rows[:].bitcast(F32)
+            for u in range(2):
+                nc.tensor.transpose(bank[:, u, :], b2_words[:, u::2], ident_f[:])
+
+        def copy_b2(copy):
+            copy(
+                out=b2_cols[:]
+                .rearrange("p c t -> p (c t)")
+                .bitcast(F32)
+                .rearrange("p (c u) -> p c u", u=2),
+                in_=out_banks["b2"][:, 0:2, 0 : B * G].rearrange("p u c -> p c u"),
+            )
+
+        widen_z(0, on_v, range(0, 1))
+        widen_z(0, on_s_activation, range(1, 2))
+        widen_z(0, on_v, range(2, 3))
+        widen_z(0, on_s, range(3, 4))
         widen_z(1, on_s, all_tiles)
-        transpose_z(0)
-        b2_bank = psum.tile([P, SUB, O], F32, name="rbank", bufs=4)
-        b2_words = b2_rows[:].bitcast(F32)
-        for u in range(2):
-            nc.tensor.transpose(b2_bank[:, u, :], b2_words[:, u::2], ident_f[:])
-        widen_z(2, on_s, all_tiles)
-        nc.scalar.copy(
-            out=b2_cols[:]
-            .rearrange("p c t -> p (c t)")
-            .bitcast(F32)
-            .rearrange("p (c u) -> p c u", u=2),
-            in_=b2_bank[:, 0:2, 0 : B * G].rearrange("p u c -> p c u"),
-        )
-        widen_z(3, on_s, all_tiles)
-        scale_z(0, 0)
+        transpose_tile(0, 0)
+        transpose_tile(0, 1)
+        transpose_z(0, (1,))
         permute_w1_codes(0)
-        quantize_z(0, left)
+        scale_tile(0, 0)
+        scale_tile(0, 1)
+        turn_b2()
+        widen_z(2, on_s, all_tiles)
+        copy_b2(on_s)
+        widen_z(3, on_s, all_tiles)
         permute_w1_scales(0)
+        quantize_z(0, left)
+        scale_z(0, 1)
         transpose_z(1, (0,))
         hidden(0, 0, all_slots, left)
         relu(0, 0, left)
         widen_z(4, on_s, all_tiles)
-        scale_z(0, 1)
         permute_w1_codes(1)
         quantize_z(0, right)
         transpose_z(1, (1,))
@@ -464,11 +518,18 @@ def tile_mlpmodelpredictor_pb_t_w8_kernel(
         scale_z(1, 0)
         scale_z(1, 1)
 
+        PLAN = ["TT-","VVT","VVT","VVT","VVT","TTI","VVT","TTI","VVT","TTI","VVT","TTI","VVT","TTI","VV-","---"]
+
         def v_tiles(s):
-            return 2 if s in (1, 2, 3) or (s % 2 == 0 and s >= 4) else 0
+            return len([x for x in PLAN[s] if x == "V"])
+
+        def span(s, c):
+            n = len([x for x in PLAN[s] if x == c])
+            lo = list(PLAN[s]).index(c) * P if n else 0
+            return (lo, lo + n * P) if n else None
 
         def t_range(s):
-            return (2 * P, G_FROM) if v_tiles(s) else (0, NT)
+            return span(s, "T")
 
         def widen_halves(lo, hi):
             for j in range(lo, min(hi, 2 * STEPS)):
@@ -481,15 +542,26 @@ def tile_mlpmodelpredictor_pb_t_w8_kernel(
             hidden_tile(s, 0, i)
             add_bias(s, 0, i)
 
-        def tile_of_turn(s):
-            return (3, s - 2) if s < 4 else (s - s % 2, s % 2)
+        w3_on_v = {}
+        w3_on_s = W3S
+        VT = {0: [(1, 1, "e"), (1, 0, "e")], 1: [(2, 1, "b"), (2, 0, "c")], 2: [(3, 0, "b")], 3: [(3, 1, "a")], 4: [(4, 0, "a")], 5: [(4, 1, "a")], 6: [(6, 0, "a")], 7: [(6, 1, "a")], 8: [(8, 0, "a")], 9: [(8, 1, "a")], 10: [(10, 0, "a")], 11: [(10, 1, "a")], 12: [(12, 0, "a")], 13: [(12, 1, "a")]}
 
-        w3_on_v = {1: (7, 8)}
-        w3_on_s = {2: (8, 9), 3: (9, 10), 10: (10, 11), 11: (11, 12), 12: (12, 15), 13: (15, 16)}
+        def tiles_at(s, pos):
+            return [(st, i) for (st, i, p) in VT.get(s, []) if p == pos]
+
+        def relu_tiles(s):
+            done = sorted((st, i) for (st, i, p) in VT.get(s, []))
+            while done:
+                st, i = done[0]
+                n = 2 if (st, i + 1) in done else 1
+                relu_in_place(st, i * P, (i + n) * P)
+                done = done[n:]
+
         for s in range(STEPS - 2):
             if s >= 1:
                 relu(s, 0, slice(v_tiles(s) * P, ROWS), (0, 1))
-                copy_mixed(s - 1, *t_range(s - 1))
+                if t_range(s - 1):
+                    copy_mixed(s - 1, *t_range(s - 1))
                 relu(s, 0, slice(v_tiles(s) * P, ROWS), (2, 3))
             if s < 4:
                 widen_halves(2 * (s + LEAD), 2 * (s + LEAD + 1))
@@ -497,19 +569,17 @@ def tile_mlpmodelpredictor_pb_t_w8_kernel(
                 widen_halves(2 * (s + LEAD), 2 * (s + LEAD) + 3)
             else:
                 widen_halves(2 * (s + LEAD) + 1, 2 * (s + LEAD) + 2)
+            if s >= 1 and span(s - 1, "S"):
+                interleave_scalar(s - 1, *span(s - 1, "S"))
             if s in w3_on_s:
                 interleave_w3_scalar(*w3_on_s[s])
             if s == 1:
-                interleave_vector(0, NT, ROWS)
+                interleave_vector(0, NT, G0)
             if s == 2:
-                quantize_h(0, 0, ROWS)
-            if s in (1, 2):
-                relu_in_place(s, 0, 2 * P)
-            elif s >= 3:
-                step, i = tile_of_turn(s - 1)
-                relu_in_place(step, i * P, (i + 1) * P)
-            if s >= 2 and not v_tiles(s - 1):
-                interleave_vector(s - 1, NT, G_FROM)
+                quantize_h(0, 0, G0)
+            relu_tiles(s - 1)
+            if s >= 2 and span(s - 1, "I"):
+                interleave_vector(s - 1, *span(s - 1, "I"))
             if s - 1 in w3_on_s:
                 quantize_w3(*w3_on_s[s - 1])
             if s - 1 in w3_on_v:
@@ -520,7 +590,11 @@ def tile_mlpmodelpredictor_pb_t_w8_kernel(
                 quantize_w3(0, 3)
             elif s == 1:
                 quantize_w3(3, 7)
+                if W3G > 7:
+                    quantize_w3(7, W3G, 3)
             elif s == 2:
+                if G0 < ROWS:
+                    quantize_h(0, G0, ROWS)
                 quantize_h(0, ROWS, COLS)
             elif s == 3:
                 quantize_h(1, 0, G_FROM)
@@ -530,29 +604,36 @@ def tile_mlpmodelpredictor_pb_t_w8_kernel(
                 quantize_step(s - 2)
             quantize_z(s + 1, whole)
             if s == 0:
-                interleave_w3_gpsimd(3, 7)
+                interleave_w3_gpsimd(3, W3G)
             else:
                 interleave_gpsimd(s - 1)
-            if s >= 3:
-                vector_tile(*tile_of_turn(s))
-            hidden(s, 1, (0, 1), whole)
-            transpose_z(s + 2)
+            for st, i in tiles_at(s, "a"):
+                vector_tile(st, i)
+            if s in (0,):
+                transpose_z(s + 2)
+                hidden(s, 1, (0, 1), whole)
+            else:
+                hidden(s, 1, (0, 1), whole)
+                transpose_z(s + 2)
+            for st, i in tiles_at(s, "e"):
+                hidden_tile(st, 0, i)
             hidden(s, 1, (2, 3), whole)
             scale_z(s + 2, 0)
-            if s < 2:
-                vector_tile(s + 1, 1)
-            elif s == 2:
-                vector_tile(3, 0)
+            for st, i in tiles_at(s, "b"):
+                vector_tile(st, i)
             scale_z(s + 2, 1)
+            for st, i in tiles_at(s, "e"):
+                add_bias(st, 0, i)
             relu(s, 1, whole)
             if s >= 3:
                 output(s - 2, all_tiles)
                 store(s - 2, all_tiles)
             hidden(s + 1, 0, (0, 1), slice(v_tiles(s + 1) * P, ROWS))
-            interleave_tensor(s, *t_range(s))
-            if s < 2:
-                vector_tile(s + 1, 0)
-            elif s == 2:
+            if t_range(s):
+                interleave_tensor(s, *t_range(s))
+            for st, i in tiles_at(s, "c"):
+                vector_tile(st, i)
+            if s == 2:
                 output(0, all_tiles)
                 store(0, all_tiles)
             hidden(s + 1, 0, (2, 3), slice(v_tiles(s + 1) * P, ROWS))
@@ -561,11 +642,16 @@ def tile_mlpmodelpredictor_pb_t_w8_kernel(
         Q = ROWS // 2
         last_tile = slice(3 * P, ROWS)
         relu(A, 0, right, (0, 1))
-        copy_mixed(A - 1, *t_range(A - 1))
+        if t_range(A - 1):
+            copy_mixed(A - 1, *t_range(A - 1))
         relu(A, 0, right, (2, 3))
-        relu_in_place(A - 2, P, 2 * P)
-        interleave_vector(A - 1, NT, G_FROM)
-        quantize_w3(*w3_on_s[A - 1])
+        if span(A - 1, "S"):
+            interleave_scalar(A - 1, *span(A - 1, "S"))
+        relu_tiles(A - 1)
+        if span(A - 1, "I"):
+            interleave_vector(A - 1, *span(A - 1, "I"))
+        if A - 1 in w3_on_s:
+            quantize_w3(*w3_on_s[A - 1])
         quantize_step(A - 2)
         quantize_z(Z, whole)
         interleave_gpsimd(A - 1)

@@ -32,6 +32,8 @@ G_FROM = 384
 G_STEPS = range(0, STEPS - 2)
 JOINED = range(2, STEPS - 2)
 W3G = 8
+W3Z = 0
+W3A = 3
 G0 = 384
 W3S = {2: (8, 9), 3: (9, 10), 10: (10, 11), 11: (11, 12), 12: (12, 15), 13: (15, 16)}
 NT = 256
@@ -135,13 +137,14 @@ def tile_mlpmodelpredictor_pb_t_w8_kernel(
         load_w1s()
         load_z(3)
         load_w1(1)
-        load_w3(0, 3)
+        load_w3(W3Z, W3A)
         load_z(4)
         load_z(5)
-        load_w3(3, W3G)
+        load_w3(W3A, W3G)
         load_z(6)
-        for c in range(W3G, 10):
-            load_w3(c, c + 1)
+        for turn in sorted(W3S):
+            if turn < 5:
+                load_w3(*W3S[turn])
         load_z(7)
         for s in range(8, 11):
             load_z(s)
@@ -152,7 +155,7 @@ def tile_mlpmodelpredictor_pb_t_w8_kernel(
         for s in range(11, STEPS):
             load_z(s)
         for turn in sorted(W3S):
-            if W3S[turn][0] >= 10:
+            if turn >= 5:
                 load_w3(*W3S[turn])
 
         z_banks, z_codes, z_exps = {}, {}, {}
@@ -307,7 +310,7 @@ def tile_mlpmodelpredictor_pb_t_w8_kernel(
 
         def relu(s, g, cols, slots=range(PACK)):
             if s not in h_planes:
-                planes = work.tile([P, PACK, COLS], BF16, name="hplanar", bufs=4)
+                planes = work.tile([P, PACK, COLS], BF16, name="hplanar", bufs=3)
                 h_planes[s] = planes
             for t in slots:
                 nc.scalar.activation(
@@ -383,8 +386,8 @@ def tile_mlpmodelpredictor_pb_t_w8_kernel(
                 in_=hbuf[:, turned(s) * PACK : (turned(s) + COLS) * PACK],
             )
 
-        def interleave_w3_gpsimd(lo, hi):
-            dst = hbuf[:, COLS * PACK - max(hi - lo, 5) * O * PACK : COLS * PACK]
+        def interleave_w3_gpsimd(lo, hi, dst=None):
+            dst = gbuf if dst is None else dst
             w3_inter[lo] = dst
             copy_gpsimd(
                 out=dst[:, 0 : (hi - lo) * O * PACK].rearrange(
@@ -514,7 +517,7 @@ def tile_mlpmodelpredictor_pb_t_w8_kernel(
         hidden(0, 0, all_slots, right)
         relu(0, 0, right)
         permute_w1_scales(1)
-        interleave_w3_gpsimd(0, 3)
+        interleave_w3_gpsimd(W3Z, W3A)
         scale_z(1, 0)
         scale_z(1, 1)
 
@@ -559,10 +562,12 @@ def tile_mlpmodelpredictor_pb_t_w8_kernel(
 
         for s in range(STEPS - 2):
             if s >= 1:
-                relu(s, 0, slice(v_tiles(s) * P, ROWS), (0, 1))
-                if t_range(s - 1):
-                    copy_mixed(s - 1, *t_range(s - 1))
-                relu(s, 0, slice(v_tiles(s) * P, ROWS), (2, 3))
+                order = "01m23" if PLAN[s - 1][0] == "T" else "01m23"
+                for c in order:
+                    if c == "m":
+                        copy_mixed(s - 1, *t_range(s - 1))
+                    else:
+                        relu(s, 0, slice(v_tiles(s) * P, ROWS), (int(c),))
             if s < 4:
                 widen_halves(2 * (s + LEAD), 2 * (s + LEAD + 1))
             elif s % 2 == 0:
@@ -587,11 +592,11 @@ def tile_mlpmodelpredictor_pb_t_w8_kernel(
             if s in w3_on_v:
                 interleave_w3_vector(*w3_on_v[s])
             if s == 0:
-                quantize_w3(0, 3)
+                quantize_w3(W3Z, W3A)
             elif s == 1:
-                quantize_w3(3, 7)
-                if W3G > 7:
-                    quantize_w3(7, W3G, 3)
+                quantize_w3(W3A, W3A + 4)
+                if W3G > W3A + 4:
+                    quantize_w3(W3A + 4, W3G, W3A)
             elif s == 2:
                 if G0 < ROWS:
                     quantize_h(0, G0, ROWS)
@@ -604,7 +609,7 @@ def tile_mlpmodelpredictor_pb_t_w8_kernel(
                 quantize_step(s - 2)
             quantize_z(s + 1, whole)
             if s == 0:
-                interleave_w3_gpsimd(3, W3G)
+                interleave_w3_gpsimd(W3A, W3G)
             else:
                 interleave_gpsimd(s - 1)
             for st, i in tiles_at(s, "a"):
@@ -628,15 +633,18 @@ def tile_mlpmodelpredictor_pb_t_w8_kernel(
             if s >= 3:
                 output(s - 2, all_tiles)
                 store(s - 2, all_tiles)
-            hidden(s + 1, 0, (0, 1), slice(v_tiles(s + 1) * P, ROWS))
-            if t_range(s):
-                interleave_tensor(s, *t_range(s))
-            for st, i in tiles_at(s, "c"):
-                vector_tile(st, i)
-            if s == 2:
-                output(0, all_tiles)
-                store(0, all_tiles)
-            hidden(s + 1, 0, (2, 3), slice(v_tiles(s + 1) * P, ROWS))
+            order = "a01bx23" if PLAN[s][0] == "T" else "a01bx23"
+            for c in order:
+                if c in "0123":
+                    hidden(s + 1, 0, (int(c),), slice(v_tiles(s + 1) * P, ROWS))
+                elif c in "ab":
+                    interleave_tensor(s, *t_range(s), parts=(0,) if c == "a" else (1,))
+                else:
+                    for st, i in tiles_at(s, "c"):
+                        vector_tile(st, i)
+                    if s == 2:
+                        output(0, all_tiles)
+                        store(0, all_tiles)
 
         A, Z = LAST - 1, LAST
         Q = ROWS // 2

@@ -35,7 +35,9 @@ W3G = 8
 W3Z = 0
 W3A = 3
 G0 = 384
-W3S = {2: (8, 9), 3: (9, 10), 10: (10, 11), 11: (11, 12), 12: (12, 15), 13: (15, 16)}
+W3S = {2: (8, 9), 3: (9, 10), 10: (10, 11), 11: (11, 12), 12: (12, 14), 13: (14, 16)}
+W = 416
+W3T = {}
 NT = 256
 
 
@@ -63,7 +65,7 @@ def tile_mlpmodelpredictor_pb_t_w8_kernel(
         w3_codes = keep.tile([P, B * G * O], U32, name="w3_codes", align_bytes=64)
         w3_exps = keep.tile([P, B * G * O], U8, name="w3_exps", align_bytes=64)
 
-        hbuf = keep.tile([P, (COLS + G_FROM) * PACK], BF16, name="hbuf", align_bytes=64)
+        hbuf = keep.tile([P, (COLS + W) * PACK], BF16, name="hbuf", align_bytes=64)
         gbuf = hbuf[:, G_FROM * PACK : COLS * PACK]
         zbuf = []
         for i in range(ZBUFS):
@@ -145,6 +147,9 @@ def tile_mlpmodelpredictor_pb_t_w8_kernel(
         for turn in sorted(W3S):
             if turn < 5:
                 load_w3(*W3S[turn])
+        for turn in sorted(W3T):
+            if turn < 5:
+                load_w3(W3T[turn], W3T[turn] + 1)
         load_z(7)
         for s in range(8, 11):
             load_z(s)
@@ -157,6 +162,9 @@ def tile_mlpmodelpredictor_pb_t_w8_kernel(
         for turn in sorted(W3S):
             if turn >= 5:
                 load_w3(*W3S[turn])
+        for turn in sorted(W3T):
+            if turn >= 5:
+                load_w3(W3T[turn], W3T[turn] + 1)
 
         z_banks, z_codes, z_exps = {}, {}, {}
         h_banks, h_planes, h_inter, h_codes, h_exps = {}, {}, {}, {}, {}
@@ -264,8 +272,16 @@ def tile_mlpmodelpredictor_pb_t_w8_kernel(
                         product(h_banks[s, g, t][:, lo : lo + width], s, g, t, lo, lo + width)
                         lo += width
 
-        def g_from(s):
-            return G0 if s == 0 else G_FROM
+        def swapped(s):
+            return s in JOINED and s % 2 == 1
+
+        def place(s, g):
+            return (1 - g if swapped(s) else g) * ROWS
+
+        def g_cols(s):
+            if swapped(s):
+                return 0, 624
+            return (G_FROM if s < 3 or s in W3T else 416), COLS
 
         def inter_tile(s):
             if s not in h_inter:
@@ -274,10 +290,8 @@ def tile_mlpmodelpredictor_pb_t_w8_kernel(
             return h_inter[s]
 
         def interleaved(s, lo, hi):
-            if s in G_STEPS and lo >= g_from(s):
-                return gbuf[:, (lo - g_from(s)) * PACK : (hi - g_from(s)) * PACK]
-            if s in JOINED:
-                base = s % 2 * COLS
+            if s in JOINED or (s in G_STEPS and lo >= G_FROM):
+                base = W if swapped(s) else 0
                 return hbuf[:, (base + lo) * PACK : (base + hi) * PACK]
             return inter_tile(s)[:, lo * PACK : hi * PACK]
 
@@ -288,7 +302,7 @@ def tile_mlpmodelpredictor_pb_t_w8_kernel(
                 product(bank[:, t, :], s, g, t, i * P, (i + 1) * P)
 
         def add_bias(s, g, i):
-            lo = g * ROWS + i * P
+            lo = place(s, g) + i * P
             nc.vector.tensor_tensor(
                 out=interleaved(s, lo, lo + P).rearrange("p (c j t) -> p c t j", j=2, t=PACK),
                 in0=v_banks[s, g, i][:].rearrange("p t (c j) -> p c t j", j=2),
@@ -314,7 +328,7 @@ def tile_mlpmodelpredictor_pb_t_w8_kernel(
                 h_planes[s] = planes
             for t in slots:
                 nc.scalar.activation(
-                    out=h_planes[s][:, t, g * ROWS + cols.start : g * ROWS + cols.stop],
+                    out=h_planes[s][:, t, place(s, g) + cols.start : place(s, g) + cols.stop],
                     in_=h_banks[s, g, t][:, cols],
                     func=ACT.Relu,
                     bias=b2_cols[:, s // HALVES * G + g, t : t + 1],
@@ -331,19 +345,21 @@ def tile_mlpmodelpredictor_pb_t_w8_kernel(
                 out=out, in0=in_, scalar1=1.0, scalar2=0.0, op0=ALU.mult, op1=ALU.add
             )
 
-        def interleave_gpsimd(s, lo=None):
-            lo = g_from(s) if lo is None else lo
+        def interleave_gpsimd(s):
+            lo, hi = g_cols(s)
             copy_gpsimd(
-                out=interleaved(s, lo, COLS).rearrange("p (n t) -> p n t", t=PACK),
-                in_=h_planes[s][:, :, lo:COLS].rearrange("p t n -> p n t"),
+                out=interleaved(s, lo, hi).rearrange("p (n t) -> p n t", t=PACK),
+                in_=h_planes[s][:, :, lo:hi].rearrange("p t n -> p n t"),
             )
 
         def interleave_tensor(s, lo, hi, parts=(0, 1), tag="rbank"):
-            if 0 in parts:
+            if 0 in parts or 2 in parts:
                 bank = psum.tile([P, ROWS // 2, PACK], BF16, name=tag, bufs=4)
                 mixed[s, lo] = bank
             bank = mixed[s, lo]
             n = (hi - lo) // 2
+            if 2 in parts:
+                n, parts = hi - lo, (0,)
             for j in parts:
                 nc.tensor.matmul(
                     bank[:, j * n : (j + 1) * n, :],
@@ -375,15 +391,12 @@ def tile_mlpmodelpredictor_pb_t_w8_kernel(
                 in_=interleaved(s, lo, hi),
             )
 
-        def turned(s):
-            return G_FROM if s in JOINED and s % 2 == 1 else 0
-
         def quantize_step(s):
             code_tiles(s)
             nc.vector.quantize_mx(
                 out=h_codes[s][:].bitcast(FP8X4),
                 scales=h_exps[s][:],
-                in_=hbuf[:, turned(s) * PACK : (turned(s) + COLS) * PACK],
+                in_=interleaved(s, 0, COLS),
             )
 
         def interleave_w3_gpsimd(lo, hi, dst=None):
@@ -416,6 +429,23 @@ def tile_mlpmodelpredictor_pb_t_w8_kernel(
                 in_=w3_raw[lo][:].rearrange("p c t (j i) -> p c j t i", i=2),
             )
 
+        def interleave_w3_tensor(c, bank):
+            nc.tensor.matmul(
+                bank[:, O : 2 * O, :],
+                lhsT=ident_b[:],
+                rhs=w3_raw[c][:, 0].rearrange("p t o -> p o t"),
+                start=True,
+                stop=True,
+            )
+
+        def copy_w3(c, bank):
+            tile = work.tile([P, O * PACK], BF16, name="w3mixed", bufs=3, align_bytes=64)
+            w3_inter[c] = tile
+            nc.scalar.copy(
+                out=tile[:].bitcast(F32),
+                in_=bank[:, O : 2 * O, :].rearrange("p n t -> p (n t)").bitcast(F32),
+            )
+
         def quantize_w3(lo, hi, first=None):
             first = lo if first is None else first
             nc.vector.quantize_mx(
@@ -436,7 +466,7 @@ def tile_mlpmodelpredictor_pb_t_w8_kernel(
             out_banks[s, tiles.start] = bank
             for i in tiles:
                 for g in range(G):
-                    at = (g * ROWS + i * P - turned(s)) % COLS
+                    at = place(s, g) + i * P
                     rows = slice(at, at + P)
                     chans = slice((b * G + g) * O, (b * G + g + 1) * O)
                     nc.tensor.matmul_mx(
@@ -521,18 +551,31 @@ def tile_mlpmodelpredictor_pb_t_w8_kernel(
         scale_z(1, 0)
         scale_z(1, 1)
 
-        PLAN = ["TT-","VVT","VVT","VVT","VVT","TTI","VVT","TTI","VVT","TTI","VVT","TTI","VVT","TTI","VV-","---"]
+        PLAN = ["TT-","VVT","VVT","VVT","VVT","TTI","VVT","TTI","VVT","TTI","VVT","TTI","VVT","TTS","VV-","---"]
 
         def v_tiles(s):
             return len([x for x in PLAN[s] if x == "V"])
 
-        def span(s, c):
-            n = len([x for x in PLAN[s] if x == c])
-            lo = list(PLAN[s]).index(c) * P if n else 0
-            return (lo, lo + n * P) if n else None
+        def own_cols(s):
+            lo, hi = g_cols(s)
+            if swapped(s):
+                return hi, COLS - v_tiles(s) * P
+            return v_tiles(s) * P, lo
 
         def t_range(s):
-            return span(s, "T")
+            lo, hi = own_cols(s)
+            return lo, min(hi, lo + NT)
+
+        def span(s, c):
+            lo, hi = own_cols(s)
+            if c in PLAN[s] and hi > lo + NT:
+                return lo + NT, hi
+            return None
+
+        def s_cols(s):
+            if swapped(s):
+                return slice(0, ROWS - v_tiles(s) * P)
+            return slice(v_tiles(s) * P, ROWS)
 
         def widen_halves(lo, hi):
             for j in range(lo, min(hi, 2 * STEPS)):
@@ -547,7 +590,7 @@ def tile_mlpmodelpredictor_pb_t_w8_kernel(
 
         w3_on_v = {}
         w3_on_s = W3S
-        VT = {0: [(1, 1, "e"), (1, 0, "e")], 1: [(2, 1, "b"), (2, 0, "c")], 2: [(3, 0, "b")], 3: [(3, 1, "a")], 4: [(4, 0, "a")], 5: [(4, 1, "a")], 6: [(6, 0, "a")], 7: [(6, 1, "a")], 8: [(8, 0, "a")], 9: [(8, 1, "a")], 10: [(10, 0, "a")], 11: [(10, 1, "a")], 12: [(12, 0, "a")], 13: [(12, 1, "a")]}
+        VT = {0: [(1, 1, "e"), (1, 0, "e")], 1: [(2, 1, "b"), (2, 0, "c")], 2: [(3, 2, "b")], 3: [(3, 3, "a")], 4: [(4, 0, "a")], 5: [(4, 1, "a")], 6: [(6, 0, "a")], 7: [(6, 1, "a")], 8: [(8, 0, "a")], 9: [(8, 1, "a")], 10: [(10, 0, "a")], 11: [(10, 1, "a")], 12: [(12, 0, "a")], 13: [(12, 1, "a")]}
 
         def tiles_at(s, pos):
             return [(st, i) for (st, i, p) in VT.get(s, []) if p == pos]
@@ -557,7 +600,7 @@ def tile_mlpmodelpredictor_pb_t_w8_kernel(
             while done:
                 st, i = done[0]
                 n = 2 if (st, i + 1) in done else 1
-                relu_in_place(st, i * P, (i + n) * P)
+                relu_in_place(st, place(st, 0) + i * P, place(st, 0) + (i + n) * P)
                 done = done[n:]
 
         for s in range(STEPS - 2):
@@ -566,8 +609,10 @@ def tile_mlpmodelpredictor_pb_t_w8_kernel(
                 for c in order:
                     if c == "m":
                         copy_mixed(s - 1, *t_range(s - 1))
+                        if s - 1 in W3T:
+                            copy_w3(W3T[s - 1], mixed[s - 1, t_range(s - 1)[0]])
                     else:
-                        relu(s, 0, slice(v_tiles(s) * P, ROWS), (int(c),))
+                        relu(s, 0, s_cols(s), (int(c),))
             if s < 4:
                 widen_halves(2 * (s + LEAD), 2 * (s + LEAD + 1))
             elif s % 2 == 0:
@@ -582,11 +627,15 @@ def tile_mlpmodelpredictor_pb_t_w8_kernel(
                 interleave_vector(0, NT, G0)
             if s == 2:
                 quantize_h(0, 0, G0)
+            if 0 and s >= 3 and span(s - 2, "I"):
+                interleave_vector(s - 2, span(s - 2, "I")[1] - 0, span(s - 2, "I")[1])
             relu_tiles(s - 1)
             if s >= 2 and span(s - 1, "I"):
-                interleave_vector(s - 1, *span(s - 1, "I"))
+                interleave_vector(s - 1, span(s - 1, "I")[0], span(s - 1, "I")[1] - 0)
             if s - 1 in w3_on_s:
                 quantize_w3(*w3_on_s[s - 1])
+            if s - 2 in W3T:
+                quantize_w3(W3T[s - 2], W3T[s - 2] + 1)
             if s - 1 in w3_on_v:
                 quantize_w3(*w3_on_v[s - 1])
             if s in w3_on_v:
@@ -636,7 +685,12 @@ def tile_mlpmodelpredictor_pb_t_w8_kernel(
             order = "a01bx23" if PLAN[s][0] == "T" else "a01bx23"
             for c in order:
                 if c in "0123":
-                    hidden(s + 1, 0, (int(c),), slice(v_tiles(s + 1) * P, ROWS))
+                    hidden(s + 1, 0, (int(c),), s_cols(s + 1))
+                elif c in "ab" and s in W3T:
+                    if c == "a":
+                        interleave_tensor(s, *t_range(s), parts=(2,))
+                    else:
+                        interleave_w3_tensor(W3T[s], mixed[s, t_range(s)[0]])
                 elif c in "ab":
                     interleave_tensor(s, *t_range(s), parts=(0,) if c == "a" else (1,))
                 else:
@@ -660,6 +714,8 @@ def tile_mlpmodelpredictor_pb_t_w8_kernel(
             interleave_vector(A - 1, *span(A - 1, "I"))
         if A - 1 in w3_on_s:
             quantize_w3(*w3_on_s[A - 1])
+        if A - 2 in W3T:
+            quantize_w3(W3T[A - 2], W3T[A - 2] + 1)
         quantize_step(A - 2)
         quantize_z(Z, whole)
         interleave_gpsimd(A - 1)

@@ -23,22 +23,30 @@ ROWS = 512
 SUB = ROWS // P
 HALVES = T // ROWS
 STEPS = B * HALVES
-LAST = STEPS - 1
-
 COLS = G * ROWS
+W3_PASSES = B * G
+BANK_COLS = 256
+
 LEAD = 5
-ZBUFS = 7
-G_FROM = 384
+ZBUFS = LEAD + 2
+
 G_STEPS = range(0, STEPS - 2)
+G_FROM_FIRST = 384
+G_FROM_EVEN = 416
+G_TO_ODD = 624
 JOINED = range(2, STEPS - 2)
-W3G = 8
-W3Z = 0
-W3A = 3
-G0 = 384
-W3S = {2: (8, 9), 3: (9, 10), 10: (10, 11), 11: (11, 12), 12: (12, 14), 13: (14, 16)}
-W = 416
-W3T = {}
-NT = 256
+ODD_BASE = G_FROM_EVEN
+
+W3_FIRST, W3_SECOND = (0, 3), (3, 8)
+W3_SCALAR = {2: (8, 9), 3: (9, 10), 10: (10, 11), 11: (11, 12), 12: (12, 14), 13: (14, 16)}
+
+PAIRED = range(2, 6)
+
+
+def rows_of(s):
+    if s in PAIRED:
+        return 1 + s % 2, (s - PAIRED.start) // 2
+    return divmod(s, HALVES)
 
 
 def tile_mlpmodelpredictor_pb_t_w8_kernel(
@@ -62,11 +70,11 @@ def tile_mlpmodelpredictor_pb_t_w8_kernel(
         b2_rows = keep.tile([P, H // G], BF16, name="b2_rows")
         b2_cols = keep.tile([P, B * G, PACK], BF16, name="b2_cols")
         b3_rows = keep.tile([P, B, O], BF16, name="b3_rows")
-        w3_codes = keep.tile([P, B * G * O], U32, name="w3_codes", align_bytes=64)
-        w3_exps = keep.tile([P, B * G * O], U8, name="w3_exps", align_bytes=64)
+        w3_codes = keep.tile([P, W3_PASSES * O], U32, name="w3_codes", align_bytes=64)
+        w3_exps = keep.tile([P, W3_PASSES * O], U8, name="w3_exps", align_bytes=64)
 
-        hbuf = keep.tile([P, (COLS + W) * PACK], BF16, name="hbuf", align_bytes=64)
-        gbuf = hbuf[:, G_FROM * PACK : COLS * PACK]
+        hbuf = keep.tile([P, (COLS + ODD_BASE) * PACK], BF16, name="hbuf", align_bytes=64)
+        gbuf = hbuf[:, G_FROM_FIRST * PACK : COLS * PACK]
         zbuf = []
         for i in range(ZBUFS):
             zbuf_tile = keep.tile([P, ROWS * PACK], BF16, name="zbuf%d" % i, align_bytes=64)
@@ -77,6 +85,22 @@ def tile_mlpmodelpredictor_pb_t_w8_kernel(
                 return gbuf[:, 0 : ROWS * PACK]
             return zbuf[s % ZBUFS][:]
 
+        pair_buf = {}
+        for s in PAIRED[::2]:
+            pair_tile = keep.tile([P, 2 * SUB * R], BF16, name="pair%d" % s, align_bytes=64)
+            pair_buf[s] = pair_tile
+
+        def widened(s):
+            if s in PAIRED:
+                return pair_buf[s - s % 2][:, s % 2 * SUB * R : (s % 2 + 1) * SUB * R]
+            return zbuf_of(s)
+
+        def tile_words(s, i):
+            if s in PAIRED:
+                at = (2 * i + s % 2) * R
+                return pair_buf[s - s % 2][:, at : at + R].bitcast(F32)
+            return zbuf_of(s)[:, i * R : (i + 1) * R].bitcast(F32)
+
         zbytes = []
         for s in range(STEPS):
             zb = loads.tile([P, SUB * R], U8, name="zb", bufs=STEPS, align_bytes=64)
@@ -84,7 +108,16 @@ def tile_mlpmodelpredictor_pb_t_w8_kernel(
         w3_raw = {}
 
         def load_z(s, tiles_a_load=SUB):
-            b, hf = divmod(s, HALVES)
+            b, hf = rows_of(s)
+            if s in PAIRED:
+                row = hf * ROWS + s % 2 * 2 * P
+                nc.sync.dma_start(
+                    out=zbytes[s][:].rearrange("p (i k) -> p i k", k=2 * R),
+                    in_=z2_bytes[row : row + 2 * P, 1:3, :].rearrange(
+                        "(i p) b k -> p i (b k)", p=P
+                    ),
+                )
+                return
             for i in range(0, SUB, tiles_a_load):
                 row = hf * ROWS + i * P
                 nc.sync.dma_start(
@@ -95,6 +128,10 @@ def tile_mlpmodelpredictor_pb_t_w8_kernel(
                         "(i p) k -> p i k", p=P
                     ),
                 )
+
+        def load_w1(g):
+            words = sw1_words[0].rearrange("p n t -> p (n t)").bitcast(I32)
+            nc.sync.dma_start(out=w1_raw[:, g, :], in_=words[:, g * H // G : (g + 1) * H // G])
 
         def load_w3(lo, hi):
             tile = loads.tile([P, hi - lo, PACK, O], BF16, name="w3_raw%d" % lo)
@@ -108,50 +145,32 @@ def tile_mlpmodelpredictor_pb_t_w8_kernel(
         nc.vector.memset(b2_rows[:], 0.0)
         make_identity(nc, ident_f[:])
         make_identity(nc, ident_b[:])
-        w1_words = sw1_words[0].rearrange("p n t -> p (n t)").bitcast(I32)
-
-        def load_kscale():
-            nc.scalar.dma_start(
-                out=kscale[:], in_=z2_scale.rearrange("a c (p t) -> p (a c t)", t=PACK)
-            )
-
-        def load_w1(g):
-            nc.sync.dma_start(out=w1_raw[:, g, :], in_=w1_words[:, g * H // G : (g + 1) * H // G])
-
-        def load_w1s():
-            for q in range(4):
-                nc.sync.dma_start(
-                    out=w1s_raw[32 * q : 32 * q + 4, :].bitcast(I32),
-                    in_=sw1_scales[0, 4 * q : 4 * q + 4, :].bitcast(I32),
-                )
-
-        def load_b2():
-            nc.sync.dma_start(
-                out=b2_rows[0 : B * G, :], in_=b2.rearrange("b (g n) -> (b g) n", g=G)
-            )
-
         load_z(0, SUB // 2)
-        load_kscale()
+        nc.scalar.dma_start(
+            out=kscale[:], in_=z2_scale.rearrange("a c (p t) -> p (a c t)", t=PACK)
+        )
         load_w1(0)
         load_z(1)
-        load_b2()
+        nc.sync.dma_start(
+            out=b2_rows[0 : B * G, :], in_=b2.rearrange("b (g n) -> (b g) n", g=G)
+        )
         load_z(2)
-        load_w1s()
+        for q in range(4):
+            nc.sync.dma_start(
+                out=w1s_raw[32 * q : 32 * q + 4, :].bitcast(I32),
+                in_=sw1_scales[0, 4 * q : 4 * q + 4, :].bitcast(I32),
+            )
         load_z(3)
         load_w1(1)
-        load_w3(W3Z, W3A)
+        load_w3(*W3_FIRST)
         load_z(4)
         load_z(5)
-        load_w3(W3A, W3G)
+        load_w3(*W3_SECOND)
         load_z(6)
-        for turn in sorted(W3S):
-            if turn < 5:
-                load_w3(*W3S[turn])
-        for turn in sorted(W3T):
-            if turn < 5:
-                load_w3(W3T[turn], W3T[turn] + 1)
-        load_z(7)
-        for s in range(8, 11):
+        early, late = sorted(W3_SCALAR)[:2], sorted(W3_SCALAR)[2:]
+        for turn in early:
+            load_w3(*W3_SCALAR[turn])
+        for s in range(7, 11):
             load_z(s)
         nc.sync.dma_start(
             out=b3_rows[:].rearrange("p b o -> p (b o)"),
@@ -159,16 +178,13 @@ def tile_mlpmodelpredictor_pb_t_w8_kernel(
         )
         for s in range(11, STEPS):
             load_z(s)
-        for turn in sorted(W3S):
-            if turn >= 5:
-                load_w3(*W3S[turn])
-        for turn in sorted(W3T):
-            if turn >= 5:
-                load_w3(W3T[turn], W3T[turn] + 1)
+        for turn in late:
+            load_w3(*W3_SCALAR[turn])
 
         z_banks, z_codes, z_exps = {}, {}, {}
         h_banks, h_planes, h_inter, h_codes, h_exps = {}, {}, {}, {}, {}
         v_banks, mixed, out_banks, w3_inter = {}, {}, {}, {}
+
 
         def permute_w1_codes(g):
             nc.vector.tensor_copy(
@@ -183,59 +199,36 @@ def tile_mlpmodelpredictor_pb_t_w8_kernel(
 
         def widen_z(s, copy, tiles):
             cols = slice(tiles.start * R, tiles.stop * R)
-            copy(out=zbuf_of(s)[:, cols], in_=zbytes[s][:, cols].bitcast(FP8))
+            copy(out=widened(s)[:, cols], in_=zbytes[s][:, cols].bitcast(FP8))
 
-        def transpose_z(s, halves=(0, 1)):
-            words = zbuf_of(s).bitcast(F32)
-            for half in halves:
-                bank = psum.tile([P, 2, 2, P], F32, name="rbank", bufs=4)
-                z_banks[s, half] = bank
-                for i in range(2):
-                    base = R // 2 * (2 * half + i)
-                    for u in range(2):
-                        nc.tensor.transpose(
-                            bank[:, u, i, :], words[:, base + u : base + R // 2 : 2], ident_f[:]
-                        )
+        def transpose_z(s, tiles):
+            bank = psum.tile([P, 2, len(tiles), P], F32, name="rbank", bufs=4)
+            z_banks[s, tiles.start] = bank
+            for i in tiles:
+                for u in range(2):
+                    nc.tensor.transpose(
+                        bank[:, u, i - tiles.start, :],
+                        tile_words(s, i)[:, u::2],
+                        ident_f[:],
+                    )
 
-        def scale_z(s, half):
-            n = ROWS // 2
+        def transpose_step(s):
+            transpose_z(s, range(0, SUB // 2))
+            transpose_z(s, range(SUB // 2, SUB))
+
+        def scale_z(s, tiles):
             nc.vector.tensor_tensor(
-                out=zbuf_of(s)[:, half * n * PACK : (half + 1) * n * PACK].rearrange(
+                out=zbuf_of(s)[:, tiles.start * R : tiles.stop * R].rearrange(
                     "p (n u e) -> p n u e", u=2, e=2
                 ),
-                in0=z_banks[s, half][:]
+                in0=z_banks[s, tiles.start][:]
                 .rearrange("p u i r -> p (u i r)")
                 .bitcast(BF16)
                 .rearrange("p (u n e) -> p n u e", u=2, e=2),
                 in1=kscale[:]
                 .rearrange("p (u e) -> p u e", e=2)
                 .unsqueeze(1)
-                .to_broadcast([P, n, 2, 2]),
-                op=ALU.mult,
-            )
-
-        def transpose_tile(s, i):
-            words = zbuf_of(s).bitcast(F32)
-            bank = psum.tile([P, 2, P], F32, name="rbank", bufs=4)
-            z_banks[s, i, "t"] = bank
-            for u in range(2):
-                nc.tensor.transpose(
-                    bank[:, u, :], words[:, R // 2 * i + u : R // 2 * (i + 1) : 2], ident_f[:]
-                )
-
-        def scale_tile(s, i):
-            nc.vector.tensor_tensor(
-                out=zbuf_of(s)[:, i * P * PACK : (i + 1) * P * PACK].rearrange(
-                    "p (n u e) -> p n u e", u=2, e=2
-                ),
-                in0=z_banks[s, i, "t"][:]
-                .rearrange("p u r -> p (u r)")
-                .bitcast(BF16)
-                .rearrange("p (u n e) -> p n u e", u=2, e=2),
-                in1=kscale[:]
-                .rearrange("p (u e) -> p u e", e=2)
-                .unsqueeze(1)
-                .to_broadcast([P, P, 2, 2]),
+                .to_broadcast([P, len(tiles) * P, 2, 2]),
                 op=ALU.mult,
             )
 
@@ -250,94 +243,115 @@ def tile_mlpmodelpredictor_pb_t_w8_kernel(
                 in_=zbuf_of(s)[:, cols.start * PACK : cols.stop * PACK],
             )
 
-        def product(dst, s, g, t, lo, hi):
+        def swapped(s):
+            return s in JOINED and s % 2 == 1
+
+        def first_col(s, g):
+            return (1 - g if swapped(s) else g) * ROWS
+
+        def gpsimd_cols(s):
+            if swapped(s):
+                return 0, G_TO_ODD
+            return (G_FROM_FIRST if s < 3 else G_FROM_EVEN), COLS
+
+        def vector_tiles(s):
+            return 2 if s in (1, 3) or (s > 0 and s % 2 == 0) else 0
+
+        def scalar_tokens(s):
+            if swapped(s):
+                return slice(0, ROWS - vector_tiles(s) * P)
+            return slice(vector_tiles(s) * P, ROWS)
+
+        def other_cols(s):
+            lo, hi = gpsimd_cols(s)
+            if swapped(s):
+                return hi, COLS - vector_tiles(s) * P
+            return vector_tiles(s) * P, lo
+
+        def tensor_cols(s):
+            lo, hi = other_cols(s)
+            return lo, min(hi, lo + BANK_COLS)
+
+        def rest_cols(s):
+            return tensor_cols(s)[1], other_cols(s)[1]
+
+        def interleaved(s, lo, hi):
+            if s in JOINED or (s in G_STEPS and lo >= G_FROM_FIRST):
+                base = ODD_BASE if swapped(s) else 0
+                return hbuf[:, (base + lo) * PACK : (base + hi) * PACK]
+            if s not in h_inter:
+                tile = work.tile([P, COLS * PACK], BF16, name="hinter", bufs=2, align_bytes=64)
+                h_inter[s] = tile
+            return h_inter[s][:, lo * PACK : hi * PACK]
+
+        def product(dst, s, g, t, tokens):
             nc.tensor.matmul_mx(
                 out=dst,
                 lhsT=w1_codes[:, g, t, :].bitcast(FP8X4),
                 lhsT_scale=w1_scales[:, g, t, :],
-                rhs=z_codes[s][:, lo:hi].bitcast(FP8X4),
-                rhs_scale=z_exps[s][:, lo:hi],
+                rhs=z_codes[s][:, tokens].bitcast(FP8X4),
+                rhs_scale=z_exps[s][:, tokens],
                 start=True,
                 stop=True,
             )
 
-        def hidden(s, g, slots, cols):
+        def hidden(s, g, slots, tokens):
             for t in slots:
                 if (s, g, t) not in h_banks:
                     bank = psum.tile([P, ROWS], F32, name="hbank", bufs=PACK)
                     h_banks[s, g, t] = bank
-                lo = cols.start
-                for width in (ROWS, ROWS // 2, ROWS // 4):
-                    if cols.stop - lo >= width:
-                        product(h_banks[s, g, t][:, lo : lo + width], s, g, t, lo, lo + width)
-                        lo += width
+                product(h_banks[s, g, t][:, tokens], s, g, t, tokens)
 
-        def swapped(s):
-            return s in JOINED and s % 2 == 1
+        def relu(s, g, slots, tokens):
+            if s not in h_planes:
+                planes = work.tile([P, PACK, COLS], BF16, name="hplanar", bufs=3)
+                h_planes[s] = planes
+            at = first_col(s, g)
+            for t in slots:
+                nc.scalar.activation(
+                    out=h_planes[s][:, t, at + tokens.start : at + tokens.stop],
+                    in_=h_banks[s, g, t][:, tokens],
+                    func=ACT.Relu,
+                    bias=b2_cols[:, rows_of(s)[0] * G + g, t : t + 1],
+                )
 
-        def place(s, g):
-            return (1 - g if swapped(s) else g) * ROWS
-
-        def g_cols(s):
-            if swapped(s):
-                return 0, 624
-            return (G_FROM if s < 3 or s in W3T else 416), COLS
-
-        def inter_tile(s):
-            if s not in h_inter:
-                tile = work.tile([P, COLS * PACK], BF16, name="hinter", bufs=2, align_bytes=64)
-                h_inter[s] = tile
-            return h_inter[s]
-
-        def interleaved(s, lo, hi):
-            if s in JOINED or (s in G_STEPS and lo >= G_FROM):
-                base = W if swapped(s) else 0
-                return hbuf[:, (base + lo) * PACK : (base + hi) * PACK]
-            return inter_tile(s)[:, lo * PACK : hi * PACK]
-
-        def hidden_tile(s, g, i):
+        def hidden_tile(s, i):
             bank = psum.tile([P, PACK, P], F32, name="rbank", bufs=4)
-            v_banks[s, g, i] = bank
+            v_banks[s, i] = bank
             for t in range(PACK):
-                product(bank[:, t, :], s, g, t, i * P, (i + 1) * P)
+                product(bank[:, t, :], s, 0, t, slice(i * P, (i + 1) * P))
 
-        def add_bias(s, g, i):
-            lo = place(s, g) + i * P
+        def add_bias(s, i):
+            lo = first_col(s, 0) + i * P
             nc.vector.tensor_tensor(
                 out=interleaved(s, lo, lo + P).rearrange("p (c j t) -> p c t j", j=2, t=PACK),
-                in0=v_banks[s, g, i][:].rearrange("p t (c j) -> p c t j", j=2),
-                in1=b2_cols[:, s // HALVES * G + g, :]
+                in0=v_banks[s, i][:].rearrange("p t (c j) -> p c t j", j=2),
+                in1=b2_cols[:, rows_of(s)[0] * G, :]
                 .unsqueeze(1)
                 .unsqueeze(3)
                 .to_broadcast([P, P // 2, PACK, 2]),
                 op=ALU.add,
             )
 
-        def relu_in_place(s, lo, hi):
-            nc.vector.tensor_scalar(
-                out=interleaved(s, lo, hi),
-                in0=interleaved(s, lo, hi),
-                scalar1=0.0,
-                scalar2=None,
-                op0=ALU.max,
-            )
+        def vector_tile(s, i):
+            hidden_tile(s, i)
+            add_bias(s, i)
 
-        def relu(s, g, cols, slots=range(PACK)):
-            if s not in h_planes:
-                planes = work.tile([P, PACK, COLS], BF16, name="hplanar", bufs=3)
-                h_planes[s] = planes
-            for t in slots:
-                nc.scalar.activation(
-                    out=h_planes[s][:, t, place(s, g) + cols.start : place(s, g) + cols.stop],
-                    in_=h_banks[s, g, t][:, cols],
-                    func=ACT.Relu,
-                    bias=b2_cols[:, s // HALVES * G + g, t : t + 1],
-                )
+        def relu_in_place(s, tiles):
+            at = first_col(s, 0)
+            cols = interleaved(s, at + tiles.start * P, at + tiles.stop * P)
+            nc.vector.tensor_scalar(out=cols, in0=cols, scalar1=0.0, scalar2=None, op0=ALU.max)
 
         def interleave_vector(s, lo, hi):
             nc.vector.tensor_copy(
                 out=interleaved(s, lo, hi).rearrange("p (c i t) -> p c t i", i=2, t=PACK),
                 in_=h_planes[s][:, :, lo:hi].rearrange("p t (c i) -> p c t i", i=2),
+            )
+
+        def interleave_scalar(s, lo, hi):
+            nc.scalar.copy(
+                out=interleaved(s, lo, hi).rearrange("p (n t) -> p n t", t=PACK),
+                in_=h_planes[s][:, :, lo:hi].rearrange("p t n -> p n t"),
             )
 
         def copy_gpsimd(out, in_):
@@ -346,23 +360,20 @@ def tile_mlpmodelpredictor_pb_t_w8_kernel(
             )
 
         def interleave_gpsimd(s):
-            lo, hi = g_cols(s)
+            lo, hi = gpsimd_cols(s)
             copy_gpsimd(
                 out=interleaved(s, lo, hi).rearrange("p (n t) -> p n t", t=PACK),
                 in_=h_planes[s][:, :, lo:hi].rearrange("p t n -> p n t"),
             )
 
-        def interleave_tensor(s, lo, hi, parts=(0, 1), tag="rbank"):
-            if 0 in parts or 2 in parts:
-                bank = psum.tile([P, ROWS // 2, PACK], BF16, name=tag, bufs=4)
+        def interleave_tensor(s, lo, hi, parts=(0, 1)):
+            if 0 in parts:
+                bank = psum.tile([P, BANK_COLS, PACK], BF16, name="rbank", bufs=4)
                 mixed[s, lo] = bank
-            bank = mixed[s, lo]
             n = (hi - lo) // 2
-            if 2 in parts:
-                n, parts = hi - lo, (0,)
             for j in parts:
                 nc.tensor.matmul(
-                    bank[:, j * n : (j + 1) * n, :],
+                    mixed[s, lo][:, j * n : (j + 1) * n, :],
                     lhsT=ident_b[:],
                     rhs=h_planes[s][:, :, lo + j * n : lo + (j + 1) * n].rearrange(
                         "p t n -> p n t"
@@ -377,32 +388,20 @@ def tile_mlpmodelpredictor_pb_t_w8_kernel(
                 in_=mixed[s, lo][:, 0 : hi - lo, :].rearrange("p n t -> p (n t)").bitcast(F32),
             )
 
-        def code_tiles(s):
-            codes = work.tile([P, COLS], U32, name="hcodes", bufs=3, align_bytes=64)
-            exps = work.tile([P, COLS], U8, name="hexp", bufs=3, align_bytes=64)
-            h_codes[s], h_exps[s] = codes, exps
-
         def quantize_h(s, lo, hi):
             if s not in h_codes:
-                code_tiles(s)
+                codes = work.tile([P, COLS], U32, name="hcodes", bufs=3, align_bytes=64)
+                exps = work.tile([P, COLS], U8, name="hexp", bufs=3, align_bytes=64)
+                h_codes[s], h_exps[s] = codes, exps
             nc.vector.quantize_mx(
                 out=h_codes[s][:, lo:hi].bitcast(FP8X4),
                 scales=h_exps[s][:, lo:hi],
                 in_=interleaved(s, lo, hi),
             )
 
-        def quantize_step(s):
-            code_tiles(s)
-            nc.vector.quantize_mx(
-                out=h_codes[s][:].bitcast(FP8X4),
-                scales=h_exps[s][:],
-                in_=interleaved(s, 0, COLS),
-            )
-
-        def interleave_w3_gpsimd(lo, hi, dst=None):
-            dst = gbuf if dst is None else dst
+        def interleave_w3(copy, dst, lo, hi):
             w3_inter[lo] = dst
-            copy_gpsimd(
+            copy(
                 out=dst[:, 0 : (hi - lo) * O * PACK].rearrange(
                     "p (c o t) -> p c o t", o=O, t=PACK
                 ),
@@ -410,69 +409,29 @@ def tile_mlpmodelpredictor_pb_t_w8_kernel(
             )
 
         def interleave_w3_scalar(lo, hi):
-            tile = work.tile([P, 3 * O * PACK], BF16, name="w3inter", bufs=2, align_bytes=64)
-            w3_inter[lo] = tile
-            nc.scalar.copy(
-                out=tile[:, 0 : (hi - lo) * O * PACK].rearrange(
-                    "p (c o t) -> p c o t", o=O, t=PACK
-                ),
-                in_=w3_raw[lo][:].rearrange("p c t o -> p c o t"),
-            )
+            tile = work.tile([P, 2 * O * PACK], BF16, name="w3inter", bufs=2, align_bytes=64)
+            interleave_w3(nc.scalar.copy, tile, lo, hi)
 
-        def interleave_w3_vector(lo, hi):
-            tile = work.tile([P, 3 * O * PACK], BF16, name="w3inter", bufs=2, align_bytes=64)
-            w3_inter[lo] = tile
-            nc.vector.tensor_copy(
-                out=tile[:, 0 : (hi - lo) * O * PACK].rearrange(
-                    "p (c j i t) -> p c j t i", c=hi - lo, i=2, t=PACK
-                ),
-                in_=w3_raw[lo][:].rearrange("p c t (j i) -> p c j t i", i=2),
-            )
-
-        def interleave_w3_tensor(c, bank):
-            nc.tensor.matmul(
-                bank[:, O : 2 * O, :],
-                lhsT=ident_b[:],
-                rhs=w3_raw[c][:, 0].rearrange("p t o -> p o t"),
-                start=True,
-                stop=True,
-            )
-
-        def copy_w3(c, bank):
-            tile = work.tile([P, O * PACK], BF16, name="w3mixed", bufs=3, align_bytes=64)
-            w3_inter[c] = tile
-            nc.scalar.copy(
-                out=tile[:].bitcast(F32),
-                in_=bank[:, O : 2 * O, :].rearrange("p n t -> p (n t)").bitcast(F32),
-            )
-
-        def quantize_w3(lo, hi, first=None):
-            first = lo if first is None else first
+        def quantize_w3(lo, hi, first):
             nc.vector.quantize_mx(
                 out=w3_codes[:, lo * O : hi * O].bitcast(FP8X4),
                 scales=w3_exps[:, lo * O : hi * O],
                 in_=w3_inter[first][:, (lo - first) * O * PACK : (hi - first) * O * PACK],
             )
 
-        def interleave_scalar(s, lo, hi):
-            nc.scalar.copy(
-                out=interleaved(s, lo, hi).rearrange("p (n t) -> p n t", t=PACK),
-                in_=h_planes[s][:, :, lo:hi].rearrange("p t n -> p n t"),
-            )
-
         def output(s, tiles):
-            b = s // HALVES
+            b = rows_of(s)[0]
             bank = psum.tile([P, SUB, O], F32, name="rbank", bufs=4)
             out_banks[s, tiles.start] = bank
             for i in tiles:
                 for g in range(G):
-                    at = place(s, g) + i * P
-                    rows = slice(at, at + P)
+                    at = first_col(s, g) + i * P
+                    tokens = slice(at, at + P)
                     chans = slice((b * G + g) * O, (b * G + g + 1) * O)
                     nc.tensor.matmul_mx(
                         out=bank[:, i, :],
-                        lhsT=h_codes[s][:, rows].bitcast(FP8X4),
-                        lhsT_scale=h_exps[s][:, rows],
+                        lhsT=h_codes[s][:, tokens].bitcast(FP8X4),
+                        lhsT_scale=h_exps[s][:, tokens],
                         rhs=w3_codes[:, chans].bitcast(FP8X4),
                         rhs_scale=w3_exps[:, chans],
                         start=(g == 0),
@@ -480,7 +439,7 @@ def tile_mlpmodelpredictor_pb_t_w8_kernel(
                     )
 
         def store(s, tiles):
-            b, hf = divmod(s, HALVES)
+            b, hf = rows_of(s)
             n = len(tiles)
             result = work.tile([P, SUB, O], F32, name="result", bufs=STEPS + 1)
             nc.vector.tensor_tensor(
@@ -495,268 +454,186 @@ def tile_mlpmodelpredictor_pb_t_w8_kernel(
                 in_=result[:, 0:n, :],
             )
 
-        def on_s_activation(out, in_):
+        def copy_by_activation(out, in_):
             nc.scalar.activation(out=out, in_=in_, func=ACT.Copy)
 
-        whole, rest = slice(0, ROWS), slice(P, ROWS)
-        left, right = slice(0, ROWS // 2), slice(ROWS // 2, ROWS)
+        whole, left, right = slice(0, ROWS), slice(0, ROWS // 2), slice(ROWS // 2, ROWS)
         all_tiles, all_slots = range(SUB), range(PACK)
-        on_v, on_s = nc.vector.tensor_copy, nc.scalar.copy
+        low_tiles, high_tiles = range(0, SUB // 2), range(SUB // 2, SUB)
+        low_slots, high_slots = (0, 1), (2, 3)
+        on_vector, on_scalar = nc.vector.tensor_copy, nc.scalar.copy
 
-        def turn_b2():
-            bank = psum.tile([P, SUB, O], F32, name="rbank", bufs=4)
-            out_banks["b2"] = bank
-            b2_words = b2_rows[:].bitcast(F32)
-            for u in range(2):
-                nc.tensor.transpose(bank[:, u, :], b2_words[:, u::2], ident_f[:])
-
-        def copy_b2(copy):
-            copy(
-                out=b2_cols[:]
-                .rearrange("p c t -> p (c t)")
-                .bitcast(F32)
-                .rearrange("p (c u) -> p c u", u=2),
-                in_=out_banks["b2"][:, 0:2, 0 : B * G].rearrange("p u c -> p c u"),
-            )
-
-        widen_z(0, on_v, range(0, 1))
-        widen_z(0, on_s_activation, range(1, 2))
-        widen_z(0, on_v, range(2, 3))
-        widen_z(0, on_s, range(3, 4))
-        widen_z(1, on_s, all_tiles)
-        transpose_tile(0, 0)
-        transpose_tile(0, 1)
-        transpose_z(0, (1,))
+        for i, copy in enumerate((on_vector, copy_by_activation, on_vector, on_scalar)):
+            widen_z(0, copy, range(i, i + 1))
+        widen_z(1, on_scalar, all_tiles)
+        transpose_z(0, range(0, 1))
+        transpose_z(0, range(1, 2))
+        transpose_z(0, high_tiles)
         permute_w1_codes(0)
-        scale_tile(0, 0)
-        scale_tile(0, 1)
-        turn_b2()
-        widen_z(2, on_s, all_tiles)
-        copy_b2(on_s)
-        widen_z(3, on_s, all_tiles)
+        scale_z(0, range(0, 1))
+        scale_z(0, range(1, 2))
+        b2_bank = psum.tile([P, SUB, O], F32, name="rbank", bufs=4)
+        for u in range(2):
+            nc.tensor.transpose(b2_bank[:, u, :], b2_rows[:].bitcast(F32)[:, u::2], ident_f[:])
+        widen_z(2, on_scalar, all_tiles)
+        nc.scalar.copy(
+            out=b2_cols[:]
+            .rearrange("p c t -> p (c t)")
+            .bitcast(F32)
+            .rearrange("p (c u) -> p c u", u=2),
+            in_=b2_bank[:, 0:2, 0 : B * G].rearrange("p u c -> p c u"),
+        )
+        widen_z(3, on_scalar, all_tiles)
         permute_w1_scales(0)
         quantize_z(0, left)
-        scale_z(0, 1)
-        transpose_z(1, (0,))
+        scale_z(0, high_tiles)
+        transpose_z(1, low_tiles)
         hidden(0, 0, all_slots, left)
-        relu(0, 0, left)
-        widen_z(4, on_s, all_tiles)
+        relu(0, 0, all_slots, left)
+        widen_z(4, on_scalar, all_tiles)
         permute_w1_codes(1)
         quantize_z(0, right)
-        transpose_z(1, (1,))
+        transpose_z(1, high_tiles)
         hidden(0, 0, all_slots, right)
-        relu(0, 0, right)
+        relu(0, 0, all_slots, right)
         permute_w1_scales(1)
-        interleave_w3_gpsimd(W3Z, W3A)
-        scale_z(1, 0)
-        scale_z(1, 1)
+        interleave_w3(copy_gpsimd, gbuf, *W3_FIRST)
+        scale_z(1, low_tiles)
+        scale_z(1, high_tiles)
 
-        PLAN = ["TT-","VVT","VVT","VVT","VVT","TTI","VVT","TTI","VVT","TTI","VVT","TTI","VVT","TTS","VV-","---"]
+        def widen_ahead(s):
+            ahead = s + LEAD
+            if ahead < STEPS:
+                widen_z(ahead, on_scalar, high_tiles if s > 4 and s % 2 == 1 else all_tiles)
+            if s >= 4 and s % 2 == 0 and ahead + 1 < STEPS:
+                widen_z(ahead + 1, on_scalar, low_tiles)
 
-        def v_tiles(s):
-            return len([x for x in PLAN[s] if x == "V"])
+        def tiles_of_turn(s):
+            if s < 2:
+                return s + 1, low_tiles
+            if s < 4:
+                return 3, range(s, s + 1)
+            return s - s % 2, range(s % 2, s % 2 + 1)
 
-        def own_cols(s):
-            lo, hi = g_cols(s)
-            if swapped(s):
-                return hi, COLS - v_tiles(s) * P
-            return v_tiles(s) * P, lo
+        def port_work(s):
+            if s == 1:
+                interleave_vector(0, *rest_cols(0))
+            if s == 2:
+                quantize_h(0, 0, G_FROM_FIRST)
+            if s >= 1:
+                relu_in_place(*tiles_of_turn(s - 1))
+            if 2 <= s < STEPS - 2 and not vector_tiles(s - 1):
+                interleave_vector(s - 1, *rest_cols(s - 1))
+            if s - 1 in W3_SCALAR:
+                quantize_w3(*W3_SCALAR[s - 1], W3_SCALAR[s - 1][0])
+            if s == 0:
+                quantize_w3(*W3_FIRST, W3_FIRST[0])
+            elif s == 1:
+                lo, hi = W3_SECOND
+                quantize_w3(lo, hi - 1, lo)
+                quantize_w3(hi - 1, hi, lo)
+            elif s < 4:
+                if s == 3:
+                    quantize_h(1, 0, G_FROM_FIRST)
+                quantize_h(s - 2, G_FROM_FIRST, ROWS)
+                quantize_h(s - 2, ROWS, COLS)
+            else:
+                quantize_h(s - 2, 0, COLS)
+            quantize_z(s + 1, whole)
 
-        def t_range(s):
-            lo, hi = own_cols(s)
-            return lo, min(hi, lo + NT)
-
-        def span(s, c):
-            lo, hi = own_cols(s)
-            if c in PLAN[s] and hi > lo + NT:
-                return lo + NT, hi
-            return None
-
-        def s_cols(s):
-            if swapped(s):
-                return slice(0, ROWS - v_tiles(s) * P)
-            return slice(v_tiles(s) * P, ROWS)
-
-        def widen_halves(lo, hi):
-            for j in range(lo, min(hi, 2 * STEPS)):
-                if j % 2 == 0 and j + 1 < hi:
-                    widen_z(j // 2, on_s, all_tiles)
-                elif j % 2 == 0 or j == lo:
-                    widen_z(j // 2, on_s, range(j % 2 * 2, j % 2 * 2 + 2))
-
-        def vector_tile(s, i):
-            hidden_tile(s, 0, i)
-            add_bias(s, 0, i)
-
-        w3_on_v = {}
-        w3_on_s = W3S
-        VT = {0: [(1, 1, "e"), (1, 0, "e")], 1: [(2, 1, "b"), (2, 0, "c")], 2: [(3, 2, "b")], 3: [(3, 3, "a")], 4: [(4, 0, "a")], 5: [(4, 1, "a")], 6: [(6, 0, "a")], 7: [(6, 1, "a")], 8: [(8, 0, "a")], 9: [(8, 1, "a")], 10: [(10, 0, "a")], 11: [(10, 1, "a")], 12: [(12, 0, "a")], 13: [(12, 1, "a")]}
-
-        def tiles_at(s, pos):
-            return [(st, i) for (st, i, p) in VT.get(s, []) if p == pos]
-
-        def relu_tiles(s):
-            done = sorted((st, i) for (st, i, p) in VT.get(s, []))
-            while done:
-                st, i = done[0]
-                n = 2 if (st, i + 1) in done else 1
-                relu_in_place(st, place(st, 0) + i * P, place(st, 0) + (i + n) * P)
-                done = done[n:]
+        def scalar_start(s):
+            relu(s, 0, low_slots, scalar_tokens(s))
+            copy_mixed(s - 1, *tensor_cols(s - 1))
+            relu(s, 0, high_slots, scalar_tokens(s))
 
         for s in range(STEPS - 2):
+            tile_step, tiles = tiles_of_turn(s)
             if s >= 1:
-                order = "01m23" if PLAN[s - 1][0] == "T" else "01m23"
-                for c in order:
-                    if c == "m":
-                        copy_mixed(s - 1, *t_range(s - 1))
-                        if s - 1 in W3T:
-                            copy_w3(W3T[s - 1], mixed[s - 1, t_range(s - 1)[0]])
-                    else:
-                        relu(s, 0, s_cols(s), (int(c),))
-            if s < 4:
-                widen_halves(2 * (s + LEAD), 2 * (s + LEAD + 1))
-            elif s % 2 == 0:
-                widen_halves(2 * (s + LEAD), 2 * (s + LEAD) + 3)
-            else:
-                widen_halves(2 * (s + LEAD) + 1, 2 * (s + LEAD) + 2)
-            if s >= 1 and span(s - 1, "S"):
-                interleave_scalar(s - 1, *span(s - 1, "S"))
-            if s in w3_on_s:
-                interleave_w3_scalar(*w3_on_s[s])
-            if s == 1:
-                interleave_vector(0, NT, G0)
-            if s == 2:
-                quantize_h(0, 0, G0)
-            if 0 and s >= 3 and span(s - 2, "I"):
-                interleave_vector(s - 2, span(s - 2, "I")[1] - 0, span(s - 2, "I")[1])
-            relu_tiles(s - 1)
-            if s >= 2 and span(s - 1, "I"):
-                interleave_vector(s - 1, span(s - 1, "I")[0], span(s - 1, "I")[1] - 0)
-            if s - 1 in w3_on_s:
-                quantize_w3(*w3_on_s[s - 1])
-            if s - 2 in W3T:
-                quantize_w3(W3T[s - 2], W3T[s - 2] + 1)
-            if s - 1 in w3_on_v:
-                quantize_w3(*w3_on_v[s - 1])
-            if s in w3_on_v:
-                interleave_w3_vector(*w3_on_v[s])
+                scalar_start(s)
+            widen_ahead(s)
+            if s in W3_SCALAR:
+                interleave_w3_scalar(*W3_SCALAR[s])
+            port_work(s)
             if s == 0:
-                quantize_w3(W3Z, W3A)
-            elif s == 1:
-                quantize_w3(W3A, W3A + 4)
-                if W3G > W3A + 4:
-                    quantize_w3(W3A + 4, W3G, W3A)
-            elif s == 2:
-                if G0 < ROWS:
-                    quantize_h(0, G0, ROWS)
-                quantize_h(0, ROWS, COLS)
-            elif s == 3:
-                quantize_h(1, 0, G_FROM)
-                quantize_h(1, G_FROM, ROWS)
-                quantize_h(1, ROWS, COLS)
-            else:
-                quantize_step(s - 2)
-            quantize_z(s + 1, whole)
-            if s == 0:
-                interleave_w3_gpsimd(W3A, W3G)
+                interleave_w3(copy_gpsimd, gbuf, *W3_SECOND)
             else:
                 interleave_gpsimd(s - 1)
-            for st, i in tiles_at(s, "a"):
-                vector_tile(st, i)
-            if s in (0,):
-                transpose_z(s + 2)
-                hidden(s, 1, (0, 1), whole)
+            if s >= 3:
+                vector_tile(tile_step, tiles.start)
+            if s == 0:
+                transpose_step(2)
+                hidden(0, 1, all_slots, whole)
+                hidden_tile(1, 1)
+                hidden_tile(1, 0)
             else:
-                hidden(s, 1, (0, 1), whole)
-                transpose_z(s + 2)
-            for st, i in tiles_at(s, "e"):
-                hidden_tile(st, 0, i)
-            hidden(s, 1, (2, 3), whole)
-            scale_z(s + 2, 0)
-            for st, i in tiles_at(s, "b"):
-                vector_tile(st, i)
-            scale_z(s + 2, 1)
-            for st, i in tiles_at(s, "e"):
-                add_bias(st, 0, i)
-            relu(s, 1, whole)
+                hidden(s, 1, low_slots, whole)
+                transpose_step(s + 2)
+                hidden(s, 1, high_slots, whole)
+            scale_z(s + 2, low_tiles)
+            if s in (1, 2):
+                vector_tile(tile_step, tiles.stop - 1)
+            scale_z(s + 2, high_tiles)
+            if s == 0:
+                add_bias(1, 1)
+                add_bias(1, 0)
+            relu(s, 1, all_slots, whole)
             if s >= 3:
                 output(s - 2, all_tiles)
                 store(s - 2, all_tiles)
-            order = "a01bx23" if PLAN[s][0] == "T" else "a01bx23"
-            for c in order:
-                if c in "0123":
-                    hidden(s + 1, 0, (int(c),), s_cols(s + 1))
-                elif c in "ab" and s in W3T:
-                    if c == "a":
-                        interleave_tensor(s, *t_range(s), parts=(2,))
-                    else:
-                        interleave_w3_tensor(W3T[s], mixed[s, t_range(s)[0]])
-                elif c in "ab":
-                    interleave_tensor(s, *t_range(s), parts=(0,) if c == "a" else (1,))
-                else:
-                    for st, i in tiles_at(s, "c"):
-                        vector_tile(st, i)
-                    if s == 2:
-                        output(0, all_tiles)
-                        store(0, all_tiles)
+            interleave_tensor(s, *tensor_cols(s), parts=(0,))
+            hidden(s + 1, 0, low_slots, scalar_tokens(s + 1))
+            interleave_tensor(s, *tensor_cols(s), parts=(1,))
+            if s == 1:
+                vector_tile(2, 0)
+            if s == 2:
+                output(0, all_tiles)
+                store(0, all_tiles)
+            hidden(s + 1, 0, high_slots, scalar_tokens(s + 1))
 
-        A, Z = LAST - 1, LAST
-        Q = ROWS // 2
-        last_tile = slice(3 * P, ROWS)
-        relu(A, 0, right, (0, 1))
-        if t_range(A - 1):
-            copy_mixed(A - 1, *t_range(A - 1))
-        relu(A, 0, right, (2, 3))
-        if span(A - 1, "S"):
-            interleave_scalar(A - 1, *span(A - 1, "S"))
-        relu_tiles(A - 1)
-        if span(A - 1, "I"):
-            interleave_vector(A - 1, *span(A - 1, "I"))
-        if A - 1 in w3_on_s:
-            quantize_w3(*w3_on_s[A - 1])
-        if A - 2 in W3T:
-            quantize_w3(W3T[A - 2], W3T[A - 2] + 1)
-        quantize_step(A - 2)
-        quantize_z(Z, whole)
-        interleave_gpsimd(A - 1)
-        hidden_tile(A, 0, 0)
-        hidden_tile(A, 0, 1)
-        add_bias(A, 0, 0)
-        add_bias(A, 0, 1)
-        hidden(A, 1, all_slots, whole)
-        output(A - 2, all_tiles)
-        store(A - 2, all_tiles)
-        relu(A, 1, whole)
-        for i in range(3):
-            hidden_tile(Z, 0, i)
-            add_bias(Z, 0, i)
-        hidden(Z, 0, all_slots, last_tile)
-        relu(Z, 0, last_tile)
-        interleave_scalar(A, ROWS, 5 * P)
-        interleave_tensor(A, Q, ROWS, parts=(0,))
-        hidden(Z, 1, all_slots, whole)
-        interleave_tensor(A, Q, ROWS, parts=(1,))
-        interleave_tensor(A, 5 * P, 7 * P)
-        relu(Z, 1, whole)
-        copy_mixed(A, Q, ROWS)
-        copy_mixed(A, 5 * P, 7 * P)
-        interleave_scalar(Z, 3 * P, ROWS)
-        relu_in_place(A, 0, Q)
-        quantize_step(A - 1)
-        output(A - 1, all_tiles)
-        relu_in_place(Z, 0, 3 * P)
-        interleave_vector(A, 7 * P, COLS)
-        interleave_tensor(Z, ROWS, ROWS + Q)
-        copy_mixed(Z, ROWS, ROWS + Q)
-        interleave_vector(Z, ROWS + Q, COLS)
-        store(A - 1, all_tiles)
-        quantize_h(A, 0, COLS)
-        output(A, all_tiles)
-        quantize_h(Z, 0, ROWS)
-        quantize_h(Z, ROWS + Q, COLS)
-        output(Z, range(2, 4))
-        quantize_h(Z, ROWS, ROWS + Q)
-        store(A, all_tiles)
-        output(Z, range(0, 2))
-        store(Z, range(2, 4))
-        store(Z, range(0, 2))
+        prev, last = STEPS - 2, STEPS - 1
+        last_tile = slice(ROWS - P, ROWS)
+        half = ROWS // 2
+        scalar_start(prev)
+        interleave_scalar(prev - 1, *rest_cols(prev - 1))
+        port_work(prev)
+        interleave_gpsimd(prev - 1)
+        hidden_tile(prev, 0)
+        hidden_tile(prev, 1)
+        add_bias(prev, 0)
+        add_bias(prev, 1)
+        hidden(prev, 1, all_slots, whole)
+        output(prev - 2, all_tiles)
+        store(prev - 2, all_tiles)
+        relu(prev, 1, all_slots, whole)
+        for i in range(SUB - 1):
+            vector_tile(last, i)
+        hidden(last, 0, all_slots, last_tile)
+        relu(last, 0, all_slots, last_tile)
+        interleave_scalar(prev, ROWS, ROWS + P)
+        interleave_tensor(prev, half, ROWS, parts=(0,))
+        hidden(last, 1, all_slots, whole)
+        interleave_tensor(prev, half, ROWS, parts=(1,))
+        interleave_tensor(prev, ROWS + P, COLS - P)
+        relu(last, 1, all_slots, whole)
+        copy_mixed(prev, half, ROWS)
+        copy_mixed(prev, ROWS + P, COLS - P)
+        interleave_scalar(last, ROWS - P, ROWS)
+        relu_in_place(prev, low_tiles)
+        quantize_h(prev - 1, 0, COLS)
+        output(prev - 1, all_tiles)
+        relu_in_place(last, range(SUB - 1))
+        interleave_vector(prev, COLS - P, COLS)
+        interleave_tensor(last, ROWS, ROWS + half)
+        copy_mixed(last, ROWS, ROWS + half)
+        interleave_vector(last, ROWS + half, COLS)
+        store(prev - 1, all_tiles)
+        quantize_h(prev, 0, COLS)
+        output(prev, all_tiles)
+        quantize_h(last, 0, ROWS)
+        quantize_h(last, ROWS + half, COLS)
+        output(last, high_tiles)
+        quantize_h(last, ROWS, ROWS + half)
+        store(prev, all_tiles)
+        output(last, low_tiles)
+        store(last, high_tiles)
+        store(last, low_tiles)

@@ -149,8 +149,8 @@ def tile_mlpmodelpredictor_pb_t_w8_kernel(
         nc.scalar.dma_start(
             out=kscale[:], in_=z2_scale.rearrange("a c (p t) -> p (a c t)", t=PACK)
         )
-        load_w1(0)
         load_z(1)
+        load_w1(0)
         nc.sync.dma_start(
             out=b2_rows[0 : B * G, :], in_=b2.rearrange("b (g n) -> (b g) n", g=G)
         )
@@ -469,9 +469,9 @@ def tile_mlpmodelpredictor_pb_t_w8_kernel(
         transpose_z(0, range(0, 1))
         transpose_z(0, range(1, 2))
         transpose_z(0, high_tiles)
-        permute_w1_codes(0)
         scale_z(0, range(0, 1))
         scale_z(0, range(1, 2))
+        permute_w1_codes(0)
         b2_bank = psum.tile([P, SUB, O], F32, name="rbank", bufs=4)
         for u in range(2):
             nc.tensor.transpose(b2_bank[:, u, :], b2_rows[:].bitcast(F32)[:, u::2], ident_f[:])
@@ -484,8 +484,8 @@ def tile_mlpmodelpredictor_pb_t_w8_kernel(
             in_=b2_bank[:, 0:2, 0 : B * G].rearrange("p u c -> p c u"),
         )
         widen_z(3, on_scalar, all_tiles)
-        permute_w1_scales(0)
         quantize_z(0, left)
+        permute_w1_scales(0)
         scale_z(0, high_tiles)
         transpose_z(1, low_tiles)
         hidden(0, 0, all_slots, left)

@@ -21,32 +21,22 @@ PACK = 4
 G = H // (P * PACK)
 ROWS = 512
 SUB = ROWS // P
-HALVES = T // ROWS
-STEPS = B * HALVES
-COLS = G * ROWS
 W3_PASSES = B * G
 BANK_COLS = 256
+QUANT_COLS = (1024, 512, 384, 256, 128, 64)
 
-LEAD = 5
-ZBUFS = LEAD + 2
-
-G_STEPS = range(0, STEPS - 2)
-G_FROM_FIRST = 384
-G_FROM_EVEN = 416
-G_TO_ODD = 624
-JOINED = range(2, STEPS - 2)
-ODD_BASE = G_FROM_EVEN
-
-W3_FIRST, W3_SECOND = (0, 3), (3, 8)
-W3_SCALAR = {2: (8, 9), 3: (9, 10), 10: (10, 11), 11: (11, 12), 12: (12, 14), 13: (14, 16)}
-
-PAIRED = range(2, 6)
-
-
-def rows_of(s):
-    if s in PAIRED:
-        return 1 + s % 2, (s - PAIRED.start) // 2
-    return divmod(s, HALVES)
+BATCHES = (
+    [(0, 1, 0), (1, 2, 0), (0, 2, 1)]
+    + [(b, 2, 1 - b % 2) for b in range(2, B - 1)]
+    + [(B - 1, 1, 0)]
+)
+LAST = len(BATCHES) - 1
+TILES = (3, 4, 3, 2, 3, 2, 2, 4, 4)
+DIRECT = (0, 0, 0, 0, 0, 0, 128, 384, 256)
+W3_CUT = 6
+G_NUM, G_DEN, G_LESS = 7, 8, 64
+FIRST_V = 6
+MIX_AT = 3
 
 
 def tile_mlpmodelpredictor_pb_t_w8_kernel(
@@ -64,78 +54,48 @@ def tile_mlpmodelpredictor_pb_t_w8_kernel(
         ident_b = keep.tile([P, P], BF16, name="ident_b")
         kscale = keep.tile([P, PACK], F32, name="kscale")
         w1_raw = keep.tile([P, G, H // G], I32, name="w1_raw", align_bytes=64)
-        w1_codes = keep.tile([P, G, PACK, P], I32, name="w1_codes", align_bytes=64)
+        w1_codes = keep.tile([P, G, PACK, P], U32, name="w1_codes", align_bytes=64)
         w1s_raw = keep.tile([P, H], U8, name="w1s_raw", align_bytes=64)
         w1_scales = keep.tile([P, G, PACK, P], U8, name="w1_scales", align_bytes=64)
         b2_rows = keep.tile([P, H // G], BF16, name="b2_rows")
         b2_cols = keep.tile([P, B * G, PACK], BF16, name="b2_cols")
-        b3_rows = keep.tile([P, B, O], BF16, name="b3_rows")
+        b3_rows = keep.tile([P, B * O], BF16, name="b3_rows")
         w3_codes = keep.tile([P, W3_PASSES * O], U32, name="w3_codes", align_bytes=64)
         w3_exps = keep.tile([P, W3_PASSES * O], U8, name="w3_exps", align_bytes=64)
+        gbuf = keep.tile([P, 3 * ROWS * PACK], BF16, name="gbuf", align_bytes=64)
+        tbuf = keep.tile([P, max(TILES) * P * PACK], BF16, name="tbuf", align_bytes=64)
 
-        hbuf = keep.tile([P, (COLS + ODD_BASE) * PACK], BF16, name="hbuf", align_bytes=64)
-        gbuf = hbuf[:, G_FROM_FIRST * PACK : COLS * PACK]
-        zbuf = []
-        for i in range(ZBUFS):
-            zbuf_tile = keep.tile([P, ROWS * PACK], BF16, name="zbuf%d" % i, align_bytes=64)
-            zbuf.append(zbuf_tile)
+        w3_parts = ((0, W3_CUT), (W3_CUT, W3_PASSES))
+        zbytes, zbuf, w3_raw = {}, {}, {}
+        z_banks, z_codes, z_exps = {}, {}, {}
+        planes, pbuf, h_codes, h_exps = {}, {}, {}, {}
 
-        def zbuf_of(s):
-            if s == 0:
-                return gbuf[:, 0 : ROWS * PACK]
-            return zbuf[s % ZBUFS][:]
+        def steps(k):
+            return range(BATCHES[k][1])
 
-        pair_buf = {}
-        for s in PAIRED[::2]:
-            pair_tile = keep.tile([P, 2 * SUB * R], BF16, name="pair%d" % s, align_bytes=64)
-            pair_buf[s] = pair_tile
-
-        def widened(s):
-            if s in PAIRED:
-                return pair_buf[s - s % 2][:, s % 2 * SUB * R : (s % 2 + 1) * SUB * R]
-            return zbuf_of(s)
-
-        def tile_words(s, i):
-            if s in PAIRED:
-                at = (2 * i + s % 2) * R
-                return pair_buf[s - s % 2][:, at : at + R].bitcast(F32)
-            return zbuf_of(s)[:, i * R : (i + 1) * R].bitcast(F32)
-
-        zbytes = []
-        for s in range(STEPS):
-            zb = loads.tile([P, SUB * R], U8, name="zb", bufs=STEPS, align_bytes=64)
-            zbytes.append(zb)
-        w3_raw = {}
-
-        def load_z(s, tiles_a_load=SUB):
-            b, hf = rows_of(s)
-            if s in PAIRED:
-                row = hf * ROWS + s % 2 * 2 * P
-                nc.sync.dma_start(
-                    out=zbytes[s][:].rearrange("p (i k) -> p i k", k=2 * R),
-                    in_=z2_bytes[row : row + 2 * P, 1:3, :].rearrange(
-                        "(i p) b k -> p i (b k)", p=P
-                    ),
-                )
-                return
-            for i in range(0, SUB, tiles_a_load):
-                row = hf * ROWS + i * P
-                nc.sync.dma_start(
-                    out=zbytes[s][:, i * R : (i + tiles_a_load) * R].rearrange(
-                        "p (i k) -> p i k", k=R
-                    ),
-                    in_=z2_bytes[row : row + tiles_a_load * P, b, :].rearrange(
-                        "(i p) k -> p i k", p=P
-                    ),
-                )
+        def load_z(k, part):
+            b, n, hf = BATCHES[k]
+            tile = loads.tile([P, 2 * n * R], U8, name="zb%d_%d" % (k, part), align_bytes=64)
+            zbytes[k, part] = tile
+            row = hf * ROWS + part * 2 * P
+            nc.sync.dma_start(
+                out=tile[:].rearrange("p (i k) -> p i k", i=2),
+                in_=z2_bytes[row : row + 2 * P, b : b + n, :].rearrange(
+                    "(i p) b k -> p i (b k)", p=P
+                ),
+            )
 
         def load_w1(g):
             words = sw1_words[0].rearrange("p n t -> p (n t)").bitcast(I32)
             nc.sync.dma_start(out=w1_raw[:, g, :], in_=words[:, g * H // G : (g + 1) * H // G])
 
-        def load_w3(lo, hi):
-            tile = loads.tile([P, hi - lo, PACK, O], BF16, name="w3_raw%d" % lo)
-            w3_raw[lo] = tile
+        def plane_tile(shape):
+            return work.tile(shape, BF16, name="planes", bufs=3)
+
+        def load_w3(part):
+            lo, hi = w3_parts[part]
+            tile = plane_tile([P, hi - lo, PACK, O])
+            w3_raw[part] = tile
             nc.sync.dma_start(
                 out=tile[:].rearrange("p c t o -> p c (t o)"),
                 in_=w3.rearrange("b (g p t) o -> p (b g) (t o)", p=P, t=PACK)[:, lo:hi],
@@ -144,51 +104,48 @@ def tile_mlpmodelpredictor_pb_t_w8_kernel(
         nc.vector.memset(w1s_raw[:].bitcast(I32), 0)
         nc.vector.memset(b2_rows[:], 0.0)
         make_identity(nc, ident_f[:])
-        make_identity(nc, ident_b[:])
-        load_z(0, SUB // 2)
+        load_z(0, 0)
+        load_z(0, 1)
         nc.scalar.dma_start(
             out=kscale[:], in_=z2_scale.rearrange("a c (p t) -> p (a c t)", t=PACK)
         )
-        load_z(1)
+        load_z(1, 0)
         load_w1(0)
         nc.sync.dma_start(
             out=b2_rows[0 : B * G, :], in_=b2.rearrange("b (g n) -> (b g) n", g=G)
         )
-        load_z(2)
+        load_z(1, 1)
         for q in range(4):
             nc.sync.dma_start(
                 out=w1s_raw[32 * q : 32 * q + 4, :].bitcast(I32),
                 in_=sw1_scales[0, 4 * q : 4 * q + 4, :].bitcast(I32),
             )
-        load_z(3)
+        load_z(2, 0)
         load_w1(1)
-        load_w3(*W3_FIRST)
-        load_z(4)
-        load_z(5)
-        load_w3(*W3_SECOND)
-        load_z(6)
-        early, late = sorted(W3_SCALAR)[:2], sorted(W3_SCALAR)[2:]
-        for turn in early:
-            load_w3(*W3_SCALAR[turn])
-        for s in range(7, 11):
-            load_z(s)
+        load_w3(0)
+        load_z(2, 1)
+        load_z(3, 0)
+        load_z(3, 1)
+        load_w3(1)
+        load_z(4, 0)
+        load_z(4, 1)
         nc.sync.dma_start(
-            out=b3_rows[:].rearrange("p b o -> p (b o)"),
-            in_=b3.rearrange("b o -> (b o)").partition_broadcast(P),
+            out=b3_rows[:], in_=b3.rearrange("b o -> (b o)").partition_broadcast(P)
         )
-        for s in range(11, STEPS):
-            load_z(s)
-        for turn in late:
-            load_w3(*W3_SCALAR[turn])
+        for k in range(5, LAST + 1):
+            load_z(k, 0)
+            load_z(k, 1)
 
-        z_banks, z_codes, z_exps = {}, {}, {}
-        h_banks, h_planes, h_inter, h_codes, h_exps = {}, {}, {}, {}, {}
-        v_banks, mixed, out_banks, w3_inter = {}, {}, {}, {}
+        def scalar_bank(shape, dtype):
+            return psum.tile(shape, dtype, name="sbank", bufs=4)
 
+        def vector_bank(shape):
+            return psum.tile(shape, F32, name="vbank", bufs=4)
 
         def permute_w1_codes(g):
-            nc.vector.tensor_copy(
-                out=w1_codes[:, g], in_=w1_raw[:, g].rearrange("p (m t) -> p t m", t=PACK)
+            nc.scalar.copy(
+                out=w1_codes[:, g],
+                in_=w1_raw[:, g].bitcast(U32).rearrange("p (m t) -> p t m", t=PACK),
             )
 
         def permute_w1_scales(g):
@@ -197,31 +154,46 @@ def tile_mlpmodelpredictor_pb_t_w8_kernel(
                 out=w1_scales[:, g], in_=w1s_raw[:, cols].rearrange("p (m t) -> p t m", t=PACK)
             )
 
-        def widen_z(s, copy, tiles):
-            cols = slice(tiles.start * R, tiles.stop * R)
-            copy(out=widened(s)[:, cols], in_=zbytes[s][:, cols].bitcast(FP8))
+        def new_zbuf():
+            return work.tile([P, 2 * ROWS * PACK], BF16, name="zbuf", bufs=3, align_bytes=64)
 
-        def transpose_z(s, tiles):
-            bank = psum.tile([P, 2, len(tiles), P], F32, name="rbank", bufs=4)
-            z_banks[s, tiles.start] = bank
+        zbuf[0] = gbuf
+        first_pair = new_zbuf()
+        zbuf[1] = new_zbuf()
+
+        def widened(k):
+            if k == 1:
+                return first_pair
+            if k not in zbuf:
+                zbuf[k] = new_zbuf()
+            return zbuf[k]
+
+        def widen_z(k, part, copy, lo, hi):
+            at = part * 2 * len(steps(k)) * R
+            copy(
+                out=widened(k)[:, at + lo : at + hi],
+                in_=zbytes[k, part][:, lo:hi].bitcast(FP8),
+            )
+
+        def widen_part(k, part):
+            widen_z(k, part, nc.scalar.copy, 0, 2 * len(steps(k)) * R)
+
+        def transpose_z(k, j, tiles):
+            bank = vector_bank([P, 2, len(tiles), P])
+            z_banks[k, j, tiles.start] = bank
             for i in tiles:
+                at = (len(steps(k)) * i + j) * R
+                words = widened(k)[:, at : at + R].bitcast(F32)
                 for u in range(2):
-                    nc.tensor.transpose(
-                        bank[:, u, i - tiles.start, :],
-                        tile_words(s, i)[:, u::2],
-                        ident_f[:],
-                    )
+                    nc.tensor.transpose(bank[:, u, i - tiles.start, :], words[:, u::2], ident_f[:])
 
-        def transpose_step(s):
-            transpose_z(s, range(0, SUB // 2))
-            transpose_z(s, range(SUB // 2, SUB))
-
-        def scale_z(s, tiles):
+        def scale_z(k, j, tiles):
+            at = j * ROWS * PACK
             nc.vector.tensor_tensor(
-                out=zbuf_of(s)[:, tiles.start * R : tiles.stop * R].rearrange(
+                out=zbuf[k][:, at + tiles.start * R : at + tiles.stop * R].rearrange(
                     "p (n u e) -> p n u e", u=2, e=2
                 ),
-                in0=z_banks[s, tiles.start][:]
+                in0=z_banks[k, j, tiles.start][:]
                 .rearrange("p u i r -> p (u i r)")
                 .bitcast(BF16)
                 .rearrange("p (u n e) -> p n u e", u=2, e=2),
@@ -232,408 +204,363 @@ def tile_mlpmodelpredictor_pb_t_w8_kernel(
                 op=ALU.mult,
             )
 
-        def quantize_z(s, cols):
-            if cols.start == 0:
+        def quantize_z(k, j, cols):
+            if (k, j) not in z_codes:
                 codes = work.tile([P, ROWS], U32, name="zcodes", bufs=4, align_bytes=64)
                 exps = work.tile([P, ROWS], U8, name="zexp", bufs=4, align_bytes=64)
-                z_codes[s], z_exps[s] = codes, exps
+                z_codes[k, j], z_exps[k, j] = codes, exps
+            at = j * ROWS
             nc.vector.quantize_mx(
-                out=z_codes[s][:, cols].bitcast(FP8X4),
-                scales=z_exps[s][:, cols],
-                in_=zbuf_of(s)[:, cols.start * PACK : cols.stop * PACK],
+                out=z_codes[k, j][:, cols].bitcast(FP8X4),
+                scales=z_exps[k, j][:, cols],
+                in_=zbuf[k][:, (at + cols.start) * PACK : (at + cols.stop) * PACK],
             )
 
-        def swapped(s):
-            return s in JOINED and s % 2 == 1
+        def plane_cols(k):
+            return len(steps(k)) * H - TILES[k] * P
 
-        def first_col(s, g):
-            return (1 - g if swapped(s) else g) * ROWS
+        def column(k, j, g, i):
+            group = G * j + g
+            if (group + 1) * ROWS <= plane_cols(k):
+                return group * ROWS + i * P
+            if i < TILES[k]:
+                return plane_cols(k) + i * P
+            return group * ROWS + (i - TILES[k]) * P
 
-        def gpsimd_cols(s):
-            if swapped(s):
-                return 0, G_TO_ODD
-            return (G_FROM_FIRST if s < 3 else G_FROM_EVEN), COLS
+        def gpsimd_cols(k):
+            if k in (0, LAST):
+                return 0
+            reads = TILES[k + 1] + len(steps(k - 1))
+            if k + 2 <= LAST:
+                reads = reads + PACK * len(steps(k + 2))
+            fit = reads * ROWS * G_NUM // (G_DEN * PACK) - G_LESS
+            return plane_cols(k) - (plane_cols(k) - fit + 31) // 64 * 64
 
-        def vector_tiles(s):
-            return 2 if s in (1, 3) or (s > 0 and s % 2 == 0) else 0
+        def rest_cols(k):
+            return plane_cols(k) - gpsimd_cols(k)
 
-        def scalar_tokens(s):
-            if swapped(s):
-                return slice(0, ROWS - vector_tiles(s) * P)
-            return slice(vector_tiles(s) * P, ROWS)
+        def rest_of(k, lo, hi):
+            if k not in pbuf:
+                tile = work.tile([P, rest_cols(k) * PACK], BF16, name="pbuf", bufs=2, align_bytes=64)
+                pbuf[k] = tile
+            return pbuf[k][:, lo * PACK : hi * PACK]
 
-        def other_cols(s):
-            lo, hi = gpsimd_cols(s)
-            if swapped(s):
-                return hi, COLS - vector_tiles(s) * P
-            return vector_tiles(s) * P, lo
+        def planes_of(k, lo, hi):
+            return planes[k][:, :, lo:hi].rearrange("p t n -> p n t")
 
-        def tensor_cols(s):
-            lo, hi = other_cols(s)
-            return lo, min(hi, lo + BANK_COLS)
-
-        def rest_cols(s):
-            return tensor_cols(s)[1], other_cols(s)[1]
-
-        def interleaved(s, lo, hi):
-            if s in JOINED or (s in G_STEPS and lo >= G_FROM_FIRST):
-                base = ODD_BASE if swapped(s) else 0
-                return hbuf[:, (base + lo) * PACK : (base + hi) * PACK]
-            if s not in h_inter:
-                tile = work.tile([P, COLS * PACK], BF16, name="hinter", bufs=2, align_bytes=64)
-                h_inter[s] = tile
-            return h_inter[s][:, lo * PACK : hi * PACK]
-
-        def product(dst, s, g, t, tokens):
+        def product(dst, k, j, g, t, tokens):
             nc.tensor.matmul_mx(
                 out=dst,
                 lhsT=w1_codes[:, g, t, :].bitcast(FP8X4),
                 lhsT_scale=w1_scales[:, g, t, :],
-                rhs=z_codes[s][:, tokens].bitcast(FP8X4),
-                rhs_scale=z_exps[s][:, tokens],
+                rhs=z_codes[k, j][:, tokens].bitcast(FP8X4),
+                rhs_scale=z_exps[k, j][:, tokens],
                 start=True,
                 stop=True,
             )
 
-        def hidden(s, g, slots, tokens):
+        def relu_bank(k, j, g, slots, tokens):
+            if k not in planes:
+                planes[k] = plane_tile([P, PACK, plane_cols(k)])
+            n = tokens.stop - tokens.start
+            bank = scalar_bank([P, len(slots), n], F32)
             for t in slots:
-                if (s, g, t) not in h_banks:
-                    bank = psum.tile([P, ROWS], F32, name="hbank", bufs=PACK)
-                    h_banks[s, g, t] = bank
-                product(h_banks[s, g, t][:, tokens], s, g, t, tokens)
-
-        def relu(s, g, slots, tokens):
-            if s not in h_planes:
-                planes = work.tile([P, PACK, COLS], BF16, name="hplanar", bufs=3)
-                h_planes[s] = planes
-            at = first_col(s, g)
+                product(bank[:, t - slots.start, :], k, j, g, t, tokens)
+            at = column(k, j, g, tokens.start // P)
             for t in slots:
                 nc.scalar.activation(
-                    out=h_planes[s][:, t, at + tokens.start : at + tokens.stop],
-                    in_=h_banks[s, g, t][:, tokens],
+                    out=planes[k][:, t, at : at + n],
+                    in_=bank[:, t - slots.start, :],
                     func=ACT.Relu,
-                    bias=b2_cols[:, rows_of(s)[0] * G + g, t : t + 1],
+                    bias=b2_cols[:, (BATCHES[k][0] + j) * G + g, t : t + 1],
                 )
 
-        def hidden_tile(s, i):
-            bank = psum.tile([P, PACK, P], F32, name="rbank", bufs=4)
-            v_banks[s, i] = bank
-            for t in range(PACK):
-                product(bank[:, t, :], s, 0, t, slice(i * P, (i + 1) * P))
+        def relu_items(k, j, g, tokens):
+            per = ROWS // (tokens.stop - tokens.start)
+            return [(relu_bank, k, j, g, range(t, t + per), tokens) for t in range(0, PACK, per)]
 
-        def add_bias(s, i):
-            lo = first_col(s, 0) + i * P
+        def scalar_items(k):
+            items = []
+            for j in steps(k):
+                for g in range(G):
+                    taken = TILES[k] if (j, g) == (steps(k).stop - 1, G - 1) else 0
+                    if taken < SUB:
+                        items.extend(relu_items(k, j, g, slice(taken * P, ROWS)))
+            return items
+
+        def vector_tile(k, i):
+            j, g = steps(k).stop - 1, G - 1
+            bank = vector_bank([P, PACK, P])
+            for t in range(PACK):
+                product(bank[:, t, :], k, j, g, t, slice(i * P, (i + 1) * P))
             nc.vector.tensor_tensor(
-                out=interleaved(s, lo, lo + P).rearrange("p (c j t) -> p c t j", j=2, t=PACK),
-                in0=v_banks[s, i][:].rearrange("p t (c j) -> p c t j", j=2),
-                in1=b2_cols[:, rows_of(s)[0] * G, :]
+                out=tbuf[:, i * ROWS : (i + 1) * ROWS].rearrange(
+                    "p (c j t) -> p c t j", j=2, t=PACK
+                ),
+                in0=bank[:].rearrange("p t (c j) -> p c t j", j=2),
+                in1=b2_cols[:, (BATCHES[k][0] + j) * G + g, :]
                 .unsqueeze(1)
                 .unsqueeze(3)
                 .to_broadcast([P, P // 2, PACK, 2]),
                 op=ALU.add,
             )
 
-        def vector_tile(s, i):
-            hidden_tile(s, i)
-            add_bias(s, i)
-
-        def relu_in_place(s, tiles):
-            at = first_col(s, 0)
-            cols = interleaved(s, at + tiles.start * P, at + tiles.stop * P)
+        def relu_in_place(k):
+            cols = tbuf[:, 0 : TILES[k] * ROWS]
             nc.vector.tensor_scalar(out=cols, in0=cols, scalar1=0.0, scalar2=None, op0=ALU.max)
-
-        def interleave_vector(s, lo, hi):
-            nc.vector.tensor_copy(
-                out=interleaved(s, lo, hi).rearrange("p (c i t) -> p c t i", i=2, t=PACK),
-                in_=h_planes[s][:, :, lo:hi].rearrange("p t (c i) -> p c t i", i=2),
-            )
-
-        def interleave_scalar(s, lo, hi):
-            nc.scalar.copy(
-                out=interleaved(s, lo, hi).rearrange("p (n t) -> p n t", t=PACK),
-                in_=h_planes[s][:, :, lo:hi].rearrange("p t n -> p n t"),
-            )
 
         def copy_gpsimd(out, in_):
             nc.gpsimd.tensor_scalar(
                 out=out, in0=in_, scalar1=1.0, scalar2=0.0, op0=ALU.mult, op1=ALU.add
             )
 
-        def interleave_gpsimd(s):
-            lo, hi = gpsimd_cols(s)
+        def gpsimd_w3(part):
+            lo, hi = w3_parts[part]
             copy_gpsimd(
-                out=interleaved(s, lo, hi).rearrange("p (n t) -> p n t", t=PACK),
-                in_=h_planes[s][:, :, lo:hi].rearrange("p t n -> p n t"),
+                out=gbuf[:, 0 : (hi - lo) * O * PACK].rearrange(
+                    "p (c o t) -> p c o t", o=O, t=PACK
+                ),
+                in_=w3_raw[part][:].rearrange("p c t o -> p c o t"),
             )
 
-        def interleave_tensor(s, lo, hi, parts=(0, 1)):
-            if 0 in parts:
-                bank = psum.tile([P, BANK_COLS, PACK], BF16, name="rbank", bufs=4)
-                mixed[s, lo] = bank
-            n = (hi - lo) // 2
-            for j in parts:
+        def gpsimd_planes(k):
+            n = gpsimd_cols(k)
+            copy_gpsimd(
+                out=gbuf[:, 0 : n * PACK].rearrange("p (n t) -> p n t", t=PACK),
+                in_=planes_of(k, 0, n),
+            )
+
+        def mix_products(k, lo, hi):
+            bank = scalar_bank([P, BANK_COLS, PACK], BF16)
+            at = gpsimd_cols(k)
+            for c in range(lo, hi, P):
+                end = min(hi, c + P)
                 nc.tensor.matmul(
-                    mixed[s, lo][:, j * n : (j + 1) * n, :],
+                    bank[:, c - lo : end - lo, :],
                     lhsT=ident_b[:],
-                    rhs=h_planes[s][:, :, lo + j * n : lo + (j + 1) * n].rearrange(
-                        "p t n -> p n t"
-                    ),
+                    rhs=planes_of(k, at + c, at + end),
                     start=True,
                     stop=True,
                 )
+            return bank
 
-        def copy_mixed(s, lo, hi):
+        def mix_copy(k, lo, hi, bank):
             nc.scalar.copy(
-                out=interleaved(s, lo, hi).bitcast(F32),
-                in_=mixed[s, lo][:, 0 : hi - lo, :].rearrange("p n t -> p (n t)").bitcast(F32),
+                out=rest_of(k, lo, hi).bitcast(F32),
+                in_=bank[:, 0 : hi - lo, :].rearrange("p n t -> p (n t)").bitcast(F32),
             )
 
-        def quantize_h(s, lo, hi):
-            if s not in h_codes:
-                codes = work.tile([P, COLS], U32, name="hcodes", bufs=3, align_bytes=64)
-                exps = work.tile([P, COLS], U8, name="hexp", bufs=3, align_bytes=64)
-                h_codes[s], h_exps[s] = codes, exps
-            nc.vector.quantize_mx(
-                out=h_codes[s][:, lo:hi].bitcast(FP8X4),
-                scales=h_exps[s][:, lo:hi],
-                in_=interleaved(s, lo, hi),
+        def mix(k, lo, hi):
+            mix_copy(k, lo, hi, mix_products(k, lo, hi))
+
+        def interleave_scalar(k):
+            lo, hi = rest_cols(k) - DIRECT[k], rest_cols(k)
+            at = gpsimd_cols(k)
+            nc.scalar.copy(
+                out=rest_of(k, lo, hi).rearrange("p (n t) -> p n t", t=PACK),
+                in_=planes_of(k, at + lo, at + hi),
             )
 
-        def interleave_w3(copy, dst, lo, hi):
-            w3_inter[lo] = dst
-            copy(
-                out=dst[:, 0 : (hi - lo) * O * PACK].rearrange(
-                    "p (c o t) -> p c o t", o=O, t=PACK
-                ),
-                in_=w3_raw[lo][:].rearrange("p c t o -> p c o t"),
-            )
+        def mix_items(k):
+            end = rest_cols(k) - DIRECT[k]
+            items = [(mix, k, c, min(end, c + BANK_COLS)) for c in range(0, end, BANK_COLS)]
+            return items + ([(interleave_scalar, k)] if DIRECT[k] else [])
 
-        def interleave_w3_scalar(lo, hi):
-            tile = work.tile([P, 2 * O * PACK], BF16, name="w3inter", bufs=2, align_bytes=64)
-            interleave_w3(nc.scalar.copy, tile, lo, hi)
+        def quantize(codes, exps, src, cols):
+            at = 0
+            while at < cols:
+                n = max(w for w in QUANT_COLS if w <= cols - at)
+                nc.vector.quantize_mx(
+                    out=codes[:, at : at + n].bitcast(FP8X4),
+                    scales=exps[:, at : at + n],
+                    in_=src[:, at * PACK : (at + n) * PACK],
+                )
+                at = at + n
 
-        def quantize_w3(lo, hi, first):
-            nc.vector.quantize_mx(
-                out=w3_codes[:, lo * O : hi * O].bitcast(FP8X4),
-                scales=w3_exps[:, lo * O : hi * O],
-                in_=w3_inter[first][:, (lo - first) * O * PACK : (hi - first) * O * PACK],
-            )
+        def quantize_h(k, src, lo, hi):
+            if k not in h_codes:
+                n = len(steps(k)) * H
+                codes = work.tile([P, n], U32, name="hcodes", bufs=3, align_bytes=64)
+                exps = work.tile([P, n], U8, name="hexp", bufs=3, align_bytes=64)
+                h_codes[k], h_exps[k] = codes, exps
+            quantize(h_codes[k][:, lo:hi], h_exps[k][:, lo:hi], src, hi - lo)
 
-        def output(s, tiles):
-            b = rows_of(s)[0]
-            bank = psum.tile([P, SUB, O], F32, name="rbank", bufs=4)
-            out_banks[s, tiles.start] = bank
+        def quantize_tiles(k):
+            quantize_h(k, tbuf, plane_cols(k), len(steps(k)) * H)
+
+        def quantize_rest(k):
+            quantize_h(k, pbuf[k], gpsimd_cols(k), plane_cols(k))
+
+        def quantize_gpsimd(k):
+            quantize_h(k, gbuf, 0, gpsimd_cols(k))
+
+        def quantize_w3(part):
+            lo, hi = w3_parts[part]
+            quantize(w3_codes[:, lo * O :], w3_exps[:, lo * O :], gbuf, (hi - lo) * O)
+
+        def output(k, tiles):
+            b, datasets, hf = BATCHES[k]
+            n, wide = len(tiles), datasets * O
+            bank = vector_bank([P, n, wide])
             for i in tiles:
-                for g in range(G):
-                    at = first_col(s, g) + i * P
-                    tokens = slice(at, at + P)
-                    chans = slice((b * G + g) * O, (b * G + g + 1) * O)
-                    nc.tensor.matmul_mx(
-                        out=bank[:, i, :],
-                        lhsT=h_codes[s][:, tokens].bitcast(FP8X4),
-                        lhsT_scale=h_exps[s][:, tokens],
-                        rhs=w3_codes[:, chans].bitcast(FP8X4),
-                        rhs_scale=w3_exps[:, chans],
-                        start=(g == 0),
-                        stop=(g == G - 1),
-                    )
-
-        def store(s, tiles):
-            b, hf = rows_of(s)
-            n = len(tiles)
-            result = work.tile([P, SUB, O], F32, name="result", bufs=STEPS + 1)
+                for j in steps(k):
+                    for g in range(G):
+                        at = column(k, j, g, i)
+                        chans = slice(((b + j) * G + g) * O, ((b + j) * G + g + 1) * O)
+                        nc.tensor.matmul_mx(
+                            out=bank[:, i - tiles.start, j * O : (j + 1) * O],
+                            lhsT=h_codes[k][:, at : at + P].bitcast(FP8X4),
+                            lhsT_scale=h_exps[k][:, at : at + P],
+                            rhs=w3_codes[:, chans].bitcast(FP8X4),
+                            rhs_scale=w3_exps[:, chans],
+                            start=(g == 0),
+                            stop=(g == G - 1),
+                        )
+            result = work.tile([P, n, wide], F32, name="result", bufs=17)
             nc.vector.tensor_tensor(
-                out=result[:, 0:n, :],
-                in0=out_banks[s, tiles.start][:, tiles.start : tiles.stop, :],
-                in1=b3_rows[:, b, :].unsqueeze(1).to_broadcast([P, n, O]),
+                out=result[:],
+                in0=bank[:],
+                in1=b3_rows[:, b * O : b * O + wide].unsqueeze(1).to_broadcast([P, n, wide]),
                 op=ALU.add,
             )
             row = hf * ROWS + tiles.start * P
             nc.sync.dma_start(
-                out=out[row : row + n * P, b, :].rearrange("(i p) o -> p i o", p=P),
-                in_=result[:, 0:n, :],
+                out=out[row : row + n * P, b : b + datasets, :].rearrange(
+                    "(i p) b o -> p i (b o)", p=P
+                ),
+                in_=result[:],
             )
 
-        def copy_by_activation(out, in_):
-            nc.scalar.activation(out=out, in_=in_, func=ACT.Copy)
-
         whole, left, right = slice(0, ROWS), slice(0, ROWS // 2), slice(ROWS // 2, ROWS)
-        all_tiles, all_slots = range(SUB), range(PACK)
+        all_tiles = range(SUB)
         low_tiles, high_tiles = range(0, SUB // 2), range(SUB // 2, SUB)
-        low_slots, high_slots = (0, 1), (2, 3)
-        on_vector, on_scalar = nc.vector.tensor_copy, nc.scalar.copy
 
-        for i, copy in enumerate((on_vector, copy_by_activation, on_vector, on_scalar)):
-            widen_z(0, copy, range(i, i + 1))
-        widen_z(1, on_scalar, all_tiles)
-        transpose_z(0, range(0, 1))
-        transpose_z(0, range(1, 2))
-        transpose_z(0, high_tiles)
-        scale_z(0, range(0, 1))
-        scale_z(0, range(1, 2))
+        def run(items):
+            for item in items:
+                item[0](*item[1:])
+
+        def vector_items(k):
+            items = []
+            if k == 2:
+                items = [(output, 0, all_tiles)]
+            if k > 2:
+                items = [(output, k - 2, low_tiles), (output, k - 2, high_tiles)]
+            return items + [(vector_tile, k, i) for i in range(TILES[k])]
+
+        def weave(s_items, v_items, z_count):
+            def freed(j):
+                older = j + z_count - 4
+                if older < 0:
+                    return 0
+                return 2 * min(older + 1, z_count) + max(older + 1 - z_count, 0)
+
+            done = 0
+            for x, item in enumerate(s_items):
+                while done < len(v_items) and x >= FIRST_V + max(freed(done), done):
+                    run(v_items[done : done + 1])
+                    done = done + 1
+                run([item])
+            run(v_items[done:])
+
+        def spread(own, mixes):
+            items = own[:MIX_AT]
+            for x, item in enumerate(mixes):
+                items.extend([item] + own[MIX_AT + 2 * x : MIX_AT + 2 * x + 2])
+            return items + own[MIX_AT + 2 * len(mixes) :]
+
+        nc.scalar.activation(out=ident_b[:], in_=ident_f[:], func=ACT.Copy)
+        for i in all_tiles:
+            copy = nc.scalar.copy if i % 2 else nc.vector.tensor_copy
+            widen_z(0, i // 2, copy, i % 2 * R, (i % 2 + 1) * R)
+        widen_part(1, 0)
+        for tiles in (range(0, 1), range(1, 2), high_tiles):
+            transpose_z(0, 0, tiles)
+        scale_z(0, 0, range(0, 1))
+        scale_z(0, 0, range(1, 2))
         permute_w1_codes(0)
-        b2_bank = psum.tile([P, SUB, O], F32, name="rbank", bufs=4)
+        transpose_z(1, 0, low_tiles)
+        b2_bank = scalar_bank([P, 2, P], F32)
         for u in range(2):
             nc.tensor.transpose(b2_bank[:, u, :], b2_rows[:].bitcast(F32)[:, u::2], ident_f[:])
-        widen_z(2, on_scalar, all_tiles)
+        widen_part(1, 1)
         nc.scalar.copy(
             out=b2_cols[:]
             .rearrange("p c t -> p (c t)")
             .bitcast(F32)
             .rearrange("p (c u) -> p c u", u=2),
-            in_=b2_bank[:, 0:2, 0 : B * G].rearrange("p u c -> p c u"),
+            in_=b2_bank[:, :, 0 : B * G].rearrange("p u c -> p c u"),
         )
-        widen_z(3, on_scalar, all_tiles)
-        quantize_z(0, left)
+        widen_part(2, 0)
+        scale_z(0, 0, high_tiles)
+        quantize_z(0, 0, left)
         permute_w1_scales(0)
-        scale_z(0, high_tiles)
-        transpose_z(1, low_tiles)
-        hidden(0, 0, all_slots, left)
-        relu(0, 0, all_slots, left)
-        widen_z(4, on_scalar, all_tiles)
+        quantize_z(0, 0, right)
+        transpose_z(1, 1, low_tiles)
+        run(relu_items(0, 0, 0, left))
         permute_w1_codes(1)
-        quantize_z(0, right)
-        transpose_z(1, high_tiles)
-        hidden(0, 0, all_slots, right)
-        relu(0, 0, all_slots, right)
+        widen_part(2, 1)
         permute_w1_scales(1)
-        interleave_w3(copy_gpsimd, gbuf, *W3_FIRST)
-        scale_z(1, low_tiles)
-        scale_z(1, high_tiles)
+        gpsimd_w3(0)
+        transpose_z(1, 0, high_tiles)
+        scale_z(1, 0, low_tiles)
+        transpose_z(1, 1, high_tiles)
+        scale_z(1, 1, low_tiles)
+        scale_z(1, 0, high_tiles)
+        scale_z(1, 1, high_tiles)
+        run(relu_items(0, 0, 0, right))
+        run(scalar_items(0)[PACK:])
+        run(vector_items(0))
 
-        def widen_ahead(s):
-            ahead = s + LEAD
-            if ahead < STEPS:
-                widen_z(ahead, on_scalar, high_tiles if s > 4 and s % 2 == 1 else all_tiles)
-            if s >= 4 and s % 2 == 0 and ahead + 1 < STEPS:
-                widen_z(ahead + 1, on_scalar, low_tiles)
-
-        def tiles_of_turn(s):
-            if s < 2:
-                return s + 1, low_tiles
-            if s < 4:
-                return 3, range(s, s + 1)
-            return s - s % 2, range(s % 2, s % 2 + 1)
-
-        def port_work(s):
-            if s == 1:
-                interleave_vector(0, *rest_cols(0))
-            if s == 2:
-                quantize_h(0, 0, G_FROM_FIRST)
-            if s >= 1:
-                relu_in_place(*tiles_of_turn(s - 1))
-            if 2 <= s < STEPS - 2 and not vector_tiles(s - 1):
-                interleave_vector(s - 1, *rest_cols(s - 1))
-            if s - 1 in W3_SCALAR:
-                quantize_w3(*W3_SCALAR[s - 1], W3_SCALAR[s - 1][0])
-            if s == 0:
-                quantize_w3(*W3_FIRST, W3_FIRST[0])
-            elif s == 1:
-                lo, hi = W3_SECOND
-                quantize_w3(lo, hi - 1, lo)
-                quantize_w3(hi - 1, hi, lo)
-            elif s < 4:
-                if s == 3:
-                    quantize_h(1, 0, G_FROM_FIRST)
-                quantize_h(s - 2, G_FROM_FIRST, ROWS)
-                quantize_h(s - 2, ROWS, COLS)
+        for k in range(1, LAST):
+            for j in steps(k + 1):
+                transpose_z(k + 1, j, low_tiles)
+                transpose_z(k + 1, j, high_tiles)
+            if k + 2 <= LAST:
+                widen_part(k + 2, 0)
+                widen_part(k + 2, 1)
+            quantize_z(k, 0, whole)
+            relu_in_place(k - 1)
+            if k >= 2:
+                quantize_rest(k - 2)
+                quantize_tiles(k - 1)
+            if k <= 2:
+                quantize_w3(k - 1)
             else:
-                quantize_h(s - 2, 0, COLS)
-            quantize_z(s + 1, whole)
-
-        def scalar_start(s):
-            relu(s, 0, low_slots, scalar_tokens(s))
-            copy_mixed(s - 1, *tensor_cols(s - 1))
-            relu(s, 0, high_slots, scalar_tokens(s))
-
-        for s in range(STEPS - 2):
-            tile_step, tiles = tiles_of_turn(s)
-            if s >= 1:
-                scalar_start(s)
-            widen_ahead(s)
-            if s in W3_SCALAR:
-                interleave_w3_scalar(*W3_SCALAR[s])
-            port_work(s)
-            if s == 0:
-                interleave_w3(copy_gpsimd, gbuf, *W3_SECOND)
+                quantize_gpsimd(k - 2)
+            if k == 1:
+                quantize_tiles(0)
+            quantize_z(k, 1, whole)
+            if k == 1:
+                gpsimd_w3(1)
             else:
-                interleave_gpsimd(s - 1)
-            if s >= 3:
-                vector_tile(tile_step, tiles.start)
-            if s == 0:
-                transpose_step(2)
-                hidden(0, 1, all_slots, whole)
-                hidden_tile(1, 1)
-                hidden_tile(1, 0)
-            else:
-                hidden(s, 1, low_slots, whole)
-                transpose_step(s + 2)
-                hidden(s, 1, high_slots, whole)
-            scale_z(s + 2, low_tiles)
-            if s in (1, 2):
-                vector_tile(tile_step, tiles.stop - 1)
-            scale_z(s + 2, high_tiles)
-            if s == 0:
-                add_bias(1, 1)
-                add_bias(1, 0)
-            relu(s, 1, all_slots, whole)
-            if s >= 3:
-                output(s - 2, all_tiles)
-                store(s - 2, all_tiles)
-            interleave_tensor(s, *tensor_cols(s), parts=(0,))
-            hidden(s + 1, 0, low_slots, scalar_tokens(s + 1))
-            interleave_tensor(s, *tensor_cols(s), parts=(1,))
-            if s == 1:
-                vector_tile(2, 0)
-            if s == 2:
-                output(0, all_tiles)
-                store(0, all_tiles)
-            hidden(s + 1, 0, high_slots, scalar_tokens(s + 1))
+                gpsimd_planes(k - 1)
+            for j in steps(k + 1):
+                scale_z(k + 1, j, low_tiles)
+                scale_z(k + 1, j, high_tiles)
+            weave(spread(scalar_items(k), mix_items(k - 1)), vector_items(k), 2 * len(steps(k + 1)))
 
-        prev, last = STEPS - 2, STEPS - 1
-        last_tile = slice(ROWS - P, ROWS)
-        half = ROWS // 2
-        scalar_start(prev)
-        interleave_scalar(prev - 1, *rest_cols(prev - 1))
-        port_work(prev)
-        interleave_gpsimd(prev - 1)
-        hidden_tile(prev, 0)
-        hidden_tile(prev, 1)
-        add_bias(prev, 0)
-        add_bias(prev, 1)
-        hidden(prev, 1, all_slots, whole)
-        output(prev - 2, all_tiles)
-        store(prev - 2, all_tiles)
-        relu(prev, 1, all_slots, whole)
-        for i in range(SUB - 1):
-            vector_tile(last, i)
-        hidden(last, 0, all_slots, last_tile)
-        relu(last, 0, all_slots, last_tile)
-        interleave_scalar(prev, ROWS, ROWS + P)
-        interleave_tensor(prev, half, ROWS, parts=(0,))
-        hidden(last, 1, all_slots, whole)
-        interleave_tensor(prev, half, ROWS, parts=(1,))
-        interleave_tensor(prev, ROWS + P, COLS - P)
-        relu(last, 1, all_slots, whole)
-        copy_mixed(prev, half, ROWS)
-        copy_mixed(prev, ROWS + P, COLS - P)
-        interleave_scalar(last, ROWS - P, ROWS)
-        relu_in_place(prev, low_tiles)
-        quantize_h(prev - 1, 0, COLS)
-        output(prev - 1, all_tiles)
-        relu_in_place(last, range(SUB - 1))
-        interleave_vector(prev, COLS - P, COLS)
-        interleave_tensor(last, ROWS, ROWS + half)
-        copy_mixed(last, ROWS, ROWS + half)
-        interleave_vector(last, ROWS + half, COLS)
-        store(prev - 1, all_tiles)
-        quantize_h(prev, 0, COLS)
-        output(prev, all_tiles)
-        quantize_h(last, 0, ROWS)
-        quantize_h(last, ROWS + half, COLS)
-        output(last, high_tiles)
-        quantize_h(last, ROWS, ROWS + half)
-        store(prev, all_tiles)
+        prev, last = LAST - 1, LAST
+        items = mix_items(prev)
+        run(items[:1] + items[-1:] + items[1:-1])
+        quantize_z(last, 0, whole)
+        relu_in_place(prev)
+        quantize_gpsimd(prev - 1)
+        quantize_tiles(prev)
+        quantize_rest(prev - 1)
+        gpsimd_planes(prev)
+        run([(vector_tile, last, i) for i in all_tiles])
+        run(scalar_items(last))
+        output(prev - 1, low_tiles)
+        output(prev - 1, high_tiles)
+        bank = mix_products(last, 0, BANK_COLS)
+        interleave_scalar(last)
+        mix_copy(last, 0, BANK_COLS, bank)
+        relu_in_place(last)
+        quantize_rest(prev)
+        quantize_gpsimd(prev)
+        quantize_tiles(last)
+        quantize_rest(last)
+        output(prev, low_tiles)
+        output(prev, high_tiles)
         output(last, low_tiles)
-        store(last, high_tiles)
-        store(last, low_tiles)
+        output(last, high_tiles)

@@ -31,12 +31,13 @@ BATCHES = (
     + [(B - 1, 1, 0)]
 )
 LAST = len(BATCHES) - 1
-TILES = (3, 4, 3, 2, 3, 2, 2, 4, 4)
-DIRECT = (0, 0, 0, 0, 0, 0, 128, 384, 256)
-W3_CUT = 6
-G_NUM, G_DEN, G_LESS = 7, 8, 64
-FIRST_V = 6
+TILES = (3, 4, 3, 2, 3, 2, 3, 4, 4)
+DIRECT = 256
+W3_CUTS = (0, 3, 7, W3_PASSES)
+G_NUM, G_DEN = 13, 16
+FIRST_V = 4
 MIX_AT = 3
+CARRY = 2
 
 
 def tile_mlpmodelpredictor_pb_t_w8_kernel(
@@ -63,12 +64,10 @@ def tile_mlpmodelpredictor_pb_t_w8_kernel(
         w3_codes = keep.tile([P, W3_PASSES * O], U32, name="w3_codes", align_bytes=64)
         w3_exps = keep.tile([P, W3_PASSES * O], U8, name="w3_exps", align_bytes=64)
         gbuf = keep.tile([P, 3 * ROWS * PACK], BF16, name="gbuf", align_bytes=64)
-        tbuf = keep.tile([P, max(TILES) * P * PACK], BF16, name="tbuf", align_bytes=64)
 
-        w3_parts = ((0, W3_CUT), (W3_CUT, W3_PASSES))
         zbytes, zbuf, w3_raw = {}, {}, {}
         z_banks, z_codes, z_exps = {}, {}, {}
-        planes, pbuf, h_codes, h_exps = {}, {}, {}, {}
+        planes, pbuf, tbuf, h_codes, h_exps = {}, {}, {}, {}, {}
 
         def steps(k):
             return range(BATCHES[k][1])
@@ -93,8 +92,11 @@ def tile_mlpmodelpredictor_pb_t_w8_kernel(
             return work.tile(shape, BF16, name="planes", bufs=3)
 
         def load_w3(part):
-            lo, hi = w3_parts[part]
-            tile = plane_tile([P, hi - lo, PACK, O])
+            lo, hi = W3_CUTS[part : part + 2]
+            if part == 0:
+                tile = loads.tile([P, hi - lo, PACK, O], BF16, name="w3_first")
+            else:
+                tile = plane_tile([P, hi - lo, PACK, O])
             w3_raw[part] = tile
             nc.sync.dma_start(
                 out=tile[:].rearrange("p c t o -> p c (t o)"),
@@ -121,12 +123,13 @@ def tile_mlpmodelpredictor_pb_t_w8_kernel(
                 in_=sw1_scales[0, 4 * q : 4 * q + 4, :].bitcast(I32),
             )
         load_z(2, 0)
-        load_w1(1)
         load_w3(0)
+        load_w1(1)
+        load_w3(1)
         load_z(2, 1)
         load_z(3, 0)
         load_z(3, 1)
-        load_w3(1)
+        load_w3(2)
         load_z(4, 0)
         load_z(4, 1)
         nc.sync.dma_start(
@@ -233,8 +236,8 @@ def tile_mlpmodelpredictor_pb_t_w8_kernel(
             reads = TILES[k + 1] + len(steps(k - 1))
             if k + 2 <= LAST:
                 reads = reads + PACK * len(steps(k + 2))
-            fit = reads * ROWS * G_NUM // (G_DEN * PACK) - G_LESS
-            return plane_cols(k) - (plane_cols(k) - fit + 31) // 64 * 64
+            fit = reads * ROWS * G_NUM // (G_DEN * PACK)
+            return plane_cols(k) - (plane_cols(k) - fit + 63) // 64 * 64
 
         def rest_cols(k):
             return plane_cols(k) - gpsimd_cols(k)
@@ -290,11 +293,14 @@ def tile_mlpmodelpredictor_pb_t_w8_kernel(
 
         def vector_tile(k, i):
             j, g = steps(k).stop - 1, G - 1
+            if k not in tbuf:
+                tile = work.tile([P, TILES[k] * ROWS], BF16, name="tbuf", bufs=2, align_bytes=64)
+                tbuf[k] = tile
             bank = vector_bank([P, PACK, P])
             for t in range(PACK):
                 product(bank[:, t, :], k, j, g, t, slice(i * P, (i + 1) * P))
             nc.vector.tensor_tensor(
-                out=tbuf[:, i * ROWS : (i + 1) * ROWS].rearrange(
+                out=tbuf[k][:, i * ROWS : (i + 1) * ROWS].rearrange(
                     "p (c j t) -> p c t j", j=2, t=PACK
                 ),
                 in0=bank[:].rearrange("p t (c j) -> p c t j", j=2),
@@ -306,7 +312,7 @@ def tile_mlpmodelpredictor_pb_t_w8_kernel(
             )
 
         def relu_in_place(k):
-            cols = tbuf[:, 0 : TILES[k] * ROWS]
+            cols = tbuf[k][:]
             nc.vector.tensor_scalar(out=cols, in0=cols, scalar1=0.0, scalar2=None, op0=ALU.max)
 
         def copy_gpsimd(out, in_):
@@ -315,9 +321,10 @@ def tile_mlpmodelpredictor_pb_t_w8_kernel(
             )
 
         def gpsimd_w3(part):
-            lo, hi = w3_parts[part]
+            lo, hi = W3_CUTS[part : part + 2]
+            at = lo if part < 2 else 0
             copy_gpsimd(
-                out=gbuf[:, 0 : (hi - lo) * O * PACK].rearrange(
+                out=gbuf[:, at * ROWS : (at + hi - lo) * ROWS].rearrange(
                     "p (c o t) -> p c o t", o=O, t=PACK
                 ),
                 in_=w3_raw[part][:].rearrange("p c t o -> p c o t"),
@@ -327,18 +334,17 @@ def tile_mlpmodelpredictor_pb_t_w8_kernel(
             n = gpsimd_cols(k)
             copy_gpsimd(
                 out=gbuf[:, 0 : n * PACK].rearrange("p (n t) -> p n t", t=PACK),
-                in_=planes_of(k, 0, n),
+                in_=planes_of(k, rest_cols(k), plane_cols(k)),
             )
 
         def mix_products(k, lo, hi):
             bank = scalar_bank([P, BANK_COLS, PACK], BF16)
-            at = gpsimd_cols(k)
             for c in range(lo, hi, P):
                 end = min(hi, c + P)
                 nc.tensor.matmul(
                     bank[:, c - lo : end - lo, :],
                     lhsT=ident_b[:],
-                    rhs=planes_of(k, at + c, at + end),
+                    rhs=planes_of(k, c, end),
                     start=True,
                     stop=True,
                 )
@@ -353,18 +359,14 @@ def tile_mlpmodelpredictor_pb_t_w8_kernel(
         def mix(k, lo, hi):
             mix_copy(k, lo, hi, mix_products(k, lo, hi))
 
-        def interleave_scalar(k):
-            lo, hi = rest_cols(k) - DIRECT[k], rest_cols(k)
-            at = gpsimd_cols(k)
+        def interleave_scalar(k, lo, hi):
             nc.scalar.copy(
                 out=rest_of(k, lo, hi).rearrange("p (n t) -> p n t", t=PACK),
-                in_=planes_of(k, at + lo, at + hi),
+                in_=planes_of(k, lo, hi),
             )
 
-        def mix_items(k):
-            end = rest_cols(k) - DIRECT[k]
-            items = [(mix, k, c, min(end, c + BANK_COLS)) for c in range(0, end, BANK_COLS)]
-            return items + ([(interleave_scalar, k)] if DIRECT[k] else [])
+        def mix_items(k, end):
+            return [(mix, k, c, min(end, c + BANK_COLS)) for c in range(0, end, BANK_COLS)]
 
         def quantize(codes, exps, src, cols):
             at = 0
@@ -386,26 +388,26 @@ def tile_mlpmodelpredictor_pb_t_w8_kernel(
             quantize(h_codes[k][:, lo:hi], h_exps[k][:, lo:hi], src, hi - lo)
 
         def quantize_tiles(k):
-            quantize_h(k, tbuf, plane_cols(k), len(steps(k)) * H)
+            quantize_h(k, tbuf[k], plane_cols(k), len(steps(k)) * H)
 
         def quantize_rest(k):
-            quantize_h(k, pbuf[k], gpsimd_cols(k), plane_cols(k))
+            quantize_h(k, pbuf[k], 0, rest_cols(k))
 
         def quantize_gpsimd(k):
-            quantize_h(k, gbuf, 0, gpsimd_cols(k))
+            quantize_h(k, gbuf, rest_cols(k), plane_cols(k))
 
         def quantize_w3(part):
-            lo, hi = w3_parts[part]
+            lo, hi = (0, W3_CUTS[2]) if part == 0 else W3_CUTS[2:]
             quantize(w3_codes[:, lo * O :], w3_exps[:, lo * O :], gbuf, (hi - lo) * O)
 
-        def output(k, tiles):
-            b, datasets, hf = BATCHES[k]
+        def output(k, js, tiles):
+            b, datasets, hf = BATCHES[k][0] + js.start, len(js), BATCHES[k][2]
             n, wide = len(tiles), datasets * O
             bank = vector_bank([P, n, wide])
             for i in tiles:
-                for j in steps(k):
+                for j in range(datasets):
                     for g in range(G):
-                        at = column(k, j, g, i)
+                        at = column(k, js.start + j, g, i)
                         chans = slice(((b + j) * G + g) * O, ((b + j) * G + g + 1) * O)
                         nc.tensor.matmul_mx(
                             out=bank[:, i - tiles.start, j * O : (j + 1) * O],
@@ -442,9 +444,9 @@ def tile_mlpmodelpredictor_pb_t_w8_kernel(
         def vector_items(k):
             items = []
             if k == 2:
-                items = [(output, 0, all_tiles)]
+                items = [(output, 0, steps(0), all_tiles)]
             if k > 2:
-                items = [(output, k - 2, low_tiles), (output, k - 2, high_tiles)]
+                items = [(output, k - 2, steps(k - 2), tiles) for tiles in (low_tiles, high_tiles)]
             return items + [(vector_tile, k, i) for i in range(TILES[k])]
 
         def weave(s_items, v_items, z_count):
@@ -501,66 +503,78 @@ def tile_mlpmodelpredictor_pb_t_w8_kernel(
         widen_part(2, 1)
         permute_w1_scales(1)
         gpsimd_w3(0)
+        gpsimd_w3(1)
         transpose_z(1, 0, high_tiles)
         scale_z(1, 0, low_tiles)
         transpose_z(1, 1, high_tiles)
         scale_z(1, 1, low_tiles)
         scale_z(1, 0, high_tiles)
         scale_z(1, 1, high_tiles)
-        run(relu_items(0, 0, 0, right))
-        run(scalar_items(0)[PACK:])
+        run(relu_items(0, 0, 0, right) + scalar_items(0)[PACK:])
         run(vector_items(0))
+        carried = []
 
+        prev, last = LAST - 1, LAST
         for k in range(1, LAST):
-            for j in steps(k + 1):
-                transpose_z(k + 1, j, low_tiles)
-                transpose_z(k + 1, j, high_tiles)
-            if k + 2 <= LAST:
-                widen_part(k + 2, 0)
-                widen_part(k + 2, 1)
+            mixes = mix_items(k - 1, rest_cols(k - 1))
+            for j in range(2):
+                if j in steps(k + 1):
+                    transpose_z(k + 1, j, low_tiles)
+                    transpose_z(k + 1, j, high_tiles)
+                if k + 2 <= LAST:
+                    widen_part(k + 2, j)
+                if j == 0:
+                    run(carried + mixes[:1])
             quantize_z(k, 0, whole)
             relu_in_place(k - 1)
             if k >= 2:
                 quantize_rest(k - 2)
                 quantize_tiles(k - 1)
+            if k == 1:
+                quantize_z(k, 1, whole)
             if k <= 2:
                 quantize_w3(k - 1)
             else:
                 quantize_gpsimd(k - 2)
             if k == 1:
                 quantize_tiles(0)
-            quantize_z(k, 1, whole)
+            if k > 1:
+                quantize_z(k, 1, whole)
             if k == 1:
-                gpsimd_w3(1)
+                gpsimd_w3(2)
             else:
                 gpsimd_planes(k - 1)
             for j in steps(k + 1):
                 scale_z(k + 1, j, low_tiles)
                 scale_z(k + 1, j, high_tiles)
-            weave(spread(scalar_items(k), mix_items(k - 1)), vector_items(k), 2 * len(steps(k + 1)))
+            own = scalar_items(k)
+            cut = len(own) - (CARRY if k < prev else 0)
+            carried = own[cut:]
+            items = spread(own[:cut], mixes[1:])
+            weave(items, vector_items(k), 2 * len(steps(k + 1)))
 
-        prev, last = LAST - 1, LAST
-        items = mix_items(prev)
-        run(items[:1] + items[-1:] + items[1:-1])
+        mixes = mix_items(prev, rest_cols(prev) - DIRECT)
+        run(mixes[:1])
         quantize_z(last, 0, whole)
         relu_in_place(prev)
+        quantize_rest(prev - 1)
         quantize_gpsimd(prev - 1)
         quantize_tiles(prev)
-        quantize_rest(prev - 1)
         gpsimd_planes(prev)
         run([(vector_tile, last, i) for i in all_tiles])
-        run(scalar_items(last))
-        output(prev - 1, low_tiles)
-        output(prev - 1, high_tiles)
-        bank = mix_products(last, 0, BANK_COLS)
-        interleave_scalar(last)
-        mix_copy(last, 0, BANK_COLS, bank)
+        interleave_scalar(prev, rest_cols(prev) - DIRECT, rest_cols(prev))
+        run(mixes[1:2] + scalar_items(last))
+        output(prev - 1, steps(prev - 1), low_tiles)
+        output(prev - 1, steps(prev - 1), high_tiles)
+        run(mixes[2:])
+        interleave_scalar(last, BANK_COLS, ROWS)
+        mix(last, 0, BANK_COLS)
         relu_in_place(last)
-        quantize_rest(prev)
         quantize_gpsimd(prev)
+        quantize_rest(prev)
         quantize_tiles(last)
         quantize_rest(last)
-        output(prev, low_tiles)
-        output(prev, high_tiles)
-        output(last, low_tiles)
-        output(last, high_tiles)
+        output(prev, steps(prev), low_tiles)
+        output(prev, steps(prev), high_tiles)
+        output(last, steps(last), low_tiles)
+        output(last, steps(last), high_tiles)

@@ -31,13 +31,17 @@ BATCHES = (
     + [(B - 1, 1, 0)]
 )
 LAST = len(BATCHES) - 1
-TILES = (3, 4, 3, 2, 3, 2, 3, 4, 4)
+TILES = (2, 4, 3, 2, 3, 2, 3, 4, 4)
 DIRECT = 256
+MIXED = (640, 512, 512, 512, 512, 512, 512)
+DIRECT_AT = 5
+SPLIT = 0
 W3_CUTS = (0, 3, 7, W3_PASSES)
-G_NUM, G_DEN = 13, 16
-FIRST_V = 4
+G_NUM, G_DEN = 55, 64
+FIRST_V = 1
 MIX_AT = 3
 CARRY = 2
+GBUF_COLS = 1408
 
 
 def tile_mlpmodelpredictor_pb_t_w8_kernel(
@@ -63,11 +67,14 @@ def tile_mlpmodelpredictor_pb_t_w8_kernel(
         b3_rows = keep.tile([P, B * O], BF16, name="b3_rows")
         w3_codes = keep.tile([P, W3_PASSES * O], U32, name="w3_codes", align_bytes=64)
         w3_exps = keep.tile([P, W3_PASSES * O], U8, name="w3_exps", align_bytes=64)
-        gbuf = keep.tile([P, 3 * ROWS * PACK], BF16, name="gbuf", align_bytes=64)
+        gbuf = []
+        for i in range(2):
+            tile = keep.tile([P, GBUF_COLS * PACK], BF16, name="gbuf%d" % i, align_bytes=64)
+            gbuf.append(tile)
 
         zbytes, zbuf, w3_raw = {}, {}, {}
         z_banks, z_codes, z_exps = {}, {}, {}
-        planes, pbuf, tbuf, h_codes, h_exps = {}, {}, {}, {}, {}
+        planes, pbuf, h_codes, h_exps = {}, {}, {}, {}
 
         def steps(k):
             return range(BATCHES[k][1])
@@ -147,8 +154,8 @@ def tile_mlpmodelpredictor_pb_t_w8_kernel(
 
         def permute_w1_codes(g):
             nc.scalar.copy(
-                out=w1_codes[:, g],
-                in_=w1_raw[:, g].bitcast(U32).rearrange("p (m t) -> p t m", t=PACK),
+                out=w1_codes[:, g].rearrange("p t (c i) -> p c t i", i=PACK),
+                in_=w1_raw[:, g].bitcast(U32).rearrange("p (c i t) -> p c t i", i=PACK, t=PACK),
             )
 
         def permute_w1_scales(g):
@@ -160,7 +167,7 @@ def tile_mlpmodelpredictor_pb_t_w8_kernel(
         def new_zbuf():
             return work.tile([P, 2 * ROWS * PACK], BF16, name="zbuf", bufs=3, align_bytes=64)
 
-        zbuf[0] = gbuf
+        zbuf[0] = gbuf[0]
         first_pair = new_zbuf()
         zbuf[1] = new_zbuf()
 
@@ -237,7 +244,7 @@ def tile_mlpmodelpredictor_pb_t_w8_kernel(
             if k + 2 <= LAST:
                 reads = reads + PACK * len(steps(k + 2))
             fit = reads * ROWS * G_NUM // (G_DEN * PACK)
-            return plane_cols(k) - (plane_cols(k) - fit + 63) // 64 * 64
+            return fit // 64 * 64
 
         def rest_cols(k):
             return plane_cols(k) - gpsimd_cols(k)
@@ -291,16 +298,16 @@ def tile_mlpmodelpredictor_pb_t_w8_kernel(
                         items.extend(relu_items(k, j, g, slice(taken * P, ROWS)))
             return items
 
+        def tile_buf(k):
+            return zbuf[LAST - 1] if k == LAST else gbuf[(k + 1) % 2]
+
         def vector_tile(k, i):
             j, g = steps(k).stop - 1, G - 1
-            if k not in tbuf:
-                tile = work.tile([P, TILES[k] * ROWS], BF16, name="tbuf", bufs=2, align_bytes=64)
-                tbuf[k] = tile
             bank = vector_bank([P, PACK, P])
             for t in range(PACK):
                 product(bank[:, t, :], k, j, g, t, slice(i * P, (i + 1) * P))
             nc.vector.tensor_tensor(
-                out=tbuf[k][:, i * ROWS : (i + 1) * ROWS].rearrange(
+                out=tile_buf(k)[:, i * ROWS : (i + 1) * ROWS].rearrange(
                     "p (c j t) -> p c t j", j=2, t=PACK
                 ),
                 in0=bank[:].rearrange("p t (c j) -> p c t j", j=2),
@@ -312,7 +319,7 @@ def tile_mlpmodelpredictor_pb_t_w8_kernel(
             )
 
         def relu_in_place(k):
-            cols = tbuf[k][:]
+            cols = tile_buf(k)[:, 0 : TILES[k] * ROWS]
             nc.vector.tensor_scalar(out=cols, in0=cols, scalar1=0.0, scalar2=None, op0=ALU.max)
 
         def copy_gpsimd(out, in_):
@@ -324,7 +331,7 @@ def tile_mlpmodelpredictor_pb_t_w8_kernel(
             lo, hi = W3_CUTS[part : part + 2]
             at = lo if part < 2 else 0
             copy_gpsimd(
-                out=gbuf[:, at * ROWS : (at + hi - lo) * ROWS].rearrange(
+                out=gbuf[part // 2][:, at * ROWS : (at + hi - lo) * ROWS].rearrange(
                     "p (c o t) -> p c o t", o=O, t=PACK
                 ),
                 in_=w3_raw[part][:].rearrange("p c t o -> p c o t"),
@@ -333,8 +340,8 @@ def tile_mlpmodelpredictor_pb_t_w8_kernel(
         def gpsimd_planes(k):
             n = gpsimd_cols(k)
             copy_gpsimd(
-                out=gbuf[:, 0 : n * PACK].rearrange("p (n t) -> p n t", t=PACK),
-                in_=planes_of(k, rest_cols(k), plane_cols(k)),
+                out=gbuf[(k + 1) % 2][:, 0 : n * PACK].rearrange("p (c i t) -> p c t i", i=2, t=PACK),
+                in_=planes[k][:, :, rest_cols(k) :].rearrange("p t (c i) -> p c t i", i=2),
             )
 
         def mix_products(k, lo, hi):
@@ -388,17 +395,27 @@ def tile_mlpmodelpredictor_pb_t_w8_kernel(
             quantize(h_codes[k][:, lo:hi], h_exps[k][:, lo:hi], src, hi - lo)
 
         def quantize_tiles(k):
-            quantize_h(k, tbuf[k], plane_cols(k), len(steps(k)) * H)
+            quantize_h(k, tile_buf(k), plane_cols(k), len(steps(k)) * H)
 
         def quantize_rest(k):
             quantize_h(k, pbuf[k], 0, rest_cols(k))
 
-        def quantize_gpsimd(k):
-            quantize_h(k, gbuf, rest_cols(k), plane_cols(k))
+        def halves(cols):
+            n = max(w for w in QUANT_COLS if w <= cols)
+            return (n, cols), (0, n)
 
-        def quantize_w3(part):
-            lo, hi = (0, W3_CUTS[2]) if part == 0 else W3_CUTS[2:]
-            quantize(w3_codes[:, lo * O :], w3_exps[:, lo * O :], gbuf, (hi - lo) * O)
+        def quantize_gpsimd(k, piece):
+            lo, hi = halves(gpsimd_cols(k))[piece]
+            if lo == hi:
+                return
+            at = rest_cols(k)
+            quantize_h(k, gbuf[(k + 1) % 2][:, lo * PACK :], at + lo, at + hi)
+
+        def quantize_w3(part, piece):
+            first, end = (0, W3_CUTS[2]) if part == 0 else W3_CUTS[2:]
+            lo, hi = halves((end - first) * O)[piece]
+            at = first * O + lo
+            quantize(w3_codes[:, at:], w3_exps[:, at:], gbuf[part][:, lo * PACK :], hi - lo)
 
         def output(k, js, tiles):
             b, datasets, hf = BATCHES[k][0] + js.start, len(js), BATCHES[k][2]
@@ -449,7 +466,7 @@ def tile_mlpmodelpredictor_pb_t_w8_kernel(
                 items = [(output, k - 2, steps(k - 2), tiles) for tiles in (low_tiles, high_tiles)]
             return items + [(vector_tile, k, i) for i in range(TILES[k])]
 
-        def weave(s_items, v_items, z_count):
+        def weave(s_items, v_items, z_count, first):
             def freed(j):
                 older = j + z_count - 4
                 if older < 0:
@@ -458,7 +475,7 @@ def tile_mlpmodelpredictor_pb_t_w8_kernel(
 
             done = 0
             for x, item in enumerate(s_items):
-                while done < len(v_items) and x >= FIRST_V + max(freed(done), done):
+                while done < len(v_items) and x >= first + max(freed(done), done):
                     run(v_items[done : done + 1])
                     done = done + 1
                 run([item])
@@ -516,30 +533,28 @@ def tile_mlpmodelpredictor_pb_t_w8_kernel(
 
         prev, last = LAST - 1, LAST
         for k in range(1, LAST):
-            mixes = mix_items(k - 1, rest_cols(k - 1))
+            end = min(rest_cols(k - 1), MIXED[k - 1])
+            mixes = mix_items(k - 1, end)
             for j in range(2):
                 if j in steps(k + 1):
                     transpose_z(k + 1, j, low_tiles)
                     transpose_z(k + 1, j, high_tiles)
                 if k + 2 <= LAST:
                     widen_part(k + 2, j)
-                if j == 0:
+                if j == SPLIT:
                     run(carried + mixes[:1])
             quantize_z(k, 0, whole)
             relu_in_place(k - 1)
             if k >= 2:
                 quantize_rest(k - 2)
-                quantize_tiles(k - 1)
-            if k == 1:
-                quantize_z(k, 1, whole)
-            if k <= 2:
-                quantize_w3(k - 1)
-            else:
-                quantize_gpsimd(k - 2)
-            if k == 1:
-                quantize_tiles(0)
-            if k > 1:
-                quantize_z(k, 1, whole)
+            quantize_z(k, 1, whole)
+            for piece in range(2):
+                if piece == 1:
+                    quantize_tiles(k - 1)
+                if k <= 2:
+                    quantize_w3(k - 1, piece)
+                else:
+                    quantize_gpsimd(k - 2, piece)
             if k == 1:
                 gpsimd_w3(2)
             else:
@@ -551,26 +566,30 @@ def tile_mlpmodelpredictor_pb_t_w8_kernel(
             cut = len(own) - (CARRY if k < prev else 0)
             carried = own[cut:]
             items = spread(own[:cut], mixes[1:])
-            weave(items, vector_items(k), 2 * len(steps(k + 1)))
+            if end < rest_cols(k - 1):
+                items.insert(DIRECT_AT, (interleave_scalar, k - 1, end, rest_cols(k - 1)))
+            weave(items, vector_items(k), 2 * len(steps(k + 1)), TILES[k - 1] + FIRST_V)
 
         mixes = mix_items(prev, rest_cols(prev) - DIRECT)
         run(mixes[:1])
         quantize_z(last, 0, whole)
         relu_in_place(prev)
         quantize_rest(prev - 1)
-        quantize_gpsimd(prev - 1)
+        quantize_gpsimd(prev - 1, 0)
         quantize_tiles(prev)
+        quantize_gpsimd(prev - 1, 1)
         gpsimd_planes(prev)
         run([(vector_tile, last, i) for i in all_tiles])
         interleave_scalar(prev, rest_cols(prev) - DIRECT, rest_cols(prev))
-        run(mixes[1:2] + scalar_items(last))
+        run(scalar_items(last))
         output(prev - 1, steps(prev - 1), low_tiles)
         output(prev - 1, steps(prev - 1), high_tiles)
-        run(mixes[2:])
         interleave_scalar(last, BANK_COLS, ROWS)
+        run(mixes[1:])
         mix(last, 0, BANK_COLS)
         relu_in_place(last)
-        quantize_gpsimd(prev)
+        quantize_gpsimd(prev, 0)
+        quantize_gpsimd(prev, 1)
         quantize_rest(prev)
         quantize_tiles(last)
         quantize_rest(last)

from contextlib import ExitStack

import concourse.mybir as mybir
from concourse.masks import make_identity

T, B, R, H, O = 1024, 8, 512, 1024, 128
FLOPS = 2 * T * B * (R * H + H * O)

F32 = mybir.dt.float32
BF16 = mybir.dt.bfloat16
U32 = mybir.dt.uint32
I32 = mybir.dt.int32
U8 = mybir.dt.uint8
FP8 = mybir.dt.float8_e4m3fn
FP8X4 = mybir.dt.float8_e4m3fn_x4
ALU = mybir.AluOpType
ACT = mybir.ActivationFunctionType

P = 128
PACK = 4
G = H // (P * PACK)
ROWS = 512
SUB = ROWS // P
W3_PASSES = B * G
BANK_COLS = 256
QUANT_COLS = (1024, 512, 384, 256, 128, 64)

BATCHES = (
    [(0, 1, 0), (1, 2, 0), (0, 2, 1)]
    + [(b, 2, 1 - b % 2) for b in range(2, B - 1)]
    + [(B - 1, 1, 0)]
)
LAST = len(BATCHES) - 1
TILES = (2, 4, 3, 2, 3, 2, 3, 4, 4)
DIRECT = 256
MIXED = (640, 512, 512, 512, 512, 512, 512)
DIRECT_AT = 5
SPLIT = 0
W3_CUTS = (0, 3, 7, W3_PASSES)
G_NUM, G_DEN = 55, 64
FIRST_V = 1
MIX_AT = 3
CARRY = 2
GBUF_COLS = 1408


def tile_mlpmodelpredictor_pb_t_w8_kernel(
    tc, z2_bytes, z2_scale, sw1_words, sw1_scales, b2, w3, b3, out
):
    nc = tc.nc
    with ExitStack() as ctx:
        keep = ctx.enter_context(tc.tile_pool(name="keep", bufs=1))
        loads = ctx.enter_context(tc.tile_pool(name="loads", bufs=1))
        work = ctx.enter_context(tc.tile_pool(name="work", bufs=2))
        psum = ctx.enter_context(tc.psum_pool(name="psum", bufs=1))
        ctx.enter_context(tc.manual_schedule())

        ident_f = keep.tile([P, P], F32, name="ident_f")
        ident_b = keep.tile([P, P], BF16, name="ident_b")
        kscale = keep.tile([P, PACK], F32, name="kscale")
        w1_raw = keep.tile([P, G, H // G], I32, name="w1_raw", align_bytes=64)
        w1_codes = keep.tile([P, G, PACK, P], U32, name="w1_codes", align_bytes=64)
        w1s_raw = keep.tile([P, H], U8, name="w1s_raw", align_bytes=64)
        w1_scales = keep.tile([P, G, PACK, P], U8, name="w1_scales", align_bytes=64)
        b2_rows = keep.tile([P, H // G], BF16, name="b2_rows")
        b2_cols = keep.tile([P, B * G, PACK], BF16, name="b2_cols")
        b3_rows = keep.tile([P, B * O], BF16, name="b3_rows")
        w3_codes = keep.tile([P, W3_PASSES * O], U32, name="w3_codes", align_bytes=64)
        w3_exps = keep.tile([P, W3_PASSES * O], U8, name="w3_exps", align_bytes=64)
        gbuf = []
        for i in range(2):
            tile = keep.tile([P, GBUF_COLS * PACK], BF16, name="gbuf%d" % i, align_bytes=64)
            gbuf.append(tile)

        zbytes, zbuf, w3_raw = {}, {}, {}
        z_banks, z_codes, z_exps = {}, {}, {}
        planes, pbuf, h_codes, h_exps = {}, {}, {}, {}

        def steps(k):
            return range(BATCHES[k][1])

        def load_z(k, part):
            b, n, hf = BATCHES[k]
            tile = loads.tile([P, 2 * n * R], U8, name="zb%d_%d" % (k, part), align_bytes=64)
            zbytes[k, part] = tile
            row = hf * ROWS + part * 2 * P
            nc.sync.dma_start(
                out=tile[:].rearrange("p (i k) -> p i k", i=2),
                in_=z2_bytes[row : row + 2 * P, b : b + n, :].rearrange(
                    "(i p) b k -> p i (b k)", p=P
                ),
            )

        def load_w1(g):
            words = sw1_words[0].rearrange("p n t -> p (n t)").bitcast(I32)
            nc.sync.dma_start(out=w1_raw[:, g, :], in_=words[:, g * H // G : (g + 1) * H // G])

        def plane_tile(shape):
            return work.tile(shape, BF16, name="planes", bufs=3)

        def load_w3(part):
            lo, hi = W3_CUTS[part : part + 2]
            if part == 0:
                tile = loads.tile([P, hi - lo, PACK, O], BF16, name="w3_first")
            else:
                tile = plane_tile([P, hi - lo, PACK, O])
            w3_raw[part] = tile
            nc.sync.dma_start(
                out=tile[:].rearrange("p c t o -> p c (t o)"),
                in_=w3.rearrange("b (g p t) o -> p (b g) (t o)", p=P, t=PACK)[:, lo:hi],
            )

        nc.vector.memset(w1s_raw[:].bitcast(I32), 0)
        nc.vector.memset(b2_rows[:], 0.0)
        make_identity(nc, ident_f[:])
        load_z(0, 0)
        load_z(0, 1)
        nc.scalar.dma_start(
            out=kscale[:], in_=z2_scale.rearrange("a c (p t) -> p (a c t)", t=PACK)
        )
        load_z(1, 0)
        load_w1(0)
        nc.sync.dma_start(
            out=b2_rows[0 : B * G, :], in_=b2.rearrange("b (g n) -> (b g) n", g=G)
        )
        load_z(1, 1)
        for q in range(4):
            nc.sync.dma_start(
                out=w1s_raw[32 * q : 32 * q + 4, :].bitcast(I32),
                in_=sw1_scales[0, 4 * q : 4 * q + 4, :].bitcast(I32),
            )
        load_z(2, 0)
        load_w3(0)
        load_w1(1)
        load_w3(1)
        load_z(2, 1)
        load_z(3, 0)
        load_z(3, 1)
        load_w3(2)
        load_z(4, 0)
        load_z(4, 1)
        nc.sync.dma_start(
            out=b3_rows[:], in_=b3.rearrange("b o -> (b o)").partition_broadcast(P)
        )
        for k in range(5, LAST + 1):
            load_z(k, 0)
            load_z(k, 1)

        def scalar_bank(shape, dtype):
            return psum.tile(shape, dtype, name="sbank", bufs=4)

        def vector_bank(shape):
            return psum.tile(shape, F32, name="vbank", bufs=4)

        def permute_w1_codes(g):
            nc.scalar.copy(
                out=w1_codes[:, g].rearrange("p t (c i) -> p c t i", i=PACK),
                in_=w1_raw[:, g].bitcast(U32).rearrange("p (c i t) -> p c t i", i=PACK, t=PACK),
            )

        def permute_w1_scales(g):
            cols = slice(g * H // G, (g + 1) * H // G)
            nc.vector.tensor_copy(
                out=w1_scales[:, g], in_=w1s_raw[:, cols].rearrange("p (m t) -> p t m", t=PACK)
            )

        def new_zbuf():
            return work.tile([P, 2 * ROWS * PACK], BF16, name="zbuf", bufs=3, align_bytes=64)

        zbuf[0] = gbuf[0]
        first_pair = new_zbuf()
        zbuf[1] = new_zbuf()

        def widened(k):
            if k == 1:
                return first_pair
            if k not in zbuf:
                zbuf[k] = new_zbuf()
            return zbuf[k]

        def widen_z(k, part, copy, lo, hi):
            at = part * 2 * len(steps(k)) * R
            copy(
                out=widened(k)[:, at + lo : at + hi],
                in_=zbytes[k, part][:, lo:hi].bitcast(FP8),
            )

        def widen_part(k, part):
            widen_z(k, part, nc.scalar.copy, 0, 2 * len(steps(k)) * R)

        def transpose_z(k, j, tiles):
            bank = vector_bank([P, 2, len(tiles), P])
            z_banks[k, j, tiles.start] = bank
            for i in tiles:
                at = (len(steps(k)) * i + j) * R
                words = widened(k)[:, at : at + R].bitcast(F32)
                for u in range(2):
                    nc.tensor.transpose(bank[:, u, i - tiles.start, :], words[:, u::2], ident_f[:])

        def scale_z(k, j, tiles):
            at = j * ROWS * PACK
            nc.vector.tensor_tensor(
                out=zbuf[k][:, at + tiles.start * R : at + tiles.stop * R].rearrange(
                    "p (n u e) -> p n u e", u=2, e=2
                ),
                in0=z_banks[k, j, tiles.start][:]
                .rearrange("p u i r -> p (u i r)")
                .bitcast(BF16)
                .rearrange("p (u n e) -> p n u e", u=2, e=2),
                in1=kscale[:]
                .rearrange("p (u e) -> p u e", e=2)
                .unsqueeze(1)
                .to_broadcast([P, len(tiles) * P, 2, 2]),
                op=ALU.mult,
            )

        def quantize_z(k, j, cols):
            if (k, j) not in z_codes:
                codes = work.tile([P, ROWS], U32, name="zcodes", bufs=4, align_bytes=64)
                exps = work.tile([P, ROWS], U8, name="zexp", bufs=4, align_bytes=64)
                z_codes[k, j], z_exps[k, j] = codes, exps
            at = j * ROWS
            nc.vector.quantize_mx(
                out=z_codes[k, j][:, cols].bitcast(FP8X4),
                scales=z_exps[k, j][:, cols],
                in_=zbuf[k][:, (at + cols.start) * PACK : (at + cols.stop) * PACK],
            )

        def plane_cols(k):
            return len(steps(k)) * H - TILES[k] * P

        def column(k, j, g, i):
            group = G * j + g
            if (group + 1) * ROWS <= plane_cols(k):
                return group * ROWS + i * P
            if i < TILES[k]:
                return plane_cols(k) + i * P
            return group * ROWS + (i - TILES[k]) * P

        def gpsimd_cols(k):
            if k in (0, LAST):
                return 0
            reads = TILES[k + 1] + len(steps(k - 1))
            if k + 2 <= LAST:
                reads = reads + PACK * len(steps(k + 2))
            fit = reads * ROWS * G_NUM // (G_DEN * PACK)
            return fit // 64 * 64

        def rest_cols(k):
            return plane_cols(k) - gpsimd_cols(k)

        def rest_of(k, lo, hi):
            if k not in pbuf:
                tile = work.tile([P, rest_cols(k) * PACK], BF16, name="pbuf", bufs=2, align_bytes=64)
                pbuf[k] = tile
            return pbuf[k][:, lo * PACK : hi * PACK]

        def planes_of(k, lo, hi):
            return planes[k][:, :, lo:hi].rearrange("p t n -> p n t")

        def product(dst, k, j, g, t, tokens):
            nc.tensor.matmul_mx(
                out=dst,
                lhsT=w1_codes[:, g, t, :].bitcast(FP8X4),
                lhsT_scale=w1_scales[:, g, t, :],
                rhs=z_codes[k, j][:, tokens].bitcast(FP8X4),
                rhs_scale=z_exps[k, j][:, tokens],
                start=True,
                stop=True,
            )

        def relu_bank(k, j, g, slots, tokens):
            if k not in planes:
                planes[k] = plane_tile([P, PACK, plane_cols(k)])
            n = tokens.stop - tokens.start
            bank = scalar_bank([P, len(slots), n], F32)
            for t in slots:
                product(bank[:, t - slots.start, :], k, j, g, t, tokens)
            at = column(k, j, g, tokens.start // P)
            for t in slots:
                nc.scalar.activation(
                    out=planes[k][:, t, at : at + n],
                    in_=bank[:, t - slots.start, :],
                    func=ACT.Relu,
                    bias=b2_cols[:, (BATCHES[k][0] + j) * G + g, t : t + 1],
                )

        def relu_items(k, j, g, tokens):
            per = ROWS // (tokens.stop - tokens.start)
            return [(relu_bank, k, j, g, range(t, t + per), tokens) for t in range(0, PACK, per)]

        def scalar_items(k):
            items = []
            for j in steps(k):
                for g in range(G):
                    taken = TILES[k] if (j, g) == (steps(k).stop - 1, G - 1) else 0
                    if taken < SUB:
                        items.extend(relu_items(k, j, g, slice(taken * P, ROWS)))
            return items

        def tile_buf(k):
            return zbuf[LAST - 1] if k == LAST else gbuf[(k + 1) % 2]

        def vector_tile(k, i):
            j, g = steps(k).stop - 1, G - 1
            bank = vector_bank([P, PACK, P])
            for t in range(PACK):
                product(bank[:, t, :], k, j, g, t, slice(i * P, (i + 1) * P))
            nc.vector.tensor_tensor(
                out=tile_buf(k)[:, i * ROWS : (i + 1) * ROWS].rearrange(
                    "p (c j t) -> p c t j", j=2, t=PACK
                ),
                in0=bank[:].rearrange("p t (c j) -> p c t j", j=2),
                in1=b2_cols[:, (BATCHES[k][0] + j) * G + g, :]
                .unsqueeze(1)
                .unsqueeze(3)
                .to_broadcast([P, P // 2, PACK, 2]),
                op=ALU.add,
            )

        def relu_in_place(k):
            cols = tile_buf(k)[:, 0 : TILES[k] * ROWS]
            nc.vector.tensor_scalar(out=cols, in0=cols, scalar1=0.0, scalar2=None, op0=ALU.max)

        def copy_gpsimd(out, in_):
            nc.gpsimd.tensor_scalar(
                out=out, in0=in_, scalar1=1.0, scalar2=0.0, op0=ALU.mult, op1=ALU.add
            )

        def gpsimd_w3(part):
            lo, hi = W3_CUTS[part : part + 2]
            at = lo if part < 2 else 0
            copy_gpsimd(
                out=gbuf[part // 2][:, at * ROWS : (at + hi - lo) * ROWS].rearrange(
                    "p (c o t) -> p c o t", o=O, t=PACK
                ),
                in_=w3_raw[part][:].rearrange("p c t o -> p c o t"),
            )

        def gpsimd_planes(k):
            n = gpsimd_cols(k)
            copy_gpsimd(
                out=gbuf[(k + 1) % 2][:, 0 : n * PACK].rearrange("p (c i t) -> p c t i", i=2, t=PACK),
                in_=planes[k][:, :, rest_cols(k) :].rearrange("p t (c i) -> p c t i", i=2),
            )

        def mix_products(k, lo, hi):
            bank = scalar_bank([P, BANK_COLS, PACK], BF16)
            for c in range(lo, hi, P):
                end = min(hi, c + P)
                nc.tensor.matmul(
                    bank[:, c - lo : end - lo, :],
                    lhsT=ident_b[:],
                    rhs=planes_of(k, c, end),
                    start=True,
                    stop=True,
                )
            return bank

        def mix_copy(k, lo, hi, bank):
            nc.scalar.copy(
                out=rest_of(k, lo, hi).bitcast(F32),
                in_=bank[:, 0 : hi - lo, :].rearrange("p n t -> p (n t)").bitcast(F32),
            )

        def mix(k, lo, hi):
            mix_copy(k, lo, hi, mix_products(k, lo, hi))

        def interleave_scalar(k, lo, hi):
            nc.scalar.copy(
                out=rest_of(k, lo, hi).rearrange("p (n t) -> p n t", t=PACK),
                in_=planes_of(k, lo, hi),
            )

        def mix_items(k, end):
            return [(mix, k, c, min(end, c + BANK_COLS)) for c in range(0, end, BANK_COLS)]

        def quantize(codes, exps, src, cols):
            at = 0
            while at < cols:
                n = max(w for w in QUANT_COLS if w <= cols - at)
                nc.vector.quantize_mx(
                    out=codes[:, at : at + n].bitcast(FP8X4),
                    scales=exps[:, at : at + n],
                    in_=src[:, at * PACK : (at + n) * PACK],
                )
                at = at + n

        def quantize_h(k, src, lo, hi):
            if k not in h_codes:
                n = len(steps(k)) * H
                codes = work.tile([P, n], U32, name="hcodes", bufs=3, align_bytes=64)
                exps = work.tile([P, n], U8, name="hexp", bufs=3, align_bytes=64)
                h_codes[k], h_exps[k] = codes, exps
            quantize(h_codes[k][:, lo:hi], h_exps[k][:, lo:hi], src, hi - lo)

        def quantize_tiles(k):
            quantize_h(k, tile_buf(k), plane_cols(k), len(steps(k)) * H)

        def quantize_rest(k):
            quantize_h(k, pbuf[k], 0, rest_cols(k))

        def halves(cols):
            n = max(w for w in QUANT_COLS if w <= cols)
            return (n, cols), (0, n)

        def quantize_gpsimd(k, piece):
            lo, hi = halves(gpsimd_cols(k))[piece]
            if lo == hi:
                return
            at = rest_cols(k)
            quantize_h(k, gbuf[(k + 1) % 2][:, lo * PACK :], at + lo, at + hi)

        def quantize_w3(part, piece):
            first, end = (0, W3_CUTS[2]) if part == 0 else W3_CUTS[2:]
            lo, hi = halves((end - first) * O)[piece]
            at = first * O + lo
            quantize(w3_codes[:, at:], w3_exps[:, at:], gbuf[part][:, lo * PACK :], hi - lo)

        def output(k, js, tiles):
            b, datasets, hf = BATCHES[k][0] + js.start, len(js), BATCHES[k][2]
            n, wide = len(tiles), datasets * O
            bank = vector_bank([P, n, wide])
            for i in tiles:
                for j in range(datasets):
                    for g in range(G):
                        at = column(k, js.start + j, g, i)
                        chans = slice(((b + j) * G + g) * O, ((b + j) * G + g + 1) * O)
                        nc.tensor.matmul_mx(
                            out=bank[:, i - tiles.start, j * O : (j + 1) * O],
                            lhsT=h_codes[k][:, at : at + P].bitcast(FP8X4),
                            lhsT_scale=h_exps[k][:, at : at + P],
                            rhs=w3_codes[:, chans].bitcast(FP8X4),
                            rhs_scale=w3_exps[:, chans],
                            start=(g == 0),
                            stop=(g == G - 1),
                        )
            result = work.tile([P, n, wide], F32, name="result", bufs=17)
            nc.vector.tensor_tensor(
                out=result[:],
                in0=bank[:],
                in1=b3_rows[:, b * O : b * O + wide].unsqueeze(1).to_broadcast([P, n, wide]),
                op=ALU.add,
            )
            row = hf * ROWS + tiles.start * P
            nc.sync.dma_start(
                out=out[row : row + n * P, b : b + datasets, :].rearrange(
                    "(i p) b o -> p i (b o)", p=P
                ),
                in_=result[:],
            )

        whole, left, right = slice(0, ROWS), slice(0, ROWS // 2), slice(ROWS // 2, ROWS)
        all_tiles = range(SUB)
        low_tiles, high_tiles = range(0, SUB // 2), range(SUB // 2, SUB)

        def run(items):
            for item in items:
                item[0](*item[1:])

        def vector_items(k):
            items = []
            if k == 2:
                items = [(output, 0, steps(0), all_tiles)]
            if k > 2:
                items = [(output, k - 2, steps(k - 2), tiles) for tiles in (low_tiles, high_tiles)]
            return items + [(vector_tile, k, i) for i in range(TILES[k])]

        def weave(s_items, v_items, z_count, first):
            def freed(j):
                older = j + z_count - 4
                if older < 0:
                    return 0
                return 2 * min(older + 1, z_count) + max(older + 1 - z_count, 0)

            done = 0
            for x, item in enumerate(s_items):
                while done < len(v_items) and x >= first + max(freed(done), done):
                    run(v_items[done : done + 1])
                    done = done + 1
                run([item])
            run(v_items[done:])

        def spread(own, mixes):
            items = own[:MIX_AT]
            for x, item in enumerate(mixes):
                items.extend([item] + own[MIX_AT + 2 * x : MIX_AT + 2 * x + 2])
            return items + own[MIX_AT + 2 * len(mixes) :]

        nc.scalar.activation(out=ident_b[:], in_=ident_f[:], func=ACT.Copy)
        for i in all_tiles:
            copy = nc.scalar.copy if i % 2 else nc.vector.tensor_copy
            widen_z(0, i // 2, copy, i % 2 * R, (i % 2 + 1) * R)
        widen_part(1, 0)
        for tiles in (range(0, 1), range(1, 2), high_tiles):
            transpose_z(0, 0, tiles)
        scale_z(0, 0, range(0, 1))
        scale_z(0, 0, range(1, 2))
        permute_w1_codes(0)
        transpose_z(1, 0, low_tiles)
        b2_bank = scalar_bank([P, 2, P], F32)
        for u in range(2):
            nc.tensor.transpose(b2_bank[:, u, :], b2_rows[:].bitcast(F32)[:, u::2], ident_f[:])
        widen_part(1, 1)
        nc.scalar.copy(
            out=b2_cols[:]
            .rearrange("p c t -> p (c t)")
            .bitcast(F32)
            .rearrange("p (c u) -> p c u", u=2),
            in_=b2_bank[:, :, 0 : B * G].rearrange("p u c -> p c u"),
        )
        widen_part(2, 0)
        scale_z(0, 0, high_tiles)
        quantize_z(0, 0, left)
        permute_w1_scales(0)
        quantize_z(0, 0, right)
        transpose_z(1, 1, low_tiles)
        run(relu_items(0, 0, 0, left))
        permute_w1_codes(1)
        widen_part(2, 1)
        permute_w1_scales(1)
        gpsimd_w3(0)
        gpsimd_w3(1)
        transpose_z(1, 0, high_tiles)
        scale_z(1, 0, low_tiles)
        transpose_z(1, 1, high_tiles)
        scale_z(1, 1, low_tiles)
        scale_z(1, 0, high_tiles)
        scale_z(1, 1, high_tiles)
        run(relu_items(0, 0, 0, right) + scalar_items(0)[PACK:])
        run(vector_items(0))
        carried = []

        prev, last = LAST - 1, LAST
        for k in range(1, LAST):
            end = min(rest_cols(k - 1), MIXED[k - 1])
            mixes = mix_items(k - 1, end)
            for j in range(2):
                if j in steps(k + 1):
                    transpose_z(k + 1, j, low_tiles)
                    transpose_z(k + 1, j, high_tiles)
                if k + 2 <= LAST:
                    widen_part(k + 2, j)
                if j == SPLIT:
                    run(carried + mixes[:1])
            quantize_z(k, 0, whole)
            relu_in_place(k - 1)
            if k >= 2:
                quantize_rest(k - 2)
            quantize_z(k, 1, whole)
            for piece in range(2):
                if piece == 1:
                    quantize_tiles(k - 1)
                if k <= 2:
                    quantize_w3(k - 1, piece)
                else:
                    quantize_gpsimd(k - 2, piece)
            if k == 1:
                gpsimd_w3(2)
            else:
                gpsimd_planes(k - 1)
            for j in steps(k + 1):
                scale_z(k + 1, j, low_tiles)
                scale_z(k + 1, j, high_tiles)
            own = scalar_items(k)
            cut = len(own) - (CARRY if k < prev else 0)
            carried = own[cut:]
            items = spread(own[:cut], mixes[1:])
            if end < rest_cols(k - 1):
                items.insert(DIRECT_AT, (interleave_scalar, k - 1, end, rest_cols(k - 1)))
            weave(items, vector_items(k), 2 * len(steps(k + 1)), TILES[k - 1] + FIRST_V)

        mixes = mix_items(prev, rest_cols(prev) - DIRECT)
        run(mixes[:1])
        quantize_z(last, 0, whole)
        relu_in_place(prev)
        quantize_rest(prev - 1)
        quantize_gpsimd(prev - 1, 0)
        quantize_tiles(prev)
        quantize_gpsimd(prev - 1, 1)
        gpsimd_planes(prev)
        run([(vector_tile, last, i) for i in all_tiles])
        interleave_scalar(prev, rest_cols(prev) - DIRECT, rest_cols(prev))
        run(scalar_items(last))
        output(prev - 1, steps(prev - 1), low_tiles)
        output(prev - 1, steps(prev - 1), high_tiles)
        interleave_scalar(last, BANK_COLS, ROWS)
        run(mixes[1:])
        mix(last, 0, BANK_COLS)
        relu_in_place(last)
        quantize_gpsimd(prev, 0)
        quantize_gpsimd(prev, 1)
        quantize_rest(prev)
        quantize_tiles(last)
        quantize_rest(last)
        output(prev, steps(prev), low_tiles)
        output(prev, steps(prev), high_tiles)
        output(last, steps(last), low_tiles)
        output(last, steps(last), high_tiles)
